import numpy as np
import ml_dtypes


def mxq(x, axis, fmt="e4m3"):
    dtype, down = {"e4m3": (ml_dtypes.float8_e4m3fn, 7), "e5m2": (ml_dtypes.float8_e5m2, 14)}[fmt]
    v = np.moveaxis(np.asarray(x, np.float32).astype(ml_dtypes.bfloat16).astype(np.float64), axis, -1)
    blocks = v.reshape(v.shape[:-1] + (-1, 32))
    amax = np.abs(blocks).max(-1, keepdims=True)
    byte = np.maximum(np.where(amax > 0, np.frexp(amax)[1] - 1 + 127, 0) - down, 1)
    scale = np.exp2(byte - 127.0)
    codes = (blocks / scale).astype(np.float32).astype(dtype).astype(np.float64)
    return np.moveaxis((codes * scale).reshape(v.shape), -1, axis)


WIDE = False


def mx_kscale(k):
    if not WIDE:
        return np.ones(k)
    levels = np.array([10, -10, 5, -5, 0])
    a = np.random.permutation(np.resize(levels, k // 512 * 4)).reshape(k // 512, 4)
    idx = np.arange(k)
    return np.exp2(a[idx // 512, idx % 128 // 32])


BF16 = ml_dtypes.bfloat16


def bf(x):
    return np.asarray(x, np.float32).astype(BF16)


def f64(x):
    return np.asarray(x).astype(np.float64)


E2M1 = np.array([0.0, 0.5, 1.0, 1.5, 2.0, 3.0, 4.0, 6.0, -0.0, -0.5, -1.0, -1.5, -2.0, -3.0, -4.0, -6.0])


def pack_weight(w, fmt):
    k, n = w.shape
    w = f64(bf(w)).reshape(k // 32, 32, n)
    amax = np.abs(w).max(1)
    if fmt == "e4m3":
        byte = np.frexp(amax)[1] - 1 + 127 - 7
    else:
        mant, ex = np.frexp(amax / 6.0)
        byte = np.where(mant > 0.5, ex, ex - 1) + 127
    byte = np.clip(np.where(amax > 0, byte, 1), 1, 254)
    scaled = (w * np.exp2(127.0 - byte)[:, None, :]).reshape(k, n).astype(np.float32)
    by_word = np.ascontiguousarray(scaled.reshape(k // 512, 128, 4, n).transpose(0, 1, 3, 2))
    if fmt == "e4m3":
        words = by_word.astype(ml_dtypes.float8_e4m3fn).view(np.uint8)
    else:
        c = by_word.astype(ml_dtypes.float4_e2m1fn).view(np.uint8) & 0xF
        words = c[..., 0::2] | (c[..., 1::2] << 4)
    return np.ascontiguousarray(words), np.ascontiguousarray(byte.astype(np.uint8).reshape(k // 512, 16, n))


def unpack_weight(words, scales, fmt):
    g, p, n, _ = words.shape
    if fmt == "e4m3":
        vals = np.ascontiguousarray(words).view(ml_dtypes.float8_e4m3fn).astype(np.float64)
    else:
        nib = np.empty((g, p, n, 4), np.uint8)
        nib[..., 0::2] = words & 0xF
        nib[..., 1::2] = words >> 4
        vals = E2M1[nib]
    vals = vals * np.repeat(np.exp2(scales.astype(np.float64) - 127.0), 8, axis=1)[..., None]
    return vals.transpose(0, 1, 3, 2).reshape(g * 512, n)


B, C, T, TF, CCONF, GROUPS = 48, 512, 64, 256, 512, 32
EPS = 1e-5


def group_norm(x, gamma, beta):
    b_, c_, t_ = x.shape
    xg = x.reshape(b_, GROUPS, c_ // GROUPS, t_)
    mu = xg.mean(axis=(2, 3), keepdims=True)
    var = xg.var(axis=(2, 3), keepdims=True)
    xg = (xg - mu) / np.sqrt(var + EPS)
    return xg.reshape(b_, c_, t_) * gamma[None, :, None] + beta[None, :, None]


def pool(fh, lo, hi):
    idx = np.arange(fh.shape[-1])
    out = np.empty((fh.shape[0], fh.shape[1], lo.shape[1]))
    for i in range(fh.shape[0]):
        mask = (idx[None, :] > lo[i][:, None] - 1.0) & (idx[None, :] <= hi[i][:, None])
        out[i] = np.where(mask[None, :, :], fh[i][:, None, :], -np.inf).max(-1)
    return np.where(np.isfinite(out), out, 0.0)


def boundary_max_pooling(feature, segments):
    tin = feature.shape[-1]
    half = feature.shape[1] // 2
    s = np.clip(segments, 0.0, tin - 1.0)
    left = pool(feature[:, :half], s[..., 0], s[..., 1])
    right = pool(feature[:, half:], s[..., 2], s[..., 3])
    return np.concatenate([left, right], axis=1)


def make_segments(n, tin):
    lo = np.random.uniform(size=(B, n, 2)) * (1.25 * tin) - 0.125 * tin
    ln = np.random.uniform(size=(B, n, 2)) * (tin / 4) + 1.0
    ln = np.where(np.random.uniform(size=(B, n, 2)) < 0.1, -ln, ln)
    hi = lo + ln
    return np.stack([lo[..., 0], hi[..., 0], lo[..., 1], hi[..., 1]], axis=-1)


def setup_inputs():
    s = mx_kscale(C)
    frame_level_feature = bf(np.random.standard_normal((B, C, TF)) * s[None, :, None])
    frame_segments = bf(make_segments(T, TF))
    w_roi = np.random.standard_normal((C, C)) * 0.5 * C ** -0.5 / s[None, :]
    w_roi_words, w_roi_scales = pack_weight(np.ascontiguousarray(w_roi.T), 'e4m3')
    return {
        'frame_level_feature': frame_level_feature,
        'frame_segments': frame_segments,
        'w_roi_words': w_roi_words,
        'w_roi_scales': w_roi_scales,
        'b_roi': bf(np.random.standard_normal(C) * 0.3),
        'g_roi': bf(1.0 + 0.2 * np.random.standard_normal(C)),
        'be_roi': bf(np.random.standard_normal(C) * 0.3),
    }


def reference(frame_level_feature, frame_segments, w_roi_words, w_roi_scales, b_roi, g_roi, be_roi):
    pooled = boundary_max_pooling(f64(frame_level_feature), f64(frame_segments))
    y = (unpack_weight(w_roi_words, w_roi_scales, 'e4m3').T @ mxq(pooled, 1, 'e4m3')) + f64(b_roi)[None, :, None]
    return np.maximum(group_norm(y, f64(g_roi), f64(be_roi)), 0.0)

@@ -1,0 +1,241 @@
+import concourse.mybir as mybir
+from concourse.masks import make_identity
+
+FLOPS = 2 * 48 * 512 * 512 * 64
+
+BF16 = mybir.dt.bfloat16
+F32 = mybir.dt.float32
+I32 = mybir.dt.int32
+U32 = mybir.dt.uint32
+U8 = mybir.dt.uint8
+FP8X4 = mybir.dt.float8_e4m3fn_x4
+ALU = mybir.AluOpType
+ACT = mybir.ActivationFunctionType
+AXIS_X = mybir.AxisListType.X
+
+P = 128
+PACK = 4
+BATCH = 48
+CHANNELS = 512
+FRAMES = 256
+PROPOSALS = 64
+GROUP_CHANNELS = 16
+GROUP_SIZE = GROUP_CHANNELS * PROPOSALS
+EPS = 1e-5
+ROUND = 8
+ROUNDS = BATCH // ROUND
+OUT_TILES = CHANNELS // P
+RUN = 8
+PART = 32
+PARTS = PROPOSALS // PART
+JOINT = 32
+
+EDGE = 2.0 ** -10
+BIG = 2.0 ** 110
+EMPTY = -(2.0 ** 99)
+
+
+def tile_coarsepyramid_pb_kernel(
+    tc, frame_level_feature, frame_segments, w_roi_words, w_roi_scales, b_roi, g_roi, be_roi, out
+):
+    nc = tc.nc
+    with tc.tile_pool(name="const", bufs=1) as const:
+        w_words = const.tile([P, CHANNELS], U32, align_bytes=64)
+        nc.sync.dma_start(
+            out=w_words[:].bitcast(I32),
+            in_=w_roi_words[0].rearrange("p n t -> p (n t)").bitcast(I32),
+        )
+        w_scales = const.tile([P, CHANNELS], U8, align_bytes=64)
+        nc.vector.memset(w_scales[:].bitcast(I32), 0)
+        for quadrant in range(4):
+            nc.sync.dma_start(
+                out=w_scales[32 * quadrant : 32 * quadrant + 4, :].bitcast(I32),
+                in_=w_roi_scales[0, 4 * quadrant : 4 * quadrant + 4, :].bitcast(I32),
+            )
+
+        identity = const.tile([P, P], BF16)
+        make_identity(nc, identity[:])
+        rows = const.tile([P, P], BF16)
+        nc.vector.memset(rows[:], 0.0)
+        for i, vector in enumerate((b_roi, g_roi, be_roi)):
+            nc.sync.dma_start(
+                out=rows[OUT_TILES * i : OUT_TILES * (i + 1), :],
+                in_=vector.rearrange("(q p) -> q p", p=P),
+            )
+        columns = const.tile([P, 3 * OUT_TILES], F32)
+        with tc.psum_pool(name="setup_psum", bufs=1) as setup_psum:
+            turned = setup_psum.tile([P, P], BF16)
+            nc.tensor.transpose(turned[:], rows[:], identity[:])
+            nc.vector.tensor_copy(out=columns[:], in_=turned[:, 0 : 3 * OUT_TILES])
+        bias_col = columns[:, 0:OUT_TILES]
+        gain_col = columns[:, OUT_TILES : 2 * OUT_TILES]
+        shift_col = columns[:, 2 * OUT_TILES : 3 * OUT_TILES]
+        eps_col = const.tile([P, 1], F32)
+        nc.vector.memset(eps_col[:], EPS)
+
+        column_group = const.tile([P, P], I32)
+        nc.gpsimd.iota(column_group[:], pattern=[[1, P // GROUP_CHANNELS], [0, GROUP_CHANNELS]], base=0, channel_multiplier=0)
+        partition_index = const.tile([P, 1], I32)
+        nc.gpsimd.iota(partition_index[:], pattern=[[0, 1]], base=0, channel_multiplier=1)
+        partition_group = const.tile([P, 1], I32)
+        nc.vector.tensor_single_scalar(out=partition_group[:], in_=partition_index[:], scalar=4, op=ALU.arith_shift_right)
+        column_group_f = const.tile([P, P], F32)
+        nc.vector.tensor_copy(out=column_group_f[:], in_=column_group[:])
+        partition_group_f = const.tile([P, 1], F32)
+        nc.vector.tensor_copy(out=partition_group_f[:], in_=partition_group[:])
+        same_group = const.tile([P, P], F32)
+        nc.vector.tensor_scalar(
+            out=same_group[:], in0=column_group_f[:], scalar1=partition_group_f[:, 0:1], scalar2=None, op0=ALU.is_equal
+        )
+
+        frame_int = const.tile([P, FRAMES], I32)
+        nc.gpsimd.iota(frame_int[:], pattern=[[1, FRAMES]], base=0, channel_multiplier=0)
+        frame_number = const.tile([P, FRAMES], F32)
+        nc.vector.tensor_copy(out=frame_number[:], in_=frame_int[:])
+
+        windows = BATCH * PROPOSALS
+        neg_middle = const.tile([P, windows], F32)
+        big_half_width = const.tile([P, windows], F32)
+        with tc.tile_pool(name="setup", bufs=1) as setup:
+            segments = setup.tile([P, windows, 4], BF16)
+            nc.sync.dma_start(
+                out=segments[:].rearrange("p w s -> p (w s)"),
+                in_=frame_segments.rearrange("b n s -> (b n s)").partition_broadcast(P),
+            )
+            lower = setup.tile([P, windows], F32)
+            upper = setup.tile([P, windows], F32)
+            for half in range(2):
+                lanes = slice(64 * half, 64 * half + 64)
+                nc.vector.tensor_scalar(
+                    out=lower[lanes, :], in0=segments[lanes, :, 2 * half], scalar1=0.0, scalar2=FRAMES - 1.0, op0=ALU.max, op1=ALU.min
+                )
+                nc.vector.tensor_scalar(
+                    out=upper[lanes, :], in0=segments[lanes, :, 2 * half + 1], scalar1=0.0, scalar2=FRAMES - 1.0, op0=ALU.max, op1=ALU.min
+                )
+            total = setup.tile([P, windows], F32)
+            nc.vector.tensor_tensor(out=total[:], in0=lower[:], in1=upper[:], op=ALU.add)
+            nc.vector.tensor_scalar(out=neg_middle[:], in0=total[:], scalar1=-0.5, scalar2=0.5 - EDGE, op0=ALU.mult, op1=ALU.add)
+            span = setup.tile([P, windows], F32)
+            nc.vector.tensor_tensor(out=span[:], in0=upper[:], in1=lower[:], op=ALU.subtract)
+            nc.vector.tensor_scalar(out=big_half_width[:], in0=span[:], scalar1=0.5 * BIG, scalar2=0.5 * BIG, op0=ALU.mult, op1=ALU.add)
+
+        with tc.tile_pool(name="features", bufs=2) as feature_pool, tc.tile_pool(name="masks", bufs=3) as mask_pool, tc.tile_pool(
+            name="distances", bufs=2
+        ) as distance_pool, tc.tile_pool(name="work", bufs=2) as work_pool, tc.tile_pool(name="operands", bufs=2) as operand_pool, tc.tile_pool(
+            name="norm", bufs=1
+        ) as norm_pool, tc.psum_pool(name="products", bufs=OUT_TILES) as product_pool, tc.psum_pool(name="sums", bufs=2) as sum_pool:
+            for r in range(ROUNDS):
+                batches = slice(ROUND * r, ROUND * (r + 1))
+                feature = feature_pool.tile([P, ROUND, PACK, FRAMES], BF16)
+                nc.sync.dma_start(
+                    out=feature[:].rearrange("p b j t -> p b (j t)"),
+                    in_=frame_level_feature[batches].rearrange("b (p j) t -> p b (j t)", j=PACK),
+                )
+                highest = operand_pool.tile([P, ROUND, PROPOSALS, PACK], BF16)
+                for b in range(ROUND):
+                    for part in range(PARTS):
+                        first = (ROUND * r + b) * PROPOSALS + PART * part
+                        mask = mask_pool.tile([P, PART, FRAMES], BF16)
+                        for n0 in range(0, PART, RUN):
+                            distance = distance_pool.tile([P, RUN, FRAMES], F32)
+                            for i in range(RUN):
+                                w = first + n0 + i
+                                nc.scalar.activation(
+                                    out=distance[:, i, :], in_=frame_number[:], func=ACT.Abs, bias=neg_middle[:, w : w + 1], scale=1.0
+                                )
+                            for i in range(RUN):
+                                w = first + n0 + i
+                                nc.scalar.activation(
+                                    out=mask[:, n0 + i, :], in_=distance[:, i, :], func=ACT.Identity, bias=big_half_width[:, w : w + 1], scale=-BIG
+                                )
+                        joint = work_pool.tile([P, PACK, PART, JOINT], BF16)
+                        for j0 in range(0, PACK, 2):
+                            pair = []
+                            for j in (j0, j0 + 1):
+                                inside = work_pool.tile([P, PART, FRAMES], BF16, name="inside", tag="inside%d" % (j - j0), bufs=1)
+                                nc.vector.tensor_tensor(
+                                    out=inside[:],
+                                    in0=feature[:, b, j, :].unsqueeze(1).to_broadcast([P, PART, FRAMES]),
+                                    in1=mask[:],
+                                    op=ALU.min,
+                                )
+                                pair.append(inside)
+                            for width in (FRAMES // 2, FRAMES // 4):
+                                for inside in pair:
+                                    nc.vector.tensor_tensor(
+                                        out=inside[:, :, 0:width], in0=inside[:, :, 0:width], in1=inside[:, :, width : 2 * width], op=ALU.max
+                                    )
+                            for j, inside in zip((j0, j0 + 1), pair):
+                                nc.vector.tensor_tensor(
+                                    out=joint[:, j], in0=inside[:, :, 0:JOINT], in1=inside[:, :, JOINT : 2 * JOINT], op=ALU.max
+                                )
+                        for width in (16, 8, 4, 2):
+                            nc.vector.tensor_tensor(
+                                out=joint[:, :, :, 0:width], in0=joint[:, :, :, 0:width], in1=joint[:, :, :, width : 2 * width], op=ALU.max
+                            )
+                        nc.vector.tensor_tensor(
+                            out=highest[:, b, PART * part : PART * (part + 1), :].rearrange("p n j -> p j n"),
+                            in0=joint[:, :, :, 0],
+                            in1=joint[:, :, :, 1],
+                            op=ALU.max,
+                        )
+
+                pooled = operand_pool.tile([P, ROUND * PROPOSALS * PACK], BF16, align_bytes=64)
+                flat = highest[:].rearrange("p b n j -> p (b n j)")
+                nc.vector.scalar_tensor_tensor(out=pooled[:], in0=flat, scalar=EMPTY, in1=flat, op0=ALU.is_gt, op1=ALU.mult)
+                codes = operand_pool.tile([P, ROUND * PROPOSALS], U32, align_bytes=64)
+                scales = operand_pool.tile([P, ROUND * PROPOSALS], U8, align_bytes=64)
+                nc.vector.quantize_mx(out=codes[:].bitcast(FP8X4), scales=scales[:], in_=pooled[:])
+
+                stats = OUT_TILES * ROUND
+                y = norm_pool.tile([P, OUT_TILES, ROUND, PROPOSALS], F32)
+                row_sum = norm_pool.tile([P, stats], F32)
+                for q in range(OUT_TILES):
+                    cols = slice(P * q, P * (q + 1))
+                    product = product_pool.tile([P, ROUND, PROPOSALS], F32)
+                    nc.tensor.matmul_mx(
+                        out=product[:].rearrange("p b n -> p (b n)"),
+                        lhsT=w_words[:, cols].bitcast(FP8X4),
+                        lhsT_scale=w_scales[:, cols],
+                        rhs=codes[:].bitcast(FP8X4),
+                        rhs_scale=scales[:],
+                        start=True,
+                        stop=True,
+                    )
+                    for b in range(ROUND):
+                        s = ROUND * q + b
+                        nc.scalar.activation(
+                            out=y[:, q, b, :], in_=product[:, b, :], func=ACT.Identity, bias=bias_col[:, q : q + 1], scale=1.0,
+                            accum_out=row_sum[:, s : s + 1],
+                        )
+                group_sum = sum_pool.tile([P, stats], F32)
+                nc.tensor.matmul(out=group_sum[:], lhsT=same_group[:], rhs=row_sum[:], start=True, stop=True)
+                neg_mean = norm_pool.tile([P, stats], F32)
+                nc.vector.tensor_scalar(out=neg_mean[:], in0=group_sum[:], scalar1=-1.0 / GROUP_SIZE, scalar2=None, op0=ALU.mult)
+
+                squares = norm_pool.tile([P, OUT_TILES, ROUND, PROPOSALS], F32)
+                row_squares = norm_pool.tile([P, stats], F32)
+                for q in range(OUT_TILES):
+                    for b in range(ROUND):
+                        s = ROUND * q + b
+                        nc.scalar.activation(
+                            out=squares[:, q, b, :], in_=y[:, q, b, :], func=ACT.Square, bias=neg_mean[:, s : s + 1], scale=1.0,
+                            accum_out=row_squares[:, s : s + 1],
+                        )
+                group_squares = sum_pool.tile([P, stats], F32)
+                nc.tensor.matmul(out=group_squares[:], lhsT=same_group[:], rhs=row_squares[:], start=True, stop=True)
+                deviation = norm_pool.tile([P, stats], F32)
+                nc.scalar.activation(out=deviation[:], in_=group_squares[:], func=ACT.Sqrt, bias=eps_col[:, 0:1], scale=1.0 / GROUP_SIZE)
+
+                factor = norm_pool.tile([P, OUT_TILES, ROUND], F32)
+                nc.vector.reciprocal(out=factor[:].rearrange("p q b -> p (q b)"), in_=deviation[:])
+                nc.vector.tensor_tensor(out=factor[:], in0=factor[:], in1=gain_col.unsqueeze(2).to_broadcast([P, OUT_TILES, ROUND]), op=ALU.mult)
+                offset = norm_pool.tile([P, OUT_TILES, ROUND], F32)
+                nc.vector.tensor_tensor(out=offset[:], in0=factor[:], in1=neg_mean[:].rearrange("p (q b) -> p q b", q=OUT_TILES), op=ALU.mult)
+                nc.vector.tensor_tensor(out=offset[:], in0=offset[:], in1=shift_col.unsqueeze(2).to_broadcast([P, OUT_TILES, ROUND]), op=ALU.add)
+                for q in range(OUT_TILES):
+                    for b in range(ROUND):
+                        nc.scalar.activation(
+                            out=y[:, q, b, :], in_=y[:, q, b, :], func=ACT.Relu, bias=offset[:, q, b : b + 1], scale=factor[:, q, b : b + 1]
+                        )
+                    nc.sync.dma_start(out=out[batches, P * q : P * (q + 1), :].rearrange("b p n -> p b n"), in_=y[:, q])

@@ -11,7 +11,6 @@ U8 = mybir.dt.uint8
 FP8X4 = mybir.dt.float8_e4m3fn_x4
 ALU = mybir.AluOpType
 ACT = mybir.ActivationFunctionType
-AXIS_X = mybir.AxisListType.X
 
 P = 128
 PACK = 4
@@ -24,15 +23,26 @@ GROUP_SIZE = GROUP_CHANNELS * PROPOSALS
 EPS = 1e-5
 ROUND = 8
 ROUNDS = BATCH // ROUND
-OUT_TILES = CHANNELS // P
-RUN = 8
-PART = 32
-PARTS = PROPOSALS // PART
-JOINT = 32
+CHUNKS = CHANNELS // P
+QUERIES = 2 * PROPOSALS
+WORDS = FRAMES // 2
+RUN_WORDS = 4
+RUN_FRAMES = 2 * RUN_WORDS
+BLOCK = 2 * RUN_WORDS
+BLOCKS = FRAMES // BLOCK
+CELLS = 2 * RUN_FRAMES + BLOCKS
+KEYS = 2 * RUN_WORDS
+SPREAD = CELLS + KEYS
+BANK = 8
+BANK_WORDS = 512
+SHARE = 16
+RING = 4
+SWEEP = 32
 
 EDGE = 2.0 ** -10
 BIG = 2.0 ** 110
 EMPTY = -(2.0 ** 99)
+ROUNDER = 1.5 * 2.0 ** 23
 
 
 def tile_coarsepyramid_pb_kernel(
@@ -55,21 +65,24 @@ def tile_coarsepyramid_pb_kernel(
 
         identity = const.tile([P, P], BF16)
         make_identity(nc, identity[:])
+        identity_words = const.tile([P, P], F32)
+        make_identity(nc, identity_words[:])
+
         rows = const.tile([P, P], BF16)
         nc.vector.memset(rows[:], 0.0)
         for i, vector in enumerate((b_roi, g_roi, be_roi)):
             nc.sync.dma_start(
-                out=rows[OUT_TILES * i : OUT_TILES * (i + 1), :],
+                out=rows[CHUNKS * i : CHUNKS * (i + 1), :],
                 in_=vector.rearrange("(q p) -> q p", p=P),
             )
-        columns = const.tile([P, 3 * OUT_TILES], F32)
+        columns = const.tile([P, 3 * CHUNKS], F32)
         with tc.psum_pool(name="setup_psum", bufs=1) as setup_psum:
-            turned = setup_psum.tile([P, P], BF16)
-            nc.tensor.transpose(turned[:], rows[:], identity[:])
-            nc.vector.tensor_copy(out=columns[:], in_=turned[:, 0 : 3 * OUT_TILES])
-        bias_col = columns[:, 0:OUT_TILES]
-        gain_col = columns[:, OUT_TILES : 2 * OUT_TILES]
-        shift_col = columns[:, 2 * OUT_TILES : 3 * OUT_TILES]
+            rows_turned = setup_psum.tile([P, P], BF16)
+            nc.tensor.transpose(rows_turned[:], rows[:], identity[:])
+            nc.vector.tensor_copy(out=columns[:], in_=rows_turned[:, 0 : 3 * CHUNKS])
+        bias_col = columns[:, 0:CHUNKS]
+        gain_col = columns[:, CHUNKS : 2 * CHUNKS]
+        shift_col = columns[:, 2 * CHUNKS : 3 * CHUNKS]
         eps_col = const.tile([P, 1], F32)
         nc.vector.memset(eps_col[:], EPS)
 
@@ -87,23 +100,25 @@ def tile_coarsepyramid_pb_kernel(
         nc.vector.tensor_scalar(
             out=same_group[:], in0=column_group_f[:], scalar1=partition_group_f[:, 0:1], scalar2=None, op0=ALU.is_equal
         )
+        partition_number = const.tile([P, 1], F32)
+        nc.vector.tensor_copy(out=partition_number[:], in_=partition_index[:])
 
-        frame_int = const.tile([P, FRAMES], I32)
-        nc.gpsimd.iota(frame_int[:], pattern=[[1, FRAMES]], base=0, channel_multiplier=0)
-        frame_number = const.tile([P, FRAMES], F32)
-        nc.vector.tensor_copy(out=frame_number[:], in_=frame_int[:])
+        count_int = const.tile([P, BLOCKS], I32)
+        nc.gpsimd.iota(count_int[:], pattern=[[1, BLOCKS]], base=0, channel_multiplier=0)
+        count = const.tile([P, BLOCKS], F32)
+        nc.vector.tensor_copy(out=count[:], in_=count_int[:])
+        block_middle = const.tile([P, BLOCKS], F32)
+        nc.vector.tensor_scalar(
+            out=block_middle[:], in0=count[:], scalar1=float(BLOCK), scalar2=0.5 * (BLOCK - 1), op0=ALU.mult, op1=ALU.add
+        )
 
-        windows = BATCH * PROPOSALS
-        neg_middle = const.tile([P, windows], F32)
-        big_half_width = const.tile([P, windows], F32)
+        window_table = const.tile([P, BATCH, SPREAD], BF16)
         with tc.tile_pool(name="setup", bufs=1) as setup:
-            segments = setup.tile([P, windows, 4], BF16)
-            nc.sync.dma_start(
-                out=segments[:].rearrange("p w s -> p (w s)"),
-                in_=frame_segments.rearrange("b n s -> (b n s)").partition_broadcast(P),
-            )
-            lower = setup.tile([P, windows], F32)
-            upper = setup.tile([P, windows], F32)
+            segments = setup.tile([P, BATCH, 4], BF16)
+            for half in range(2):
+                nc.sync.dma_start(out=segments[64 * half : 64 * half + 64], in_=frame_segments.rearrange("b n s -> n b s"))
+            lower = setup.tile([P, BATCH], F32)
+            upper = setup.tile([P, BATCH], F32)
             for half in range(2):
                 lanes = slice(64 * half, 64 * half + 64)
                 nc.vector.tensor_scalar(
@@ -112,87 +127,191 @@ def tile_coarsepyramid_pb_kernel(
                 nc.vector.tensor_scalar(
                     out=upper[lanes, :], in0=segments[lanes, :, 2 * half + 1], scalar1=0.0, scalar2=FRAMES - 1.0, op0=ALU.max, op1=ALU.min
                 )
-            total = setup.tile([P, windows], F32)
-            nc.vector.tensor_tensor(out=total[:], in0=lower[:], in1=upper[:], op=ALU.add)
-            nc.vector.tensor_scalar(out=neg_middle[:], in0=total[:], scalar1=-0.5, scalar2=0.5 - EDGE, op0=ALU.mult, op1=ALU.add)
-            span = setup.tile([P, windows], F32)
-            nc.vector.tensor_tensor(out=span[:], in0=upper[:], in1=lower[:], op=ALU.subtract)
-            nc.vector.tensor_scalar(out=big_half_width[:], in0=span[:], scalar1=0.5 * BIG, scalar2=0.5 * BIG, op0=ALU.mult, op1=ALU.add)
+            middle = setup.tile([P, BATCH], F32)
+            nc.vector.tensor_tensor(out=middle[:], in0=lower[:], in1=upper[:], op=ALU.add)
+            nc.vector.tensor_scalar(out=middle[:], in0=middle[:], scalar1=0.5, scalar2=EDGE - 0.5, op0=ALU.mult, op1=ALU.add)
+            half_width = setup.tile([P, BATCH], F32)
+            nc.vector.tensor_tensor(out=half_width[:], in0=upper[:], in1=lower[:], op=ALU.subtract)
+            nc.vector.tensor_scalar(out=half_width[:], in0=half_width[:], scalar1=0.5, scalar2=0.5, op0=ALU.mult, op1=ALU.add)
 
-        with tc.tile_pool(name="features", bufs=2) as feature_pool, tc.tile_pool(name="masks", bufs=3) as mask_pool, tc.tile_pool(
-            name="distances", bufs=2
-        ) as distance_pool, tc.tile_pool(name="work", bufs=2) as work_pool, tc.tile_pool(name="operands", bufs=2) as operand_pool, tc.tile_pool(
-            name="norm", bufs=1
-        ) as norm_pool, tc.psum_pool(name="products", bufs=OUT_TILES) as product_pool, tc.psum_pool(name="sums", bufs=2) as sum_pool:
+            end_word = []
+            for end, name in ((lower, "lower_word"), (upper, "upper_word")):
+                nudged = setup.tile([P, BATCH], F32, name=name + "_nudged")
+                nc.vector.tensor_scalar(out=nudged[:], in0=end[:], scalar1=0.5, scalar2=0.5 * EDGE - 0.5, op0=ALU.mult, op1=ALU.add)
+                raised = setup.tile([P, BATCH], F32, name=name + "_raised")
+                nc.vector.tensor_scalar(out=raised[:], in0=nudged[:], scalar1=ROUNDER, scalar2=None, op0=ALU.add)
+                whole = setup.tile([P, BATCH], F32, name=name + "_whole")
+                nc.vector.tensor_scalar(out=whole[:], in0=raised[:], scalar1=-ROUNDER, scalar2=None, op0=ALU.add)
+                as_int = setup.tile([P, BATCH], I32, name=name + "_int")
+                nc.vector.tensor_copy(out=as_int[:], in_=whole[:])
+                word = setup.tile([P, BATCH], F32, name=name)
+                nc.vector.tensor_copy(out=word[:], in_=as_int[:])
+                end_word.append(word)
+            left_start = setup.tile([P, BATCH], F32)
+            nc.vector.tensor_scalar(out=left_start[:], in0=end_word[0][:], scalar1=float(WORDS - KEYS), scalar2=None, op0=ALU.min)
+            after_left = setup.tile([P, BATCH], F32)
+            nc.vector.tensor_scalar(out=after_left[:], in0=left_start[:], scalar1=float(RUN_WORDS), scalar2=None, op0=ALU.add)
+            right_start = setup.tile([P, BATCH], F32)
+            nc.vector.tensor_scalar(out=right_start[:], in0=end_word[1][:], scalar1=-float(RUN_WORDS - 1), scalar2=None, op0=ALU.add)
+            nc.vector.tensor_tensor(out=right_start[:], in0=right_start[:], in1=after_left[:], op=ALU.max)
+
+            distance = setup.tile([P, BATCH, CELLS], F32)
+            for i, start in enumerate((left_start, right_start)):
+                keys = slice(CELLS + RUN_WORDS * i, CELLS + RUN_WORDS * (i + 1))
+                nc.vector.tensor_tensor(
+                    out=window_table[:, :, keys],
+                    in0=start[:].unsqueeze(2).to_broadcast([P, BATCH, RUN_WORDS]),
+                    in1=count[:, 0:RUN_WORDS].unsqueeze(1).to_broadcast([P, BATCH, RUN_WORDS]),
+                    op=ALU.add,
+                )
+                from_middle = setup.tile([P, BATCH], F32, name="from_middle%d" % i)
+                nc.vector.scalar_tensor_tensor(out=from_middle[:], in0=start[:], scalar=2.0, in1=middle[:], op0=ALU.mult, op1=ALU.subtract)
+                nc.vector.tensor_tensor(
+                    out=distance[:, :, RUN_FRAMES * i : RUN_FRAMES * (i + 1)],
+                    in0=from_middle[:].unsqueeze(2).to_broadcast([P, BATCH, RUN_FRAMES]),
+                    in1=count[:, 0:RUN_FRAMES].unsqueeze(1).to_broadcast([P, BATCH, RUN_FRAMES]),
+                    op=ALU.add,
+                )
+            nc.vector.tensor_tensor(
+                out=distance[:, :, 2 * RUN_FRAMES : CELLS],
+                in0=block_middle[:].unsqueeze(1).to_broadcast([P, BATCH, BLOCKS]),
+                in1=middle[:].unsqueeze(2).to_broadcast([P, BATCH, BLOCKS]),
+                op=ALU.subtract,
+            )
+            nc.scalar.activation(out=distance[:], in_=distance[:], func=ACT.Abs)
+            block_reach = setup.tile([P, BATCH], F32)
+            nc.vector.tensor_scalar(out=block_reach[:], in0=half_width[:], scalar1=-0.5 * (BLOCK - 1), scalar2=None, op0=ALU.add)
+            nc.vector.tensor_tensor(
+                out=distance[:, :, 0 : 2 * RUN_FRAMES],
+                in0=distance[:, :, 0 : 2 * RUN_FRAMES],
+                in1=half_width[:].unsqueeze(2).to_broadcast([P, BATCH, 2 * RUN_FRAMES]),
+                op=ALU.subtract,
+            )
+            nc.vector.tensor_tensor(
+                out=distance[:, :, 2 * RUN_FRAMES : CELLS],
+                in0=distance[:, :, 2 * RUN_FRAMES : CELLS],
+                in1=block_reach[:].unsqueeze(2).to_broadcast([P, BATCH, BLOCKS]),
+                op=ALU.subtract,
+            )
+            nc.vector.tensor_scalar(out=window_table[:, :, 0:CELLS], in0=distance[:], scalar1=-BIG, scalar2=None, op0=ALU.mult)
+
+        select_ring = []
+        for s in range(RING):
+            select = const.tile([P, SHARE, P], F32, name="select%d" % s)
+            nc.vector.memset(select[:], 0.0)
+            select_ring.append(select)
+
+        with tc.tile_pool(name="batch", bufs=3) as batch_pool, tc.tile_pool(name="work", bufs=2) as work_pool, tc.tile_pool(
+            name="operands", bufs=2
+        ) as operand_pool, tc.tile_pool(name="norm", bufs=1) as norm_pool, tc.psum_pool(name="table_psum", bufs=1) as table_psum, tc.psum_pool(
+            name="spread_psum", bufs=2
+        ) as spread_psum, tc.psum_pool(name="gather_psum", bufs=3) as gather_psum, tc.psum_pool(name="late_psum", bufs=2) as late_psum:
+
+            def prepare(b):
+                feature = batch_pool.tile([P, CHUNKS, FRAMES], BF16, name="feature")
+                nc.sync.dma_start(out=feature[:], in_=frame_level_feature[b].rearrange("(q m) t -> m q t", m=P))
+                turned = table_psum.tile([P, CHUNKS, P], F32, name="turned")
+                for q in range(CHUNKS):
+                    nc.tensor.transpose(turned[:, q, :], feature[:, q, :].bitcast(F32), identity_words[:])
+                table = batch_pool.tile([P, CHUNKS, P], F32, name="table")
+                nc.scalar.copy(out=table[:], in_=turned[:])
+
+                blocks = feature[:].rearrange("m q (a f) -> m (q a) f", f=BLOCK)
+                of_four = batch_pool.tile([P, CHUNKS * BLOCKS, 4], BF16, name="of_four")
+                nc.vector.tensor_tensor(out=of_four[:], in0=blocks[:, :, 0:4], in1=blocks[:, :, 4:8], op=ALU.max)
+                of_two = batch_pool.tile([P, CHUNKS * BLOCKS, 2], BF16, name="of_two")
+                nc.vector.tensor_tensor(out=of_two[:], in0=of_four[:, :, 0:2], in1=of_four[:, :, 2:4], op=ALU.max)
+                block_max = batch_pool.tile([P, CHUNKS, BLOCKS], BF16, name="block_max")
+                nc.vector.tensor_tensor(
+                    out=block_max[:].rearrange("m q a -> m (q a)"), in0=of_two[:, :, 0], in1=of_two[:, :, 1], op=ALU.max
+                )
+
+                window = batch_pool.tile([P, QUERIES, SPREAD], BF16, name="window")
+                for g in range(SPREAD // BANK):
+                    spread = spread_psum.tile([P, BANK, QUERIES], BF16, name="spread")
+                    for i in range(BANK):
+                        col = BANK * g + i
+                        nc.tensor.transpose(spread[:, i, :], window_table[:, b, col : col + 1].to_broadcast([P, P]), identity[:])
+                    nc.scalar.copy(out=window[:, :, BANK * g : BANK * (g + 1)], in_=spread[:].rearrange("p i k -> p k i"))
+                return table, block_max, window
+
+            def pool_windows(prepared, best, i):
+                table, block_max, window = prepared
+                cells = work_pool.tile([P, CHUNKS, PROPOSALS, CELLS], BF16, name="cells")
+                for half in range(2):
+                    for sweep in range(PROPOSALS // SWEEP):
+                        first = PROPOSALS * half + SWEEP * sweep
+                        shares = select_ring[2 * sweep : 2 * sweep + 2]
+                        for s, select in enumerate(shares):
+                            nc.vector.tensor_scalar(
+                                out=select[:, :, 0:KEYS],
+                                in0=window[:, first + SHARE * s : first + SHARE * (s + 1), CELLS:SPREAD],
+                                scalar1=partition_number[:, 0:1],
+                                scalar2=None,
+                                op0=ALU.is_equal,
+                            )
+                        for q in (2 * half, 2 * half + 1):
+                            runs = gather_psum.tile([P, BANK_WORDS], F32, name="runs")
+                            for n in range(SWEEP):
+                                nc.tensor.transpose(runs[:, KEYS * n : KEYS * n + P], table[:, q, :], shares[n // SHARE][:, n % SHARE, :])
+                            nc.vector.tensor_tensor(
+                                out=cells[:, q, SWEEP * sweep : SWEEP * (sweep + 1), 0 : 2 * RUN_FRAMES],
+                                in0=runs[:, 0 : KEYS * SWEEP].bitcast(BF16).rearrange("p (n f) -> p n f", f=2 * RUN_FRAMES),
+                                in1=window[:, first : first + SWEEP, 0 : 2 * RUN_FRAMES],
+                                op=ALU.min,
+                            )
+                for q in range(CHUNKS):
+                    first = PROPOSALS * (q // 2)
+                    nc.vector.tensor_tensor(
+                        out=cells[:, q, :, 2 * RUN_FRAMES : CELLS],
+                        in0=block_max[:, q, :].unsqueeze(1).to_broadcast([P, PROPOSALS, BLOCKS]),
+                        in1=window[:, first : first + PROPOSALS, 2 * RUN_FRAMES : CELLS],
+                        op=ALU.min,
+                    )
+                lines = cells[:].rearrange("p q n c -> p (q n) c")
+                nc.vector.tensor_tensor(out=lines[:, :, 16:32], in0=lines[:, :, 16:32], in1=lines[:, :, 32:48], op=ALU.max)
+                for width in (16, 8, 4, 2):
+                    nc.vector.tensor_tensor(out=lines[:, :, 0:width], in0=lines[:, :, 0:width], in1=lines[:, :, width : 2 * width], op=ALU.max)
+                nc.vector.tensor_tensor(out=best[:, :, i, :], in0=cells[:, :, :, 0], in1=cells[:, :, :, 1], op=ALU.max)
+
+            ready = prepare(0)
             for r in range(ROUNDS):
                 batches = slice(ROUND * r, ROUND * (r + 1))
-                feature = feature_pool.tile([P, ROUND, PACK, FRAMES], BF16)
-                nc.sync.dma_start(
-                    out=feature[:].rearrange("p b j t -> p b (j t)"),
-                    in_=frame_level_feature[batches].rearrange("b (p j) t -> p b (j t)", j=PACK),
-                )
-                highest = operand_pool.tile([P, ROUND, PROPOSALS, PACK], BF16)
-                for b in range(ROUND):
-                    for part in range(PARTS):
-                        first = (ROUND * r + b) * PROPOSALS + PART * part
-                        mask = mask_pool.tile([P, PART, FRAMES], BF16)
-                        for n0 in range(0, PART, RUN):
-                            distance = distance_pool.tile([P, RUN, FRAMES], F32)
-                            for i in range(RUN):
-                                w = first + n0 + i
-                                nc.scalar.activation(
-                                    out=distance[:, i, :], in_=frame_number[:], func=ACT.Abs, bias=neg_middle[:, w : w + 1], scale=1.0
-                                )
-                            for i in range(RUN):
-                                w = first + n0 + i
-                                nc.scalar.activation(
-                                    out=mask[:, n0 + i, :], in_=distance[:, i, :], func=ACT.Identity, bias=big_half_width[:, w : w + 1], scale=-BIG
-                                )
-                        joint = work_pool.tile([P, PACK, PART, JOINT], BF16)
-                        for j0 in range(0, PACK, 2):
-                            pair = []
-                            for j in (j0, j0 + 1):
-                                inside = work_pool.tile([P, PART, FRAMES], BF16, name="inside", tag="inside%d" % (j - j0), bufs=1)
-                                nc.vector.tensor_tensor(
-                                    out=inside[:],
-                                    in0=feature[:, b, j, :].unsqueeze(1).to_broadcast([P, PART, FRAMES]),
-                                    in1=mask[:],
-                                    op=ALU.min,
-                                )
-                                pair.append(inside)
-                            for width in (FRAMES // 2, FRAMES // 4):
-                                for inside in pair:
-                                    nc.vector.tensor_tensor(
-                                        out=inside[:, :, 0:width], in0=inside[:, :, 0:width], in1=inside[:, :, width : 2 * width], op=ALU.max
-                                    )
-                            for j, inside in zip((j0, j0 + 1), pair):
-                                nc.vector.tensor_tensor(
-                                    out=joint[:, j], in0=inside[:, :, 0:JOINT], in1=inside[:, :, JOINT : 2 * JOINT], op=ALU.max
-                                )
-                        for width in (16, 8, 4, 2):
-                            nc.vector.tensor_tensor(
-                                out=joint[:, :, :, 0:width], in0=joint[:, :, :, 0:width], in1=joint[:, :, :, width : 2 * width], op=ALU.max
-                            )
-                        nc.vector.tensor_tensor(
-                            out=highest[:, b, PART * part : PART * (part + 1), :].rearrange("p n j -> p j n"),
-                            in0=joint[:, :, :, 0],
-                            in1=joint[:, :, :, 1],
-                            op=ALU.max,
-                        )
+                best = operand_pool.tile([P, CHUNKS, ROUND, PROPOSALS], BF16)
+                for i in range(ROUND):
+                    b = ROUND * r + i
+                    following = prepare(b + 1) if b + 1 < BATCH else None
+                    pool_windows(ready, best, i)
+                    ready = following
 
-                pooled = operand_pool.tile([P, ROUND * PROPOSALS * PACK], BF16, align_bytes=64)
-                flat = highest[:].rearrange("p b n j -> p (b n j)")
-                nc.vector.scalar_tensor_tensor(out=pooled[:], in0=flat, scalar=EMPTY, in1=flat, op0=ALU.is_gt, op1=ALU.mult)
+                kept = operand_pool.tile([P, CHUNKS, ROUND, PROPOSALS], BF16)
+                flat = best[:].rearrange("p q b n -> p (q b n)")
+                nc.vector.scalar_tensor_tensor(
+                    out=kept[:].rearrange("p q b n -> p (q b n)"), in0=flat, scalar=EMPTY, in1=flat, op0=ALU.is_gt, op1=ALU.mult
+                )
+                pooled = operand_pool.tile([P, ROUND, PROPOSALS, PACK], BF16, align_bytes=64)
+                for pair in range(ROUND // 2):
+                    two = slice(2 * pair, 2 * pair + 2)
+                    across = late_psum.tile([P, CHANNELS], BF16, name="across", tag="late")
+                    for q in range(CHUNKS):
+                        nc.tensor.transpose(across[:, P * q : P * (q + 1)], kept[:, q, two, :].rearrange("p b n -> p (b n)"), identity[:])
+                    sorted_channels = operand_pool.tile([P, PACK, P], BF16)
+                    nc.scalar.copy(out=sorted_channels[:], in_=across[:].rearrange("k (p j) -> k j p", j=PACK))
+                    back = late_psum.tile([P, PACK, P], BF16, name="back", tag="late")
+                    for j in range(PACK):
+                        nc.tensor.transpose(back[:, j, :], sorted_channels[:, j, :], identity[:])
+                    nc.scalar.copy(out=pooled[:, two].rearrange("p b n j -> p (b n) j"), in_=back[:].rearrange("p j k -> p k j"))
+
                 codes = operand_pool.tile([P, ROUND * PROPOSALS], U32, align_bytes=64)
                 scales = operand_pool.tile([P, ROUND * PROPOSALS], U8, align_bytes=64)
-                nc.vector.quantize_mx(out=codes[:].bitcast(FP8X4), scales=scales[:], in_=pooled[:])
+                nc.vector.quantize_mx(out=codes[:].bitcast(FP8X4), scales=scales[:], in_=pooled[:].rearrange("p b n j -> p (b n j)"))
 
-                stats = OUT_TILES * ROUND
-                y = norm_pool.tile([P, OUT_TILES, ROUND, PROPOSALS], F32)
+                stats = CHUNKS * ROUND
+                y = norm_pool.tile([P, CHUNKS, ROUND, PROPOSALS], F32)
                 row_sum = norm_pool.tile([P, stats], F32)
-                for q in range(OUT_TILES):
+                for q in range(CHUNKS):
                     cols = slice(P * q, P * (q + 1))
-                    product = product_pool.tile([P, ROUND, PROPOSALS], F32)
+                    product = late_psum.tile([P, ROUND, PROPOSALS], F32, name="product", tag="late")
                     nc.tensor.matmul_mx(
                         out=product[:].rearrange("p b n -> p (b n)"),
                         lhsT=w_words[:, cols].bitcast(FP8X4),
@@ -202,40 +321,40 @@ def tile_coarsepyramid_pb_kernel(
                         start=True,
                         stop=True,
                     )
-                    for b in range(ROUND):
-                        s = ROUND * q + b
+                    for i in range(ROUND):
+                        s = ROUND * q + i
                         nc.scalar.activation(
-                            out=y[:, q, b, :], in_=product[:, b, :], func=ACT.Identity, bias=bias_col[:, q : q + 1], scale=1.0,
+                            out=y[:, q, i, :], in_=product[:, i, :], func=ACT.Identity, bias=bias_col[:, q : q + 1], scale=1.0,
                             accum_out=row_sum[:, s : s + 1],
                         )
-                group_sum = sum_pool.tile([P, stats], F32)
+                group_sum = late_psum.tile([P, stats], F32, name="group_sum", tag="late")
                 nc.tensor.matmul(out=group_sum[:], lhsT=same_group[:], rhs=row_sum[:], start=True, stop=True)
                 neg_mean = norm_pool.tile([P, stats], F32)
                 nc.vector.tensor_scalar(out=neg_mean[:], in0=group_sum[:], scalar1=-1.0 / GROUP_SIZE, scalar2=None, op0=ALU.mult)
 
-                squares = norm_pool.tile([P, OUT_TILES, ROUND, PROPOSALS], F32)
+                squares = norm_pool.tile([P, CHUNKS, ROUND, PROPOSALS], F32)
                 row_squares = norm_pool.tile([P, stats], F32)
-                for q in range(OUT_TILES):
-                    for b in range(ROUND):
-                        s = ROUND * q + b
+                for q in range(CHUNKS):
+                    for i in range(ROUND):
+                        s = ROUND * q + i
                         nc.scalar.activation(
-                            out=squares[:, q, b, :], in_=y[:, q, b, :], func=ACT.Square, bias=neg_mean[:, s : s + 1], scale=1.0,
+                            out=squares[:, q, i, :], in_=y[:, q, i, :], func=ACT.Square, bias=neg_mean[:, s : s + 1], scale=1.0,
                             accum_out=row_squares[:, s : s + 1],
                         )
-                group_squares = sum_pool.tile([P, stats], F32)
+                group_squares = late_psum.tile([P, stats], F32, name="group_squares", tag="late")
                 nc.tensor.matmul(out=group_squares[:], lhsT=same_group[:], rhs=row_squares[:], start=True, stop=True)
                 deviation = norm_pool.tile([P, stats], F32)
                 nc.scalar.activation(out=deviation[:], in_=group_squares[:], func=ACT.Sqrt, bias=eps_col[:, 0:1], scale=1.0 / GROUP_SIZE)
 
-                factor = norm_pool.tile([P, OUT_TILES, ROUND], F32)
+                factor = norm_pool.tile([P, CHUNKS, ROUND], F32)
                 nc.vector.reciprocal(out=factor[:].rearrange("p q b -> p (q b)"), in_=deviation[:])
-                nc.vector.tensor_tensor(out=factor[:], in0=factor[:], in1=gain_col.unsqueeze(2).to_broadcast([P, OUT_TILES, ROUND]), op=ALU.mult)
-                offset = norm_pool.tile([P, OUT_TILES, ROUND], F32)
-                nc.vector.tensor_tensor(out=offset[:], in0=factor[:], in1=neg_mean[:].rearrange("p (q b) -> p q b", q=OUT_TILES), op=ALU.mult)
-                nc.vector.tensor_tensor(out=offset[:], in0=offset[:], in1=shift_col.unsqueeze(2).to_broadcast([P, OUT_TILES, ROUND]), op=ALU.add)
-                for q in range(OUT_TILES):
-                    for b in range(ROUND):
+                nc.vector.tensor_tensor(out=factor[:], in0=factor[:], in1=gain_col.unsqueeze(2).to_broadcast([P, CHUNKS, ROUND]), op=ALU.mult)
+                offset = norm_pool.tile([P, CHUNKS, ROUND], F32)
+                nc.vector.tensor_tensor(out=offset[:], in0=factor[:], in1=neg_mean[:].rearrange("p (q b) -> p q b", q=CHUNKS), op=ALU.mult)
+                nc.vector.tensor_tensor(out=offset[:], in0=offset[:], in1=shift_col.unsqueeze(2).to_broadcast([P, CHUNKS, ROUND]), op=ALU.add)
+                for q in range(CHUNKS):
+                    for i in range(ROUND):
                         nc.scalar.activation(
-                            out=y[:, q, b, :], in_=y[:, q, b, :], func=ACT.Relu, bias=offset[:, q, b : b + 1], scale=factor[:, q, b : b + 1]
+                            out=y[:, q, i, :], in_=y[:, q, i, :], func=ACT.Relu, bias=offset[:, q, i : i + 1], scale=factor[:, q, i : i + 1]
                         )
                     nc.sync.dma_start(out=out[batches, P * q : P * (q + 1), :].rearrange("b p n -> p b n"), in_=y[:, q])

@@ -33,7 +33,7 @@ BLOCKS = FRAMES // BLOCK
 CELLS = 2 * RUN_FRAMES + BLOCKS
 KEYS = 2 * RUN_WORDS
 SPREAD = CELLS + KEYS
-BANK = 8
+SPREAD_WORDS = SPREAD // 2
 BANK_WORDS = 512
 SHARE = 16
 RING = 4
@@ -195,6 +195,12 @@ def tile_coarsepyramid_pb_kernel(
             )
             nc.vector.tensor_scalar(out=window_table[:, :, 0:CELLS], in0=distance[:], scalar1=-BIG, scalar2=None, op0=ALU.mult)
 
+        parked = out[BATCH - ROUND : BATCH].rearrange("b c n -> (b c n)")
+        nc.sync.dma_start(
+            out=parked[0 : BATCH * QUERIES * SPREAD_WORDS].rearrange("(b k w) -> k b w", k=QUERIES, w=SPREAD_WORDS),
+            in_=window_table[:].rearrange("k b s -> k (b s)").bitcast(F32).rearrange("k (b w) -> k b w", w=SPREAD_WORDS),
+        )
+
         select_ring = []
         for s in range(RING):
             select = const.tile([P, SHARE, P], F32, name="select%d" % s)
@@ -203,9 +209,9 @@ def tile_coarsepyramid_pb_kernel(
 
         with tc.tile_pool(name="batch", bufs=3) as batch_pool, tc.tile_pool(name="work", bufs=2) as work_pool, tc.tile_pool(
             name="operands", bufs=2
-        ) as operand_pool, tc.tile_pool(name="norm", bufs=1) as norm_pool, tc.psum_pool(name="table_psum", bufs=1) as table_psum, tc.psum_pool(
-            name="spread_psum", bufs=2
-        ) as spread_psum, tc.psum_pool(name="gather_psum", bufs=3) as gather_psum, tc.psum_pool(name="late_psum", bufs=2) as late_psum:
+        ) as operand_pool, tc.tile_pool(name="norm", bufs=1) as norm_pool, tc.psum_pool(name="table_psum", bufs=2) as table_psum, tc.psum_pool(
+            name="gather_psum", bufs=4
+        ) as gather_psum, tc.psum_pool(name="late_psum", bufs=2) as late_psum:
 
             def prepare(b):
                 feature = batch_pool.tile([P, CHUNKS, FRAMES], BF16, name="feature")
@@ -227,12 +233,10 @@ def tile_coarsepyramid_pb_kernel(
                 )
 
                 window = batch_pool.tile([P, QUERIES, SPREAD], BF16, name="window")
-                for g in range(SPREAD // BANK):
-                    spread = spread_psum.tile([P, BANK, QUERIES], BF16, name="spread")
-                    for i in range(BANK):
-                        col = BANK * g + i
-                        nc.tensor.transpose(spread[:, i, :], window_table[:, b, col : col + 1].to_broadcast([P, P]), identity[:])
-                    nc.scalar.copy(out=window[:, :, BANK * g : BANK * (g + 1)], in_=spread[:].rearrange("p i k -> p k i"))
+                row = QUERIES * SPREAD_WORDS
+                nc.sync.dma_start(
+                    out=window[:].rearrange("p k s -> p (k s)").bitcast(F32), in_=parked[row * b : row * (b + 1)].partition_broadcast(P)
+                )
                 return table, block_max, window
 
             def pool_windows(prepared, best, i):

@@ -254,10 +254,15 @@ def tile_coarsepyramid_pb_kernel(
                                 scalar2=None,
                                 op0=ALU.is_equal,
                             )
-                        for q in (2 * half, 2 * half + 1):
+                        chunks = (2 * half, 2 * half + 1)
+                        banks = []
+                        for q in chunks:
                             runs = gather_psum.tile([P, BANK_WORDS], F32, name="runs")
-                            for n in range(SWEEP):
+                            banks.append(runs)
+                        for n in range(SWEEP):
+                            for q, runs in zip(chunks, banks):
                                 nc.tensor.transpose(runs[:, KEYS * n : KEYS * n + P], table[:, q, :], shares[n // SHARE][:, n % SHARE, :])
+                        for q, runs in zip(chunks, banks):
                             nc.vector.tensor_tensor(
                                 out=cells[:, q, SWEEP * sweep : SWEEP * (sweep + 1), 0 : 2 * RUN_FRAMES],
                                 in0=runs[:, 0 : KEYS * SWEEP].bitcast(BF16).rearrange("p (n f) -> p n f", f=2 * RUN_FRAMES),

@@ -85,6 +85,8 @@ def tile_coarsepyramid_pb_kernel(
         shift_col = columns[:, 2 * CHUNKS : 3 * CHUNKS]
         eps_col = const.tile([P, 1], F32)
         nc.vector.memset(eps_col[:], EPS)
+        one_col = const.tile([P, 1], F32)
+        nc.vector.memset(one_col[:], 1.0)
 
         column_group = const.tile([P, P], I32)
         nc.gpsimd.iota(column_group[:], pattern=[[1, P // GROUP_CHANNELS], [0, GROUP_CHANNELS]], base=0, channel_multiplier=0)
@@ -100,8 +102,8 @@ def tile_coarsepyramid_pb_kernel(
         nc.vector.tensor_scalar(
             out=same_group[:], in0=column_group_f[:], scalar1=partition_group_f[:, 0:1], scalar2=None, op0=ALU.is_equal
         )
-        partition_number = const.tile([P, 1], F32)
-        nc.vector.tensor_copy(out=partition_number[:], in_=partition_index[:])
+        neg_partition = const.tile([P, 1], F32)
+        nc.vector.tensor_scalar(out=neg_partition[:], in0=partition_index[:], scalar1=-1.0, scalar2=None, op0=ALU.mult)
 
         count_int = const.tile([P, BLOCKS], I32)
         nc.gpsimd.iota(count_int[:], pattern=[[1, BLOCKS]], base=0, channel_multiplier=0)
@@ -207,7 +209,7 @@ def tile_coarsepyramid_pb_kernel(
             nc.vector.memset(select[:], 0.0)
             select_ring.append(select)
 
-        with tc.tile_pool(name="batch", bufs=3) as batch_pool, tc.tile_pool(name="work", bufs=2) as work_pool, tc.tile_pool(
+        with tc.tile_pool(name="batch", bufs=3) as batch_pool, tc.tile_pool(name="work", bufs=1) as work_pool, tc.tile_pool(
             name="operands", bufs=2
         ) as operand_pool, tc.tile_pool(name="norm", bufs=1) as norm_pool, tc.psum_pool(name="table_psum", bufs=2) as table_psum, tc.psum_pool(
             name="gather_psum", bufs=4
@@ -237,44 +239,42 @@ def tile_coarsepyramid_pb_kernel(
                 nc.sync.dma_start(
                     out=window[:].rearrange("p k s -> p (k s)").bitcast(F32), in_=parked[row * b : row * (b + 1)].partition_broadcast(P)
                 )
-                return table, block_max, window
+                apart = batch_pool.tile([P, QUERIES, KEYS], BF16, name="apart")
+                nc.scalar.activation(out=apart[:], in_=window[:, :, CELLS:SPREAD], func=ACT.Abs, bias=neg_partition[:, 0:1], scale=1.0)
+                return table, block_max, window, apart
 
             def pool_windows(prepared, best, i):
-                table, block_max, window = prepared
-                cells = work_pool.tile([P, CHUNKS, PROPOSALS, CELLS], BF16, name="cells")
+                table, block_max, window, apart = prepared
+                fetched = batch_pool.tile([P, CHUNKS, PROPOSALS, KEYS], F32, name="fetched")
                 for half in range(2):
                     for sweep in range(PROPOSALS // SWEEP):
                         first = PROPOSALS * half + SWEEP * sweep
                         shares = select_ring[2 * sweep : 2 * sweep + 2]
                         for s, select in enumerate(shares):
-                            nc.vector.tensor_scalar(
-                                out=select[:, :, 0:KEYS],
-                                in0=window[:, first + SHARE * s : first + SHARE * (s + 1), CELLS:SPREAD],
-                                scalar1=partition_number[:, 0:1],
-                                scalar2=None,
-                                op0=ALU.is_equal,
+                            nc.scalar.activation(
+                                out=select[:, :, 0:KEYS], in_=apart[:, first + SHARE * s : first + SHARE * (s + 1), :], func=ACT.Relu, bias=one_col[:, 0:1], scale=-1.0
                             )
-                        chunks = (2 * half, 2 * half + 1)
-                        banks = []
-                        for q in chunks:
+                        for q in (2 * half, 2 * half + 1):
                             runs = gather_psum.tile([P, BANK_WORDS], F32, name="runs")
-                            banks.append(runs)
-                        for n in range(SWEEP):
-                            for q, runs in zip(chunks, banks):
+                            for n in range(SWEEP):
                                 nc.tensor.transpose(runs[:, KEYS * n : KEYS * n + P], table[:, q, :], shares[n // SHARE][:, n % SHARE, :])
-                        for q, runs in zip(chunks, banks):
-                            nc.vector.tensor_tensor(
-                                out=cells[:, q, SWEEP * sweep : SWEEP * (sweep + 1), 0 : 2 * RUN_FRAMES],
-                                in0=runs[:, 0 : KEYS * SWEEP].bitcast(BF16).rearrange("p (n f) -> p n f", f=2 * RUN_FRAMES),
-                                in1=window[:, first : first + SWEEP, 0 : 2 * RUN_FRAMES],
-                                op=ALU.min,
+                            nc.scalar.copy(
+                                out=fetched[:, q, SWEEP * sweep : SWEEP * (sweep + 1), :].rearrange("p n w -> p (n w)"), in_=runs[:, 0 : KEYS * SWEEP]
                             )
-                for q in range(CHUNKS):
-                    first = PROPOSALS * (q // 2)
+                cells = work_pool.tile([P, CHUNKS, PROPOSALS, CELLS], BF16, name="cells")
+                for half in range(2):
+                    both = slice(2 * half, 2 * half + 2)
+                    mask = window[:, PROPOSALS * half : PROPOSALS * (half + 1), :].unsqueeze(1)
                     nc.vector.tensor_tensor(
-                        out=cells[:, q, :, 2 * RUN_FRAMES : CELLS],
-                        in0=block_max[:, q, :].unsqueeze(1).to_broadcast([P, PROPOSALS, BLOCKS]),
-                        in1=window[:, first : first + PROPOSALS, 2 * RUN_FRAMES : CELLS],
+                        out=cells[:, both, :, 0 : 2 * RUN_FRAMES],
+                        in0=fetched[:, both].bitcast(BF16),
+                        in1=mask[:, :, :, 0 : 2 * RUN_FRAMES].to_broadcast([P, 2, PROPOSALS, 2 * RUN_FRAMES]),
+                        op=ALU.min,
+                    )
+                    nc.vector.tensor_tensor(
+                        out=cells[:, both, :, 2 * RUN_FRAMES : CELLS],
+                        in0=block_max[:, both, :].unsqueeze(2).to_broadcast([P, 2, PROPOSALS, BLOCKS]),
+                        in1=mask[:, :, :, 2 * RUN_FRAMES : CELLS].to_broadcast([P, 2, PROPOSALS, BLOCKS]),
                         op=ALU.min,
                     )
                 lines = cells[:].rearrange("p q n c -> p (q n) c")

@@ -1,3 +1,4 @@
+import concourse.bass as bass
 import concourse.mybir as mybir
 from concourse.masks import make_identity
 
@@ -11,11 +12,13 @@ U8 = mybir.dt.uint8
 FP8X4 = mybir.dt.float8_e4m3fn_x4
 ALU = mybir.AluOpType
 ACT = mybir.ActivationFunctionType
+AXIS = mybir.AxisListType
 
 P = 128
 PACK = 4
 BATCH = 48
 CHANNELS = 512
+HALF = CHANNELS // 2
 FRAMES = 256
 PROPOSALS = 64
 GROUP_CHANNELS = 16
@@ -24,31 +27,28 @@ EPS = 1e-5
 ROUND = 8
 ROUNDS = BATCH // ROUND
 CHUNKS = CHANNELS // P
-QUERIES = 2 * PROPOSALS
-WORDS = FRAMES // 2
-RUN_WORDS = 4
-RUN_FRAMES = 2 * RUN_WORDS
-BLOCK = 2 * RUN_WORDS
-BLOCKS = FRAMES // BLOCK
-CELLS = 2 * RUN_FRAMES + BLOCKS
-KEYS = 2 * RUN_WORDS
-SPREAD = CELLS + KEYS
-SPREAD_WORDS = SPREAD // 2
-BANK_WORDS = 512
-SHARE = 16
-RING = 4
-SWEEP = 32
-
-EDGE = 2.0 ** -10
-BIG = 2.0 ** 110
-EMPTY = -(2.0 ** 99)
-ROUNDER = 1.5 * 2.0 ** 23
+LEVELS = 8
+TABLE_TILES = 15
+ENTRIES = TABLE_TILES * P
+ROW_WORDS = HALF // 2
+REGIONS = 3
+REGION_ROWS = 2 * ENTRIES
+BANK_TILES = 2
+VECTOR_BANKS = (6, 7)
 
 
 def tile_coarsepyramid_pb_kernel(
     tc, frame_level_feature, frame_segments, w_roi_words, w_roi_scales, b_roi, g_roi, be_roi, out
 ):
     nc = tc.nc
+    level_size = [FRAMES] + [FRAMES + 2 - 2 ** k for k in range(1, LEVELS)]
+    level_start = [sum(level_size[0:k]) for k in range(LEVELS)]
+    assert level_start[LEVELS - 1] + level_size[LEVELS - 1] <= ENTRIES
+
+    flat_out = out.rearrange("b c n -> (b c n)")
+    out_rows = flat_out.rearrange("(r w) -> r w", w=ROW_WORDS)
+    assert REGIONS * REGION_ROWS <= BATCH * CHANNELS * PROPOSALS // ROW_WORDS
+
     with tc.tile_pool(name="const", bufs=1) as const:
         w_words = const.tile([P, CHANNELS], U32, align_bytes=64)
         nc.sync.dma_start(
@@ -65,28 +65,6 @@ def tile_coarsepyramid_pb_kernel(
 
         identity = const.tile([P, P], BF16)
         make_identity(nc, identity[:])
-        identity_words = const.tile([P, P], F32)
-        make_identity(nc, identity_words[:])
-
-        rows = const.tile([P, P], BF16)
-        nc.vector.memset(rows[:], 0.0)
-        for i, vector in enumerate((b_roi, g_roi, be_roi)):
-            nc.sync.dma_start(
-                out=rows[CHUNKS * i : CHUNKS * (i + 1), :],
-                in_=vector.rearrange("(q p) -> q p", p=P),
-            )
-        columns = const.tile([P, 3 * CHUNKS], F32)
-        with tc.psum_pool(name="setup_psum", bufs=1) as setup_psum:
-            rows_turned = setup_psum.tile([P, P], BF16)
-            nc.tensor.transpose(rows_turned[:], rows[:], identity[:])
-            nc.vector.tensor_copy(out=columns[:], in_=rows_turned[:, 0 : 3 * CHUNKS])
-        bias_col = columns[:, 0:CHUNKS]
-        gain_col = columns[:, CHUNKS : 2 * CHUNKS]
-        shift_col = columns[:, 2 * CHUNKS : 3 * CHUNKS]
-        eps_col = const.tile([P, 1], F32)
-        nc.vector.memset(eps_col[:], EPS)
-        one_col = const.tile([P, 1], F32)
-        nc.vector.memset(one_col[:], 1.0)
 
         column_group = const.tile([P, P], I32)
         nc.gpsimd.iota(column_group[:], pattern=[[1, P // GROUP_CHANNELS], [0, GROUP_CHANNELS]], base=0, channel_multiplier=0)
@@ -98,229 +76,218 @@ def tile_coarsepyramid_pb_kernel(
         nc.vector.tensor_copy(out=column_group_f[:], in_=column_group[:])
         partition_group_f = const.tile([P, 1], F32)
         nc.vector.tensor_copy(out=partition_group_f[:], in_=partition_group[:])
-        same_group = const.tile([P, P], F32)
+        group_average = const.tile([P, P], F32)
         nc.vector.tensor_scalar(
-            out=same_group[:], in0=column_group_f[:], scalar1=partition_group_f[:, 0:1], scalar2=None, op0=ALU.is_equal
+            out=group_average[:], in0=column_group_f[:], scalar1=partition_group_f[:, 0:1], scalar2=1.0 / GROUP_SIZE,
+            op0=ALU.is_equal, op1=ALU.mult,
         )
-        neg_partition = const.tile([P, 1], F32)
-        nc.vector.tensor_scalar(out=neg_partition[:], in0=partition_index[:], scalar1=-1.0, scalar2=None, op0=ALU.mult)
+        partition_f = const.tile([P, 1], F32)
+        nc.vector.tensor_copy(out=partition_f[:], in_=partition_index[:])
+        side = const.tile([P, 1], F32)
+        nc.vector.tensor_scalar(out=side[:], in0=partition_f[:], scalar1=float(PROPOSALS), scalar2=None, op0=ALU.is_ge)
 
-        count_int = const.tile([P, BLOCKS], I32)
-        nc.gpsimd.iota(count_int[:], pattern=[[1, BLOCKS]], base=0, channel_multiplier=0)
-        count = const.tile([P, BLOCKS], F32)
-        nc.vector.tensor_copy(out=count[:], in_=count_int[:])
-        block_middle = const.tile([P, BLOCKS], F32)
-        nc.vector.tensor_scalar(
-            out=block_middle[:], in0=count[:], scalar1=float(BLOCK), scalar2=0.5 * (BLOCK - 1), op0=ALU.mult, op1=ALU.add
-        )
+        rows = const.tile([P, P], BF16)
+        nc.vector.memset(rows[:], 0.0)
+        for i, vector in enumerate((b_roi, g_roi, be_roi)):
+            nc.sync.dma_start(
+                out=rows[CHUNKS * i : CHUNKS * (i + 1), :],
+                in_=vector.rearrange("(q p) -> q p", p=P),
+            )
+        columns = const.tile([P, 3 * CHUNKS], F32)
+        bias_centred = const.tile([P, CHUNKS], F32)
+        with tc.psum_pool(name="setup_psum", bufs=1) as setup_psum:
+            rows_turned = setup_psum.tile([P, P], BF16)
+            nc.tensor.transpose(rows_turned[:], rows[:], identity[:])
+            nc.vector.tensor_copy(out=columns[:], in_=rows_turned[:, 0 : 3 * CHUNKS])
+            bias_rows = const.tile([P, CHUNKS], F32)
+            nc.vector.tensor_scalar(out=bias_rows[:], in0=columns[:, 0:CHUNKS], scalar1=float(PROPOSALS), scalar2=None, op0=ALU.mult)
+            bias_mean = setup_psum.tile([P, CHUNKS], F32)
+            nc.tensor.matmul(out=bias_mean[:], lhsT=group_average[:], rhs=bias_rows[:], start=True, stop=True)
+            nc.vector.tensor_tensor(out=bias_centred[:], in0=columns[:, 0:CHUNKS], in1=bias_mean[:], op=ALU.subtract)
+        gain_col = columns[:, CHUNKS : 2 * CHUNKS]
+        shift_col = columns[:, 2 * CHUNKS : 3 * CHUNKS]
+        eps_col = const.tile([P, 1], F32)
+        nc.vector.memset(eps_col[:], EPS)
 
-        window_table = const.tile([P, BATCH, SPREAD], BF16)
+        row_index = const.tile([P, BATCH, 2], I32)
+        keep = const.tile([P, BATCH, P], BF16)
         with tc.tile_pool(name="setup", bufs=1) as setup:
             segments = setup.tile([P, BATCH, 4], BF16)
             for half in range(2):
                 nc.sync.dma_start(out=segments[64 * half : 64 * half + 64], in_=frame_segments.rearrange("b n s -> n b s"))
-            lower = setup.tile([P, BATCH], F32)
-            upper = setup.tile([P, BATCH], F32)
+            ends = setup.tile([P, 2, BATCH], F32)
             for half in range(2):
                 lanes = slice(64 * half, 64 * half + 64)
+                for e in range(2):
+                    nc.vector.tensor_scalar(
+                        out=ends[lanes, e, :], in0=segments[lanes, :, 2 * half + e], scalar1=0.0, scalar2=FRAMES - 1.0, op0=ALU.max, op1=ALU.min
+                    )
+            as_int = setup.tile([P, 2, BATCH], I32)
+            nc.vector.tensor_copy(out=as_int[:], in_=ends[:])
+            near = setup.tile([P, 2, BATCH], F32)
+            nc.vector.tensor_copy(out=near[:], in_=as_int[:])
+            above = setup.tile([P, 2, BATCH], F32)
+            nc.vector.tensor_tensor(out=above[:], in0=near[:], in1=ends[:], op=ALU.is_gt)
+            whole = setup.tile([P, 2, BATCH], F32)
+            nc.vector.tensor_tensor(out=whole[:], in0=near[:], in1=above[:], op=ALU.subtract)
+            first = whole[:, 0, :]
+            span = setup.tile([P, BATCH], F32)
+            nc.vector.tensor_tensor(out=span[:], in0=whole[:, 1, :], in1=first, op=ALU.subtract)
+            filled = setup.tile([P, BATCH], F32)
+            nc.vector.tensor_scalar(out=filled[:], in0=span[:], scalar1=0.0, scalar2=None, op0=ALU.is_ge)
+            nc.vector.tensor_tensor(
+                out=keep[:],
+                in0=identity[:].unsqueeze(1).to_broadcast([P, BATCH, P]),
+                in1=filled[:].unsqueeze(2).to_broadcast([P, BATCH, P]),
+                op=ALU.mult,
+            )
+            nc.vector.tensor_scalar(out=span[:], in0=span[:], scalar1=0.0, scalar2=None, op0=ALU.max)
+            start = setup.tile([P, BATCH], F32)
+            nc.vector.memset(start[:], 0.0)
+            back = setup.tile([P, BATCH], F32)
+            nc.vector.memset(back[:], 0.0)
+            step = setup.tile([P, 2, BATCH], F32)
+            for k in range(1, LEVELS):
                 nc.vector.tensor_scalar(
-                    out=lower[lanes, :], in0=segments[lanes, :, 2 * half], scalar1=0.0, scalar2=FRAMES - 1.0, op0=ALU.max, op1=ALU.min
+                    out=step[:, 0, :], in0=span[:], scalar1=2.0 ** k - 1.0, scalar2=float(level_start[k] - level_start[k - 1]),
+                    op0=ALU.is_ge, op1=ALU.mult,
                 )
                 nc.vector.tensor_scalar(
-                    out=upper[lanes, :], in0=segments[lanes, :, 2 * half + 1], scalar1=0.0, scalar2=FRAMES - 1.0, op0=ALU.max, op1=ALU.min
+                    out=step[:, 1, :], in0=span[:], scalar1=2.0 ** k - 1.0, scalar2=2.0 ** (k - 1), op0=ALU.is_ge, op1=ALU.mult
                 )
-            middle = setup.tile([P, BATCH], F32)
-            nc.vector.tensor_tensor(out=middle[:], in0=lower[:], in1=upper[:], op=ALU.add)
-            nc.vector.tensor_scalar(out=middle[:], in0=middle[:], scalar1=0.5, scalar2=EDGE - 0.5, op0=ALU.mult, op1=ALU.add)
-            half_width = setup.tile([P, BATCH], F32)
-            nc.vector.tensor_tensor(out=half_width[:], in0=upper[:], in1=lower[:], op=ALU.subtract)
-            nc.vector.tensor_scalar(out=half_width[:], in0=half_width[:], scalar1=0.5, scalar2=0.5, op0=ALU.mult, op1=ALU.add)
-
-            end_word = []
-            for end, name in ((lower, "lower_word"), (upper, "upper_word")):
-                nudged = setup.tile([P, BATCH], F32, name=name + "_nudged")
-                nc.vector.tensor_scalar(out=nudged[:], in0=end[:], scalar1=0.5, scalar2=0.5 * EDGE - 0.5, op0=ALU.mult, op1=ALU.add)
-                raised = setup.tile([P, BATCH], F32, name=name + "_raised")
-                nc.vector.tensor_scalar(out=raised[:], in0=nudged[:], scalar1=ROUNDER, scalar2=None, op0=ALU.add)
-                whole = setup.tile([P, BATCH], F32, name=name + "_whole")
-                nc.vector.tensor_scalar(out=whole[:], in0=raised[:], scalar1=-ROUNDER, scalar2=None, op0=ALU.add)
-                as_int = setup.tile([P, BATCH], I32, name=name + "_int")
-                nc.vector.tensor_copy(out=as_int[:], in_=whole[:])
-                word = setup.tile([P, BATCH], F32, name=name)
-                nc.vector.tensor_copy(out=word[:], in_=as_int[:])
-                end_word.append(word)
-            left_start = setup.tile([P, BATCH], F32)
-            nc.vector.tensor_scalar(out=left_start[:], in0=end_word[0][:], scalar1=float(WORDS - KEYS), scalar2=None, op0=ALU.min)
-            after_left = setup.tile([P, BATCH], F32)
-            nc.vector.tensor_scalar(out=after_left[:], in0=left_start[:], scalar1=float(RUN_WORDS), scalar2=None, op0=ALU.add)
-            right_start = setup.tile([P, BATCH], F32)
-            nc.vector.tensor_scalar(out=right_start[:], in0=end_word[1][:], scalar1=-float(RUN_WORDS - 1), scalar2=None, op0=ALU.add)
-            nc.vector.tensor_tensor(out=right_start[:], in0=right_start[:], in1=after_left[:], op=ALU.max)
-
-            distance = setup.tile([P, BATCH, CELLS], F32)
-            for i, start in enumerate((left_start, right_start)):
-                keys = slice(CELLS + RUN_WORDS * i, CELLS + RUN_WORDS * (i + 1))
-                nc.vector.tensor_tensor(
-                    out=window_table[:, :, keys],
-                    in0=start[:].unsqueeze(2).to_broadcast([P, BATCH, RUN_WORDS]),
-                    in1=count[:, 0:RUN_WORDS].unsqueeze(1).to_broadcast([P, BATCH, RUN_WORDS]),
-                    op=ALU.add,
-                )
-                from_middle = setup.tile([P, BATCH], F32, name="from_middle%d" % i)
-                nc.vector.scalar_tensor_tensor(out=from_middle[:], in0=start[:], scalar=2.0, in1=middle[:], op0=ALU.mult, op1=ALU.subtract)
-                nc.vector.tensor_tensor(
-                    out=distance[:, :, RUN_FRAMES * i : RUN_FRAMES * (i + 1)],
-                    in0=from_middle[:].unsqueeze(2).to_broadcast([P, BATCH, RUN_FRAMES]),
-                    in1=count[:, 0:RUN_FRAMES].unsqueeze(1).to_broadcast([P, BATCH, RUN_FRAMES]),
-                    op=ALU.add,
-                )
-            nc.vector.tensor_tensor(
-                out=distance[:, :, 2 * RUN_FRAMES : CELLS],
-                in0=block_middle[:].unsqueeze(1).to_broadcast([P, BATCH, BLOCKS]),
-                in1=middle[:].unsqueeze(2).to_broadcast([P, BATCH, BLOCKS]),
-                op=ALU.subtract,
+                nc.vector.tensor_tensor(out=start[:], in0=start[:], in1=step[:, 0, :], op=ALU.add)
+                nc.vector.tensor_tensor(out=back[:], in0=back[:], in1=step[:, 1, :], op=ALU.add)
+            entry = setup.tile([P, BATCH, 2], F32)
+            nc.vector.tensor_tensor(out=entry[:, :, 0], in0=start[:], in1=first, op=ALU.add)
+            nc.vector.tensor_tensor(out=span[:], in0=span[:], in1=back[:], op=ALU.subtract)
+            nc.vector.tensor_tensor(out=entry[:, :, 1], in0=entry[:, :, 0], in1=span[:], op=ALU.add)
+            entry_int = setup.tile([P, BATCH, 2], I32)
+            nc.vector.tensor_copy(out=entry_int[:], in_=entry[:])
+            tile_int = setup.tile([P, BATCH, 2], I32)
+            nc.vector.tensor_single_scalar(out=tile_int[:], in_=entry_int[:], scalar=7, op=ALU.arith_shift_right)
+            tile_f = setup.tile([P, BATCH, 2], F32)
+            nc.vector.tensor_copy(out=tile_f[:], in_=tile_int[:])
+            row_f = setup.tile([P, BATCH, 2], F32)
+            nc.vector.tensor_scalar(
+                out=row_f[:], in0=entry[:], scalar1=2.0 * TABLE_TILES, scalar2=side[:, 0:1], op0=ALU.mult, op1=ALU.add
             )
-            nc.scalar.activation(out=distance[:], in_=distance[:], func=ACT.Abs)
-            block_reach = setup.tile([P, BATCH], F32)
-            nc.vector.tensor_scalar(out=block_reach[:], in0=half_width[:], scalar1=-0.5 * (BLOCK - 1), scalar2=None, op0=ALU.add)
-            nc.vector.tensor_tensor(
-                out=distance[:, :, 0 : 2 * RUN_FRAMES],
-                in0=distance[:, :, 0 : 2 * RUN_FRAMES],
-                in1=half_width[:].unsqueeze(2).to_broadcast([P, BATCH, 2 * RUN_FRAMES]),
-                op=ALU.subtract,
+            nc.vector.scalar_tensor_tensor(
+                out=row_f[:], in0=tile_f[:], scalar=2.0 - 2.0 * TABLE_TILES * P, in1=row_f[:], op0=ALU.mult, op1=ALU.add
             )
-            nc.vector.tensor_tensor(
-                out=distance[:, :, 2 * RUN_FRAMES : CELLS],
-                in0=distance[:, :, 2 * RUN_FRAMES : CELLS],
-                in1=block_reach[:].unsqueeze(2).to_broadcast([P, BATCH, BLOCKS]),
-                op=ALU.subtract,
-            )
-            nc.vector.tensor_scalar(out=window_table[:, :, 0:CELLS], in0=distance[:], scalar1=-BIG, scalar2=None, op0=ALU.mult)
+            region_int = setup.tile([P, BATCH], I32)
+            nc.gpsimd.iota(region_int[:], pattern=[[0, BATCH // REGIONS], [REGION_ROWS, REGIONS]], base=0, channel_multiplier=0)
+            region_f = setup.tile([P, BATCH], F32)
+            nc.vector.tensor_copy(out=region_f[:], in_=region_int[:])
+            nc.vector.tensor_tensor(out=row_f[:], in0=row_f[:], in1=region_f[:].unsqueeze(2).to_broadcast([P, BATCH, 2]), op=ALU.add)
+            nc.vector.tensor_copy(out=row_index[:], in_=row_f[:])
 
-        parked = out[BATCH - ROUND : BATCH].rearrange("b c n -> (b c n)")
-        nc.sync.dma_start(
-            out=parked[0 : BATCH * QUERIES * SPREAD_WORDS].rearrange("(b k w) -> k b w", k=QUERIES, w=SPREAD_WORDS),
-            in_=window_table[:].rearrange("k b s -> k (b s)").bitcast(F32).rearrange("k (b w) -> k b w", w=SPREAD_WORDS),
-        )
+        table_ring = []
+        for s in range(REGIONS):
+            table = const.tile([P, CHUNKS, ENTRIES], BF16, name="table%d" % s)
+            nc.vector.memset(table[:, :, level_start[1] + FRAMES - 1 : level_start[2]], 0.0)
+            nc.vector.memset(table[:, :, level_start[LEVELS - 1] + level_size[LEVELS - 1] : ENTRIES], 0.0)
+            table_ring.append(table)
 
-        select_ring = []
-        for s in range(RING):
-            select = const.tile([P, SHARE, P], F32, name="select%d" % s)
-            nc.vector.memset(select[:], 0.0)
-            select_ring.append(select)
+        best_ring = []
+        for s in range(3):
+            best = const.tile([P, 2, HALF + P], BF16, name="best%d" % s)
+            nc.vector.memset(best[:], 0.0)
+            best_ring.append(best)
 
-        with tc.tile_pool(name="batch", bufs=3) as batch_pool, tc.tile_pool(name="work", bufs=1) as work_pool, tc.tile_pool(
+        result = const.tile([P, CHUNKS, BATCH, PROPOSALS], F32)
+
+        with tc.tile_pool(name="turned", bufs=3) as turned_pool, tc.tile_pool(name="fetch", bufs=4) as fetch_pool, tc.tile_pool(
             name="operands", bufs=2
-        ) as operand_pool, tc.tile_pool(name="norm", bufs=1) as norm_pool, tc.psum_pool(name="table_psum", bufs=2) as table_psum, tc.psum_pool(
-            name="gather_psum", bufs=4
-        ) as gather_psum, tc.psum_pool(name="late_psum", bufs=2) as late_psum:
+        ) as operand_pool, tc.tile_pool(name="norm", bufs=2) as norm_pool, tc.psum_pool(name="table_psum", bufs=4) as table_psum, tc.psum_pool(
+            name="back_psum", bufs=1
+        ) as back_psum, tc.psum_pool(name="product_psum", bufs=2) as product_psum, tc.psum_pool(name="stat_psum", bufs=1) as stat_psum:
 
-            def prepare(b):
-                feature = batch_pool.tile([P, CHUNKS, FRAMES], BF16, name="feature")
-                nc.sync.dma_start(out=feature[:], in_=frame_level_feature[b].rearrange("(q m) t -> m q t", m=P))
-                turned = table_psum.tile([P, CHUNKS, P], F32, name="turned")
-                for q in range(CHUNKS):
-                    nc.tensor.transpose(turned[:, q, :], feature[:, q, :].bitcast(F32), identity_words[:])
-                table = batch_pool.tile([P, CHUNKS, P], F32, name="table")
-                nc.scalar.copy(out=table[:], in_=turned[:])
-
-                blocks = feature[:].rearrange("m q (a f) -> m (q a) f", f=BLOCK)
-                of_four = batch_pool.tile([P, CHUNKS * BLOCKS, 4], BF16, name="of_four")
-                nc.vector.tensor_tensor(out=of_four[:], in0=blocks[:, :, 0:4], in1=blocks[:, :, 4:8], op=ALU.max)
-                of_two = batch_pool.tile([P, CHUNKS * BLOCKS, 2], BF16, name="of_two")
-                nc.vector.tensor_tensor(out=of_two[:], in0=of_four[:, :, 0:2], in1=of_four[:, :, 2:4], op=ALU.max)
-                block_max = batch_pool.tile([P, CHUNKS, BLOCKS], BF16, name="block_max")
-                nc.vector.tensor_tensor(
-                    out=block_max[:].rearrange("m q a -> m (q a)"), in0=of_two[:, :, 0], in1=of_two[:, :, 1], op=ALU.max
-                )
-
-                window = batch_pool.tile([P, QUERIES, SPREAD], BF16, name="window")
-                row = QUERIES * SPREAD_WORDS
-                nc.sync.dma_start(
-                    out=window[:].rearrange("p k s -> p (k s)").bitcast(F32), in_=parked[row * b : row * (b + 1)].partition_broadcast(P)
-                )
-                apart = batch_pool.tile([P, QUERIES, KEYS], BF16, name="apart")
-                nc.scalar.activation(out=apart[:], in_=window[:, :, CELLS:SPREAD], func=ACT.Abs, bias=neg_partition[:, 0:1], scale=1.0)
-                return table, block_max, window, apart
-
-            def pool_windows(prepared, best, i):
-                table, block_max, window, apart = prepared
-                fetched = batch_pool.tile([P, CHUNKS, PROPOSALS, KEYS], F32, name="fetched")
+            def load(b):
+                table = table_ring[b % REGIONS]
                 for half in range(2):
-                    for sweep in range(PROPOSALS // SWEEP):
-                        first = PROPOSALS * half + SWEEP * sweep
-                        shares = select_ring[2 * sweep : 2 * sweep + 2]
-                        for s, select in enumerate(shares):
-                            nc.scalar.activation(
-                                out=select[:, :, 0:KEYS], in_=apart[:, first + SHARE * s : first + SHARE * (s + 1), :], func=ACT.Relu, bias=one_col[:, 0:1], scale=-1.0
-                            )
-                        for q in (2 * half, 2 * half + 1):
-                            runs = gather_psum.tile([P, BANK_WORDS], F32, name="runs")
-                            for n in range(SWEEP):
-                                nc.tensor.transpose(runs[:, KEYS * n : KEYS * n + P], table[:, q, :], shares[n // SHARE][:, n % SHARE, :])
-                            nc.scalar.copy(
-                                out=fetched[:, q, SWEEP * sweep : SWEEP * (sweep + 1), :].rearrange("p n w -> p (n w)"), in_=runs[:, 0 : KEYS * SWEEP]
-                            )
-                cells = work_pool.tile([P, CHUNKS, PROPOSALS, CELLS], BF16, name="cells")
-                for half in range(2):
-                    both = slice(2 * half, 2 * half + 2)
-                    mask = window[:, PROPOSALS * half : PROPOSALS * (half + 1), :].unsqueeze(1)
-                    nc.vector.tensor_tensor(
-                        out=cells[:, both, :, 0 : 2 * RUN_FRAMES],
-                        in0=fetched[:, both].bitcast(BF16),
-                        in1=mask[:, :, :, 0 : 2 * RUN_FRAMES].to_broadcast([P, 2, PROPOSALS, 2 * RUN_FRAMES]),
-                        op=ALU.min,
+                    nc.sync.dma_start(
+                        out=table[:, 2 * half : 2 * half + 2, 0:FRAMES],
+                        in_=frame_level_feature[b, HALF * half : HALF * (half + 1), :].rearrange("(m j) t -> m j t", j=2),
                     )
-                    nc.vector.tensor_tensor(
-                        out=cells[:, both, :, 2 * RUN_FRAMES : CELLS],
-                        in0=block_max[:, both, :].unsqueeze(2).to_broadcast([P, 2, PROPOSALS, BLOCKS]),
-                        in1=mask[:, :, :, 2 * RUN_FRAMES : CELLS].to_broadcast([P, 2, PROPOSALS, BLOCKS]),
-                        op=ALU.min,
-                    )
-                lines = cells[:].rearrange("p q n c -> p (q n) c")
-                nc.vector.tensor_tensor(out=lines[:, :, 16:32], in0=lines[:, :, 16:32], in1=lines[:, :, 32:48], op=ALU.max)
-                for width in (16, 8, 4, 2):
-                    nc.vector.tensor_tensor(out=lines[:, :, 0:width], in0=lines[:, :, 0:width], in1=lines[:, :, width : 2 * width], op=ALU.max)
-                nc.vector.tensor_tensor(out=best[:, :, i, :], in0=cells[:, :, :, 0], in1=cells[:, :, :, 1], op=ALU.max)
 
-            ready = prepare(0)
-            for r in range(ROUNDS):
+            def build(b):
+                table = table_ring[b % REGIONS]
+                region = flat_out[(b % REGIONS) * REGION_ROWS * ROW_WORDS : (b % REGIONS + 1) * REGION_ROWS * ROW_WORDS].rearrange(
+                    "(p a w) -> p a w", p=P, w=2 * ROW_WORDS
+                )
+                for k in range(1, LEVELS):
+                    width = level_size[k] if k > 1 else FRAMES - 1
+                    lower = level_start[k - 1]
+                    nc.vector.tensor_tensor(
+                        out=table[:, :, level_start[k] : level_start[k] + width],
+                        in0=table[:, :, lower : lower + width],
+                        in1=table[:, :, lower + 2 ** (k - 1) : lower + 2 ** (k - 1) + width],
+                        op=ALU.max,
+                    )
+                turned = turned_pool.tile([P, TABLE_TILES, CHANNELS], BF16, name="turned")
+                turned_words = turned[:].rearrange("p a c -> p (a c)").bitcast(F32).rearrange("p (a w) -> p a w", w=2 * ROW_WORDS)
+                banks = (TABLE_TILES + BANK_TILES - 1) // BANK_TILES
+                for bank in range(banks):
+                    tiles = range(BANK_TILES * bank, min(BANK_TILES * (bank + 1), TABLE_TILES))
+                    landing = table_psum.tile([P, BANK_TILES, CHUNKS, P], BF16, name="landing")
+                    for a in tiles:
+                        for q in range(CHUNKS):
+                            nc.tensor.transpose(landing[:, a - tiles[0], q, :], table[:, q, P * a : P * (a + 1)], identity[:])
+                    count = len(tiles)
+                    target = turned[:, tiles[0] : tiles[0] + count, :].rearrange("p a c -> p (a c)")
+                    source = landing[:, 0:count].rearrange("p a q m -> p (a q m)")
+                    if bank in VECTOR_BANKS:
+                        nc.vector.tensor_copy(out=target, in_=source)
+                    else:
+                        nc.scalar.copy(out=target, in_=source)
+                    if bank % 2 == 1:
+                        done = slice(BANK_TILES * (bank - 1), tiles[0] + count)
+                        nc.sync.dma_start(out=region[:, done, :], in_=turned_words[:, done, :])
+
+            def fetch(b, fetched):
+                region_rows = out_rows[0 : (b % REGIONS + 1) * REGION_ROWS, :]
+                for s in range(2):
+                    nc.gpsimd.indirect_dma_start(
+                        out=fetched[:, b % 2, s, :],
+                        out_offset=None,
+                        in_=region_rows,
+                        in_offset=bass.IndirectOffsetOnAxis(ap=row_index[:, b, s : s + 1], axis=0),
+                    )
+
+            def pool_pair(b, fetched, pooled):
+                values = fetched[:].rearrange("p b s w -> p (b s w)").bitcast(BF16).rearrange("p (b s c) -> p b s c", b=2, s=2)
+                best = best_ring[(b // 2) % len(best_ring)]
+                for half in range(2):
+                    lanes = slice(64 * half, 64 * half + 64)
+                    nc.vector.tensor_tensor(
+                        out=best[lanes, :, P * half : P * half + HALF], in0=values[lanes, :, 0, :], in1=values[lanes, :, 1, :], op=ALU.max
+                    )
+                back = back_psum.tile([P, 2, PACK, P], BF16, name="back")
+                for i in range(2):
+                    for t in range(PACK):
+                        slot = P * (t % 2) + t // 2
+                        nc.tensor.transpose(
+                            back[:, i, t, :],
+                            best[:, i, slot : slot + 2 * P - 1 : 2],
+                            keep[:, b + i, :],
+                        )
+                for half in range(2):
+                    lanes = slice(64 * half, 64 * half + 64)
+                    nc.scalar.copy(
+                        out=pooled[lanes, b % ROUND : b % ROUND + 2, :, :],
+                        in_=back[lanes, :, :, 64 * half : 64 * half + 64].rearrange("p b t n -> p b n t"),
+                    )
+
+            def finish_round(r, pooled):
                 batches = slice(ROUND * r, ROUND * (r + 1))
-                best = operand_pool.tile([P, CHUNKS, ROUND, PROPOSALS], BF16)
-                for i in range(ROUND):
-                    b = ROUND * r + i
-                    following = prepare(b + 1) if b + 1 < BATCH else None
-                    pool_windows(ready, best, i)
-                    ready = following
-
-                kept = operand_pool.tile([P, CHUNKS, ROUND, PROPOSALS], BF16)
-                flat = best[:].rearrange("p q b n -> p (q b n)")
-                nc.vector.scalar_tensor_tensor(
-                    out=kept[:].rearrange("p q b n -> p (q b n)"), in0=flat, scalar=EMPTY, in1=flat, op0=ALU.is_gt, op1=ALU.mult
-                )
-                pooled = operand_pool.tile([P, ROUND, PROPOSALS, PACK], BF16, align_bytes=64)
-                for pair in range(ROUND // 2):
-                    two = slice(2 * pair, 2 * pair + 2)
-                    across = late_psum.tile([P, CHANNELS], BF16, name="across", tag="late")
-                    for q in range(CHUNKS):
-                        nc.tensor.transpose(across[:, P * q : P * (q + 1)], kept[:, q, two, :].rearrange("p b n -> p (b n)"), identity[:])
-                    sorted_channels = operand_pool.tile([P, PACK, P], BF16)
-                    nc.scalar.copy(out=sorted_channels[:], in_=across[:].rearrange("k (p j) -> k j p", j=PACK))
-                    back = late_psum.tile([P, PACK, P], BF16, name="back", tag="late")
-                    for j in range(PACK):
-                        nc.tensor.transpose(back[:, j, :], sorted_channels[:, j, :], identity[:])
-                    nc.scalar.copy(out=pooled[:, two].rearrange("p b n j -> p (b n) j"), in_=back[:].rearrange("p j k -> p k j"))
-
-                codes = operand_pool.tile([P, ROUND * PROPOSALS], U32, align_bytes=64)
-                scales = operand_pool.tile([P, ROUND * PROPOSALS], U8, align_bytes=64)
+                codes = operand_pool.tile([P, ROUND * PROPOSALS], U32, align_bytes=64, name="codes")
+                scales = operand_pool.tile([P, ROUND * PROPOSALS], U8, align_bytes=64, name="scales")
                 nc.vector.quantize_mx(out=codes[:].bitcast(FP8X4), scales=scales[:], in_=pooled[:].rearrange("p b n j -> p (b n j)"))
-
                 stats = CHUNKS * ROUND
-                y = norm_pool.tile([P, CHUNKS, ROUND, PROPOSALS], F32)
-                row_sum = norm_pool.tile([P, stats], F32)
+                centred = norm_pool.tile([P, CHUNKS, ROUND, PROPOSALS], F32, name="centred")
                 for q in range(CHUNKS):
                     cols = slice(P * q, P * (q + 1))
-                    product = late_psum.tile([P, ROUND, PROPOSALS], F32, name="product", tag="late")
+                    product = product_psum.tile([P, ROUND, PROPOSALS], F32, name="product")
                     nc.tensor.matmul_mx(
                         out=product[:].rearrange("p b n -> p (b n)"),
                         lhsT=w_words[:, cols].bitcast(FP8X4),
@@ -330,40 +297,58 @@ def tile_coarsepyramid_pb_kernel(
                         start=True,
                         stop=True,
                     )
-                    for i in range(ROUND):
-                        s = ROUND * q + i
-                        nc.scalar.activation(
-                            out=y[:, q, i, :], in_=product[:, i, :], func=ACT.Identity, bias=bias_col[:, q : q + 1], scale=1.0,
-                            accum_out=row_sum[:, s : s + 1],
-                        )
-                group_sum = late_psum.tile([P, stats], F32, name="group_sum", tag="late")
-                nc.tensor.matmul(out=group_sum[:], lhsT=same_group[:], rhs=row_sum[:], start=True, stop=True)
-                neg_mean = norm_pool.tile([P, stats], F32)
-                nc.vector.tensor_scalar(out=neg_mean[:], in0=group_sum[:], scalar1=-1.0 / GROUP_SIZE, scalar2=None, op0=ALU.mult)
-
-                squares = norm_pool.tile([P, CHUNKS, ROUND, PROPOSALS], F32)
-                row_squares = norm_pool.tile([P, stats], F32)
+                    row_sum = norm_pool.tile([P, ROUND], F32, name="row_sum")
+                    nc.vector.tensor_reduce(out=row_sum[:], in_=product[:], axis=AXIS.X, op=ALU.add)
+                    group_mean = stat_psum.tile([P, ROUND], F32, name="group_mean", tag="stat")
+                    nc.tensor.matmul(out=group_mean[:], lhsT=group_average[:], rhs=row_sum[:], start=True, stop=True)
+                    to_centre = norm_pool.tile([P, ROUND], F32, name="to_centre")
+                    nc.vector.tensor_scalar(
+                        out=to_centre[:], in0=group_mean[:], scalar1=-1.0, scalar2=bias_centred[:, q : q + 1], op0=ALU.mult, op1=ALU.add
+                    )
+                    nc.vector.tensor_tensor(
+                        out=centred[:, q], in0=product[:], in1=to_centre[:].unsqueeze(2).to_broadcast([P, ROUND, PROPOSALS]), op=ALU.add
+                    )
+                lines = centred[:].rearrange("p q b n -> p (q b) n")
+                squares = norm_pool.tile([P, stats, PROPOSALS], F32, name="squares")
+                nc.scalar.activation(out=squares[:], in_=lines, func=ACT.Square)
+                row_squares = norm_pool.tile([P, stats], F32, name="row_squares")
+                nc.vector.tensor_reduce(out=row_squares[:], in_=squares[:], axis=AXIS.X, op=ALU.add)
+                group_var = stat_psum.tile([P, stats], F32, name="group_var", tag="stat")
+                nc.tensor.matmul(out=group_var[:], lhsT=group_average[:], rhs=row_squares[:], start=True, stop=True)
+                deviation = norm_pool.tile([P, stats], F32, name="deviation")
+                nc.scalar.activation(out=deviation[:], in_=group_var[:], func=ACT.Sqrt, bias=eps_col[:, 0:1], scale=1.0)
+                inverse = norm_pool.tile([P, stats], F32, name="inverse")
+                nc.vector.reciprocal(out=inverse[:], in_=deviation[:])
+                nc.vector.tensor_tensor(out=lines, in0=lines, in1=inverse[:].unsqueeze(2).to_broadcast([P, stats, PROPOSALS]), op=ALU.mult)
                 for q in range(CHUNKS):
-                    for i in range(ROUND):
-                        s = ROUND * q + i
-                        nc.scalar.activation(
-                            out=squares[:, q, i, :], in_=y[:, q, i, :], func=ACT.Square, bias=neg_mean[:, s : s + 1], scale=1.0,
-                            accum_out=row_squares[:, s : s + 1],
-                        )
-                group_squares = late_psum.tile([P, stats], F32, name="group_squares", tag="late")
-                nc.tensor.matmul(out=group_squares[:], lhsT=same_group[:], rhs=row_squares[:], start=True, stop=True)
-                deviation = norm_pool.tile([P, stats], F32)
-                nc.scalar.activation(out=deviation[:], in_=group_squares[:], func=ACT.Sqrt, bias=eps_col[:, 0:1], scale=1.0 / GROUP_SIZE)
+                    nc.scalar.activation(
+                        out=result[:, q, batches, :], in_=centred[:, q], func=ACT.Relu, bias=shift_col[:, q : q + 1], scale=gain_col[:, q : q + 1]
+                    )
 
-                factor = norm_pool.tile([P, CHUNKS, ROUND], F32)
-                nc.vector.reciprocal(out=factor[:].rearrange("p q b -> p (q b)"), in_=deviation[:])
-                nc.vector.tensor_tensor(out=factor[:], in0=factor[:], in1=gain_col.unsqueeze(2).to_broadcast([P, CHUNKS, ROUND]), op=ALU.mult)
-                offset = norm_pool.tile([P, CHUNKS, ROUND], F32)
-                nc.vector.tensor_tensor(out=offset[:], in0=factor[:], in1=neg_mean[:].rearrange("p (q b) -> p q b", q=CHUNKS), op=ALU.mult)
-                nc.vector.tensor_tensor(out=offset[:], in0=offset[:], in1=shift_col.unsqueeze(2).to_broadcast([P, CHUNKS, ROUND]), op=ALU.add)
+            FETCH_LAG = 1
+            POOL_LAG = 3
+            fetched_of = {}
+            pooled_of = {}
+            load(0)
+            for i in range(BATCH + POOL_LAG):
+                if i + 1 < BATCH:
+                    load(i + 1)
+                b = i - FETCH_LAG
+                if 0 <= b < BATCH:
+                    if b % 2 == 0:
+                        fetched_of[b // 2] = fetch_pool.tile([P, 2, 2, ROW_WORDS], F32, name="fetched")
+                    fetch(b, fetched_of[b // 2])
+                if i < BATCH:
+                    build(i)
+                b = i - POOL_LAG
+                if b >= 0 and b % 2 == 1:
+                    if (b - 1) % ROUND == 0:
+                        pooled_of[b // ROUND] = operand_pool.tile([P, ROUND, PROPOSALS, PACK], BF16, align_bytes=64, name="pooled")
+                    pool_pair(b - 1, fetched_of[b // 2], pooled_of[b // ROUND])
+                    if b % ROUND == ROUND - 1:
+                        finish_round(b // ROUND, pooled_of[b // ROUND])
+
+            for r in range(ROUNDS):
+                batches = slice(ROUND * r, ROUND * (r + 1))
                 for q in range(CHUNKS):
-                    for i in range(ROUND):
-                        nc.scalar.activation(
-                            out=y[:, q, i, :], in_=y[:, q, i, :], func=ACT.Relu, bias=offset[:, q, i : i + 1], scale=factor[:, q, i : i + 1]
-                        )
-                    nc.sync.dma_start(out=out[batches, P * q : P * (q + 1), :].rearrange("b p n -> p b n"), in_=y[:, q])
+                    nc.sync.dma_start(out=out[batches, P * q : P * (q + 1), :].rearrange("b p n -> p b n"), in_=result[:, q, batches, :])

@@ -34,7 +34,7 @@ ROW_WORDS = HALF // 2
 REGIONS = 3
 REGION_ROWS = 2 * ENTRIES
 BANK_TILES = 2
-VECTOR_BANKS = (6, 7)
+VECTOR_BANKS = (0,)
 
 
 def tile_coarsepyramid_pb_kernel(
@@ -43,7 +43,8 @@ def tile_coarsepyramid_pb_kernel(
     nc = tc.nc
     level_size = [FRAMES] + [FRAMES + 2 - 2 ** k for k in range(1, LEVELS)]
     level_start = [sum(level_size[0:k]) for k in range(LEVELS)]
-    assert level_start[LEVELS - 1] + level_size[LEVELS - 1] <= ENTRIES
+    used_entries = level_start[LEVELS - 1] + level_size[LEVELS - 1]
+    assert used_entries <= ENTRIES and used_entries // P == TABLE_TILES - 1
 
     flat_out = out.rearrange("b c n -> (b c n)")
     out_rows = flat_out.rearrange("(r w) -> r w", w=ROW_WORDS)
@@ -188,6 +189,12 @@ def tile_coarsepyramid_pb_kernel(
             nc.vector.memset(table[:, :, level_start[LEVELS - 1] + level_size[LEVELS - 1] : ENTRIES], 0.0)
             table_ring.append(table)
 
+        zero_rows = const.tile([P, 2 * ROW_WORDS], F32)
+        nc.vector.memset(zero_rows[:], 0.0)
+        for s in range(REGIONS):
+            unused = flat_out[s * REGION_ROWS * ROW_WORDS : (s + 1) * REGION_ROWS * ROW_WORDS].rearrange("(p a w) -> p a w", p=P, w=2 * ROW_WORDS)
+            nc.sync.dma_start(out=unused[used_entries % P : P, TABLE_TILES - 1, :], in_=zero_rows[used_entries % P : P, :])
+
         best_ring = []
         for s in range(3):
             best = const.tile([P, 2, HALF + P], BF16, name="best%d" % s)
@@ -198,9 +205,9 @@ def tile_coarsepyramid_pb_kernel(
 
         with tc.tile_pool(name="turned", bufs=3) as turned_pool, tc.tile_pool(name="fetch", bufs=4) as fetch_pool, tc.tile_pool(
             name="operands", bufs=2
-        ) as operand_pool, tc.tile_pool(name="norm", bufs=2) as norm_pool, tc.psum_pool(name="table_psum", bufs=4) as table_psum, tc.psum_pool(
-            name="back_psum", bufs=1
-        ) as back_psum, tc.psum_pool(name="product_psum", bufs=2) as product_psum, tc.psum_pool(name="stat_psum", bufs=1) as stat_psum:
+        ) as operand_pool, tc.tile_pool(name="norm", bufs=2) as norm_pool, tc.psum_pool(name="table_psum", bufs=3) as table_psum, tc.psum_pool(
+            name="small_psum", bufs=1
+        ) as small_psum, tc.psum_pool(name="product_psum", bufs=CHUNKS) as product_psum:
 
             def load(b):
                 table = table_ring[b % REGIONS]
@@ -218,12 +225,14 @@ def tile_coarsepyramid_pb_kernel(
                 for k in range(1, LEVELS):
                     width = level_size[k] if k > 1 else FRAMES - 1
                     lower = level_start[k - 1]
-                    nc.vector.tensor_tensor(
-                        out=table[:, :, level_start[k] : level_start[k] + width],
-                        in0=table[:, :, lower : lower + width],
-                        in1=table[:, :, lower + 2 ** (k - 1) : lower + 2 ** (k - 1) + width],
-                        op=ALU.max,
-                    )
+                    for half in range(2):
+                        both = slice(2 * half, 2 * half + 2)
+                        nc.vector.tensor_tensor(
+                            out=table[:, both, level_start[k] : level_start[k] + width],
+                            in0=table[:, both, lower : lower + width],
+                            in1=table[:, both, lower + 2 ** (k - 1) : lower + 2 ** (k - 1) + width],
+                            op=ALU.max,
+                        )
                 turned = turned_pool.tile([P, TABLE_TILES, CHANNELS], BF16, name="turned")
                 turned_words = turned[:].rearrange("p a c -> p (a c)").bitcast(F32).rearrange("p (a w) -> p a w", w=2 * ROW_WORDS)
                 banks = (TABLE_TILES + BANK_TILES - 1) // BANK_TILES
@@ -237,12 +246,16 @@ def tile_coarsepyramid_pb_kernel(
                     target = turned[:, tiles[0] : tiles[0] + count, :].rearrange("p a c -> p (a c)")
                     source = landing[:, 0:count].rearrange("p a q m -> p (a q m)")
                     if bank in VECTOR_BANKS:
-                        nc.vector.tensor_copy(out=target, in_=source)
+                        for a in range(count):
+                            nc.vector.tensor_copy(out=turned[:, tiles[0] + a, :], in_=landing[:, a].rearrange("p q m -> p (q m)"))
                     else:
                         nc.scalar.copy(out=target, in_=source)
                     if bank % 2 == 1:
-                        done = slice(BANK_TILES * (bank - 1), tiles[0] + count)
-                        nc.sync.dma_start(out=region[:, done, :], in_=turned_words[:, done, :])
+                        whole_tiles = slice(BANK_TILES * (bank - 1), min(tiles[0] + count, used_entries // P))
+                        nc.sync.dma_start(out=region[:, whole_tiles, :], in_=turned_words[:, whole_tiles, :])
+                rest = used_entries % P
+                last = slice(used_entries // P, used_entries // P + 1)
+                nc.sync.dma_start(out=region[0:rest, last, :], in_=turned_words[0:rest, last, :])
 
             def fetch(b, fetched):
                 region_rows = out_rows[0 : (b % REGIONS + 1) * REGION_ROWS, :]
@@ -262,7 +275,7 @@ def tile_coarsepyramid_pb_kernel(
                     nc.vector.tensor_tensor(
                         out=best[lanes, :, P * half : P * half + HALF], in0=values[lanes, :, 0, :], in1=values[lanes, :, 1, :], op=ALU.max
                     )
-                back = back_psum.tile([P, 2, PACK, P], BF16, name="back")
+                back = small_psum.tile([P, 2, PACK, P], BF16, name="back", tag="small")
                 for i in range(2):
                     for t in range(PACK):
                         slot = P * (t % 2) + t // 2
@@ -284,7 +297,8 @@ def tile_coarsepyramid_pb_kernel(
                 scales = operand_pool.tile([P, ROUND * PROPOSALS], U8, align_bytes=64, name="scales")
                 nc.vector.quantize_mx(out=codes[:].bitcast(FP8X4), scales=scales[:], in_=pooled[:].rearrange("p b n j -> p (b n j)"))
                 stats = CHUNKS * ROUND
-                centred = norm_pool.tile([P, CHUNKS, ROUND, PROPOSALS], F32, name="centred")
+                products = []
+                row_sum = norm_pool.tile([P, CHUNKS, ROUND], F32, name="row_sum")
                 for q in range(CHUNKS):
                     cols = slice(P * q, P * (q + 1))
                     product = product_psum.tile([P, ROUND, PROPOSALS], F32, name="product")
@@ -297,33 +311,42 @@ def tile_coarsepyramid_pb_kernel(
                         start=True,
                         stop=True,
                     )
-                    row_sum = norm_pool.tile([P, ROUND], F32, name="row_sum")
-                    nc.vector.tensor_reduce(out=row_sum[:], in_=product[:], axis=AXIS.X, op=ALU.add)
-                    group_mean = stat_psum.tile([P, ROUND], F32, name="group_mean", tag="stat")
-                    nc.tensor.matmul(out=group_mean[:], lhsT=group_average[:], rhs=row_sum[:], start=True, stop=True)
-                    to_centre = norm_pool.tile([P, ROUND], F32, name="to_centre")
-                    nc.vector.tensor_scalar(
-                        out=to_centre[:], in0=group_mean[:], scalar1=-1.0, scalar2=bias_centred[:, q : q + 1], op0=ALU.mult, op1=ALU.add
-                    )
-                    nc.vector.tensor_tensor(
-                        out=centred[:, q], in0=product[:], in1=to_centre[:].unsqueeze(2).to_broadcast([P, ROUND, PROPOSALS]), op=ALU.add
-                    )
-                lines = centred[:].rearrange("p q b n -> p (q b) n")
+                    nc.vector.tensor_reduce(out=row_sum[:, q, :], in_=product[:], axis=AXIS.X, op=ALU.add)
+                    products.append(product)
+                group_mean = small_psum.tile([P, CHUNKS, ROUND], F32, name="group_mean", tag="small")
+                nc.tensor.matmul(
+                    out=group_mean[:].rearrange("p q b -> p (q b)"), lhsT=group_average[:], rhs=row_sum[:].rearrange("p q b -> p (q b)"), start=True, stop=True
+                )
+                to_centre = norm_pool.tile([P, CHUNKS, ROUND], F32, name="to_centre")
+                nc.vector.scalar_tensor_tensor(
+                    out=to_centre[:], in0=group_mean[:], scalar=-1.0, in1=bias_centred[:].unsqueeze(2).to_broadcast([P, CHUNKS, ROUND]),
+                    op0=ALU.mult, op1=ALU.add,
+                )
                 squares = norm_pool.tile([P, stats, PROPOSALS], F32, name="squares")
-                nc.scalar.activation(out=squares[:], in_=lines, func=ACT.Square)
                 row_squares = norm_pool.tile([P, stats], F32, name="row_squares")
-                nc.vector.tensor_reduce(out=row_squares[:], in_=squares[:], axis=AXIS.X, op=ALU.add)
-                group_var = stat_psum.tile([P, stats], F32, name="group_var", tag="stat")
+                for q in range(CHUNKS):
+                    for i in range(ROUND):
+                        s = ROUND * q + i
+                        nc.scalar.activation(
+                            out=squares[:, s, :], in_=products[q][:, i, :], func=ACT.Square, bias=to_centre[:, q, i : i + 1], scale=1.0,
+                            accum_out=row_squares[:, s : s + 1],
+                        )
+                group_var = small_psum.tile([P, stats], F32, name="group_var", tag="small")
                 nc.tensor.matmul(out=group_var[:], lhsT=group_average[:], rhs=row_squares[:], start=True, stop=True)
                 deviation = norm_pool.tile([P, stats], F32, name="deviation")
                 nc.scalar.activation(out=deviation[:], in_=group_var[:], func=ACT.Sqrt, bias=eps_col[:, 0:1], scale=1.0)
-                inverse = norm_pool.tile([P, stats], F32, name="inverse")
-                nc.vector.reciprocal(out=inverse[:], in_=deviation[:])
-                nc.vector.tensor_tensor(out=lines, in0=lines, in1=inverse[:].unsqueeze(2).to_broadcast([P, stats, PROPOSALS]), op=ALU.mult)
+                factor = norm_pool.tile([P, CHUNKS, ROUND], F32, name="factor")
+                nc.vector.reciprocal(out=factor[:].rearrange("p q b -> p (q b)"), in_=deviation[:])
+                nc.vector.tensor_tensor(out=factor[:], in0=factor[:], in1=gain_col.unsqueeze(2).to_broadcast([P, CHUNKS, ROUND]), op=ALU.mult)
+                offset = norm_pool.tile([P, CHUNKS, ROUND], F32, name="offset")
+                nc.vector.tensor_tensor(out=offset[:], in0=factor[:], in1=to_centre[:], op=ALU.mult)
+                nc.vector.tensor_tensor(out=offset[:], in0=offset[:], in1=shift_col.unsqueeze(2).to_broadcast([P, CHUNKS, ROUND]), op=ALU.add)
                 for q in range(CHUNKS):
-                    nc.scalar.activation(
-                        out=result[:, q, batches, :], in_=centred[:, q], func=ACT.Relu, bias=shift_col[:, q : q + 1], scale=gain_col[:, q : q + 1]
-                    )
+                    for i in range(ROUND):
+                        nc.scalar.activation(
+                            out=result[:, q, ROUND * r + i, :], in_=products[q][:, i, :], func=ACT.Relu,
+                            bias=offset[:, q, i : i + 1], scale=factor[:, q, i : i + 1],
+                        )
 
             FETCH_LAG = 1
             POOL_LAG = 3

@@ -34,7 +34,7 @@ ROW_WORDS = HALF // 2
 REGIONS = 3
 REGION_ROWS = 2 * ENTRIES
 BANK_TILES = 2
-VECTOR_BANKS = (0,)
+VECTOR_BANKS = (0, 1, 2)
 
 
 def tile_coarsepyramid_pb_kernel(
@@ -222,37 +222,61 @@ def tile_coarsepyramid_pb_kernel(
                 region = flat_out[(b % REGIONS) * REGION_ROWS * ROW_WORDS : (b % REGIONS + 1) * REGION_ROWS * ROW_WORDS].rearrange(
                     "(p a w) -> p a w", p=P, w=2 * ROW_WORDS
                 )
-                for k in range(1, LEVELS):
-                    width = level_size[k] if k > 1 else FRAMES - 1
-                    lower = level_start[k - 1]
-                    for half in range(2):
-                        both = slice(2 * half, 2 * half + 2)
-                        nc.vector.tensor_tensor(
-                            out=table[:, both, level_start[k] : level_start[k] + width],
-                            in0=table[:, both, lower : lower + width],
-                            in1=table[:, both, lower + 2 ** (k - 1) : lower + 2 ** (k - 1) + width],
-                            op=ALU.max,
-                        )
                 turned = turned_pool.tile([P, TABLE_TILES, CHANNELS], BF16, name="turned")
                 turned_words = turned[:].rearrange("p a c -> p (a c)").bitcast(F32).rearrange("p (a w) -> p a w", w=2 * ROW_WORDS)
                 banks = (TABLE_TILES + BANK_TILES - 1) // BANK_TILES
-                for bank in range(banks):
+                landings = {}
+
+                def turn(bank):
                     tiles = range(BANK_TILES * bank, min(BANK_TILES * (bank + 1), TABLE_TILES))
                     landing = table_psum.tile([P, BANK_TILES, CHUNKS, P], BF16, name="landing")
                     for a in tiles:
                         for q in range(CHUNKS):
                             nc.tensor.transpose(landing[:, a - tiles[0], q, :], table[:, q, P * a : P * (a + 1)], identity[:])
-                    count = len(tiles)
-                    target = turned[:, tiles[0] : tiles[0] + count, :].rearrange("p a c -> p (a c)")
-                    source = landing[:, 0:count].rearrange("p a q m -> p (a q m)")
-                    if bank in VECTOR_BANKS:
-                        for a in range(count):
-                            nc.vector.tensor_copy(out=turned[:, tiles[0] + a, :], in_=landing[:, a].rearrange("p q m -> p (q m)"))
-                    else:
-                        nc.scalar.copy(out=target, in_=source)
-                    if bank % 2 == 1:
-                        whole_tiles = slice(BANK_TILES * (bank - 1), min(tiles[0] + count, used_entries // P))
+                    landings[bank] = landing
+                    if bank not in VECTOR_BANKS:
+                        count = len(tiles)
+                        nc.scalar.copy(
+                            out=turned[:, tiles[0] : tiles[0] + count, :].rearrange("p a c -> p (a c)"),
+                            in_=landing[:, 0:count].rearrange("p a q m -> p (a q m)"),
+                        )
+                        write(bank)
+
+                emptied_banks = set()
+
+                def write(bank):
+                    emptied_banks.add(bank)
+                    pair = bank - bank % 2
+                    if pair in emptied_banks and pair + 1 in emptied_banks:
+                        whole_tiles = slice(BANK_TILES * pair, min(BANK_TILES * (pair + 2), used_entries // P))
                         nc.sync.dma_start(out=region[:, whole_tiles, :], in_=turned_words[:, whole_tiles, :])
+
+                turned_banks = 0
+                emptied_tiles = 0
+                for k in range(LEVELS):
+                    if k > 0:
+                        width = level_size[k] if k > 1 else FRAMES - 1
+                        lower = level_start[k - 1]
+                        for half in range(2):
+                            both = slice(2 * half, 2 * half + 2)
+                            nc.vector.tensor_tensor(
+                                out=table[:, both, level_start[k] : level_start[k] + width],
+                                in0=table[:, both, lower : lower + width],
+                                in1=table[:, both, lower + 2 ** (k - 1) : lower + 2 ** (k - 1) + width],
+                                op=ALU.max,
+                            )
+                        if emptied_tiles < BANK_TILES * len(VECTOR_BANKS):
+                            bank = emptied_tiles // BANK_TILES
+                            nc.vector.tensor_copy(
+                                out=turned[:, emptied_tiles, :], in_=landings[bank][:, emptied_tiles % BANK_TILES].rearrange("p q m -> p (q m)")
+                            )
+                            emptied_tiles += 1
+                            if emptied_tiles % BANK_TILES == 0:
+                                write(bank)
+                    built = level_start[k] + level_size[k] if k < LEVELS - 1 else ENTRIES
+                    while turned_banks < banks and min(BANK_TILES * P * (turned_banks + 1), ENTRIES) <= built:
+                        turn(turned_banks)
+                        turned_banks += 1
                 rest = used_entries % P
                 last = slice(used_entries // P, used_entries // P + 1)
                 nc.sync.dma_start(out=region[0:rest, last, :], in_=turned_words[0:rest, last, :])

@@ -34,7 +34,7 @@ ROW_WORDS = HALF // 2
 REGIONS = 3
 REGION_ROWS = 2 * ENTRIES
 BANK_TILES = 2
-VECTOR_BANKS = (0, 1, 2)
+VECTOR_BANKS = (0, 1)
 
 
 def tile_coarsepyramid_pb_kernel(
@@ -66,6 +66,8 @@ def tile_coarsepyramid_pb_kernel(
 
         identity = const.tile([P, P], BF16)
         make_identity(nc, identity[:])
+        identity_words = const.tile([P, P], F32)
+        make_identity(nc, identity_words[:])
 
         column_group = const.tile([P, P], I32)
         nc.gpsimd.iota(column_group[:], pattern=[[1, P // GROUP_CHANNELS], [0, GROUP_CHANNELS]], base=0, channel_multiplier=0)
@@ -184,9 +186,9 @@ def tile_coarsepyramid_pb_kernel(
 
         table_ring = []
         for s in range(REGIONS):
-            table = const.tile([P, CHUNKS, ENTRIES], BF16, name="table%d" % s)
-            nc.vector.memset(table[:, :, level_start[1] + FRAMES - 1 : level_start[2]], 0.0)
-            nc.vector.memset(table[:, :, level_start[LEVELS - 1] + level_size[LEVELS - 1] : ENTRIES], 0.0)
+            table = const.tile([P, 2, ENTRIES, 2], BF16, name="table%d" % s)
+            nc.vector.memset(table[:, :, level_start[1] + FRAMES - 1 : level_start[2], :], 0.0)
+            nc.vector.memset(table[:, :, used_entries:ENTRIES, :], 0.0)
             table_ring.append(table)
 
         zero_rows = const.tile([P, 2 * ROW_WORDS], F32)
@@ -197,25 +199,29 @@ def tile_coarsepyramid_pb_kernel(
 
         best_ring = []
         for s in range(3):
-            best = const.tile([P, 2, HALF + P], BF16, name="best%d" % s)
+            best = const.tile([P, 2, 2 * HALF], BF16, name="best%d" % s)
             nc.vector.memset(best[:], 0.0)
             best_ring.append(best)
 
         result = const.tile([P, CHUNKS, BATCH, PROPOSALS], F32)
 
-        with tc.tile_pool(name="turned", bufs=3) as turned_pool, tc.tile_pool(name="fetch", bufs=4) as fetch_pool, tc.tile_pool(
+        with tc.tile_pool(name="raw", bufs=3) as raw_pool, tc.tile_pool(name="turned", bufs=3) as turned_pool, tc.tile_pool(name="fetch", bufs=4) as fetch_pool, tc.tile_pool(
             name="operands", bufs=2
         ) as operand_pool, tc.tile_pool(name="norm", bufs=2) as norm_pool, tc.psum_pool(name="table_psum", bufs=3) as table_psum, tc.psum_pool(
             name="small_psum", bufs=1
         ) as small_psum, tc.psum_pool(name="product_psum", bufs=CHUNKS) as product_psum:
 
             def load(b):
-                table = table_ring[b % REGIONS]
+                raw = raw_pool.tile([P, 2, 2, FRAMES], BF16, name="raw")
                 for half in range(2):
                     nc.sync.dma_start(
-                        out=table[:, 2 * half : 2 * half + 2, 0:FRAMES],
+                        out=raw[:, half],
                         in_=frame_level_feature[b, HALF * half : HALF * (half + 1), :].rearrange("(m j) t -> m j t", j=2),
                     )
+                raw_of[b] = raw
+
+            def weave(b):
+                nc.vector.tensor_copy(out=table_ring[b % REGIONS][:, :, 0:FRAMES, :], in_=raw_of[b][:].rearrange("p h j t -> p h t j"))
 
             def build(b):
                 table = table_ring[b % REGIONS]
@@ -229,16 +235,20 @@ def tile_coarsepyramid_pb_kernel(
 
                 def turn(bank):
                     tiles = range(BANK_TILES * bank, min(BANK_TILES * (bank + 1), TABLE_TILES))
-                    landing = table_psum.tile([P, BANK_TILES, CHUNKS, P], BF16, name="landing")
+                    landing = table_psum.tile([P, BANK_TILES, 2, P], F32, name="landing")
                     for a in tiles:
-                        for q in range(CHUNKS):
-                            nc.tensor.transpose(landing[:, a - tiles[0], q, :], table[:, q, P * a : P * (a + 1)], identity[:])
+                        for half in range(2):
+                            nc.tensor.transpose(
+                                landing[:, a - tiles[0], half, :],
+                                table[:, half, P * a : P * (a + 1), :].rearrange("p e j -> p (e j)").bitcast(F32),
+                                identity_words[:],
+                            )
                     landings[bank] = landing
                     if bank not in VECTOR_BANKS:
                         count = len(tiles)
                         nc.scalar.copy(
                             out=turned[:, tiles[0] : tiles[0] + count, :].rearrange("p a c -> p (a c)"),
-                            in_=landing[:, 0:count].rearrange("p a q m -> p (a q m)"),
+                            in_=landing[:, 0:count].rearrange("p a h m -> p (a h m)").bitcast(BF16),
                         )
                         write(bank)
 
@@ -258,17 +268,16 @@ def tile_coarsepyramid_pb_kernel(
                         width = level_size[k] if k > 1 else FRAMES - 1
                         lower = level_start[k - 1]
                         for half in range(2):
-                            both = slice(2 * half, 2 * half + 2)
                             nc.vector.tensor_tensor(
-                                out=table[:, both, level_start[k] : level_start[k] + width],
-                                in0=table[:, both, lower : lower + width],
-                                in1=table[:, both, lower + 2 ** (k - 1) : lower + 2 ** (k - 1) + width],
+                                out=table[:, half, level_start[k] : level_start[k] + width, :],
+                                in0=table[:, half, lower : lower + width, :],
+                                in1=table[:, half, lower + 2 ** (k - 1) : lower + 2 ** (k - 1) + width, :],
                                 op=ALU.max,
                             )
                         if emptied_tiles < BANK_TILES * len(VECTOR_BANKS):
                             bank = emptied_tiles // BANK_TILES
                             nc.vector.tensor_copy(
-                                out=turned[:, emptied_tiles, :], in_=landings[bank][:, emptied_tiles % BANK_TILES].rearrange("p q m -> p (q m)")
+                                out=turned[:, emptied_tiles, :], in_=landings[bank][:, emptied_tiles % BANK_TILES].rearrange("p h m -> p (h m)").bitcast(BF16)
                             )
                             emptied_tiles += 1
                             if emptied_tiles % BANK_TILES == 0:
@@ -297,15 +306,14 @@ def tile_coarsepyramid_pb_kernel(
                 for half in range(2):
                     lanes = slice(64 * half, 64 * half + 64)
                     nc.vector.tensor_tensor(
-                        out=best[lanes, :, P * half : P * half + HALF], in0=values[lanes, :, 0, :], in1=values[lanes, :, 1, :], op=ALU.max
+                        out=best[lanes, :, HALF * half : HALF * (half + 1)], in0=values[lanes, :, 0, :], in1=values[lanes, :, 1, :], op=ALU.max
                     )
                 back = small_psum.tile([P, 2, PACK, P], BF16, name="back", tag="small")
                 for i in range(2):
                     for t in range(PACK):
-                        slot = P * (t % 2) + t // 2
                         nc.tensor.transpose(
                             back[:, i, t, :],
-                            best[:, i, slot : slot + 2 * P - 1 : 2],
+                            best[:, i, t : t + PACK * (P - 1) + 1 : PACK],
                             keep[:, b + i, :],
                         )
                 for half in range(2):
@@ -376,10 +384,13 @@ def tile_coarsepyramid_pb_kernel(
             POOL_LAG = 3
             fetched_of = {}
             pooled_of = {}
+            raw_of = {}
             load(0)
+            load(1)
+            weave(0)
             for i in range(BATCH + POOL_LAG):
-                if i + 1 < BATCH:
-                    load(i + 1)
+                if i + 2 < BATCH:
+                    load(i + 2)
                 b = i - FETCH_LAG
                 if 0 <= b < BATCH:
                     if b % 2 == 0:
@@ -387,6 +398,8 @@ def tile_coarsepyramid_pb_kernel(
                     fetch(b, fetched_of[b // 2])
                 if i < BATCH:
                     build(i)
+                if i + 1 < BATCH:
+                    weave(i + 1)
                 b = i - POOL_LAG
                 if b >= 0 and b % 2 == 1:
                     if (b - 1) % ROUND == 0:

@@ -31,10 +31,12 @@ LEVELS = 8
 TABLE_TILES = 15
 ENTRIES = TABLE_TILES * P
 ROW_WORDS = HALF // 2
-REGIONS = 3
-REGION_ROWS = 2 * ENTRIES
-BANK_TILES = 2
-VECTOR_BANKS = (0, 1)
+RING = 3
+REGIONS = 6
+REGION_ROWS = ENTRIES
+BANK_TILES = 4
+EARLY_BANKS = 2
+VECTOR_BANKS = (0,)
 
 
 def tile_coarsepyramid_pb_kernel(
@@ -113,57 +115,47 @@ def tile_coarsepyramid_pb_kernel(
         nc.vector.memset(eps_col[:], EPS)
 
         row_index = const.tile([P, BATCH, 2], I32)
-        keep = const.tile([P, BATCH, P], BF16)
         with tc.tile_pool(name="setup", bufs=1) as setup:
             segments = setup.tile([P, BATCH, 4], BF16)
-            for half in range(2):
-                nc.sync.dma_start(out=segments[64 * half : 64 * half + 64], in_=frame_segments.rearrange("b n s -> n b s"))
-            ends = setup.tile([P, 2, BATCH], F32)
-            for half in range(2):
-                lanes = slice(64 * half, 64 * half + 64)
-                for e in range(2):
-                    nc.vector.tensor_scalar(
-                        out=ends[lanes, e, :], in0=segments[lanes, :, 2 * half + e], scalar1=0.0, scalar2=FRAMES - 1.0, op0=ALU.max, op1=ALU.min
-                    )
-            as_int = setup.tile([P, 2, BATCH], I32)
-            nc.vector.tensor_copy(out=as_int[:], in_=ends[:])
-            near = setup.tile([P, 2, BATCH], F32)
-            nc.vector.tensor_copy(out=near[:], in_=as_int[:])
-            above = setup.tile([P, 2, BATCH], F32)
-            nc.vector.tensor_tensor(out=above[:], in0=near[:], in1=ends[:], op=ALU.is_gt)
-            whole = setup.tile([P, 2, BATCH], F32)
-            nc.vector.tensor_tensor(out=whole[:], in0=near[:], in1=above[:], op=ALU.subtract)
-            first = whole[:, 0, :]
-            span = setup.tile([P, BATCH], F32)
-            nc.vector.tensor_tensor(out=span[:], in0=whole[:, 1, :], in1=first, op=ALU.subtract)
-            filled = setup.tile([P, BATCH], F32)
-            nc.vector.tensor_scalar(out=filled[:], in0=span[:], scalar1=0.0, scalar2=None, op0=ALU.is_ge)
-            nc.vector.tensor_tensor(
-                out=keep[:],
-                in0=identity[:].unsqueeze(1).to_broadcast([P, BATCH, P]),
-                in1=filled[:].unsqueeze(2).to_broadcast([P, BATCH, P]),
-                op=ALU.mult,
+            for s in range(2):
+                nc.sync.dma_start(out=segments[64 * s : 64 * s + 64], in_=frame_segments.rearrange("b n s -> n b s"))
+            ends = setup.tile([P, 2, BATCH, 2], F32)
+            nc.vector.tensor_scalar(
+                out=ends[:], in0=segments[:].rearrange("p b (h e) -> p e b h", e=2), scalar1=0.0, scalar2=FRAMES - 1.0, op0=ALU.max, op1=ALU.min
             )
+            as_int = setup.tile([P, 2, BATCH, 2], I32)
+            nc.vector.tensor_copy(out=as_int[:], in_=ends[:])
+            near = setup.tile([P, 2, BATCH, 2], F32)
+            nc.vector.tensor_copy(out=near[:], in_=as_int[:])
+            above = setup.tile([P, 2, BATCH, 2], F32)
+            nc.vector.tensor_tensor(out=above[:], in0=near[:], in1=ends[:], op=ALU.is_gt)
+            whole = setup.tile([P, 2, BATCH, 2], F32)
+            nc.vector.tensor_tensor(out=whole[:], in0=near[:], in1=above[:], op=ALU.subtract)
+            first = whole[:, 0]
+            span = setup.tile([P, BATCH, 2], F32)
+            nc.vector.tensor_tensor(out=span[:], in0=whole[:, 1], in1=first, op=ALU.subtract)
+            filled = setup.tile([P, BATCH, 2], F32)
+            nc.vector.tensor_scalar(out=filled[:], in0=span[:], scalar1=0.0, scalar2=None, op0=ALU.is_ge)
             nc.vector.tensor_scalar(out=span[:], in0=span[:], scalar1=0.0, scalar2=None, op0=ALU.max)
-            start = setup.tile([P, BATCH], F32)
+            start = setup.tile([P, BATCH, 2], F32)
             nc.vector.memset(start[:], 0.0)
-            back = setup.tile([P, BATCH], F32)
-            nc.vector.memset(back[:], 0.0)
-            step = setup.tile([P, 2, BATCH], F32)
+            reach = setup.tile([P, BATCH, 2], F32)
+            nc.vector.memset(reach[:], 0.0)
+            step = setup.tile([P, 2, BATCH, 2], F32)
             for k in range(1, LEVELS):
                 nc.vector.tensor_scalar(
-                    out=step[:, 0, :], in0=span[:], scalar1=2.0 ** k - 1.0, scalar2=float(level_start[k] - level_start[k - 1]),
+                    out=step[:, 0], in0=span[:], scalar1=2.0 ** k - 1.0, scalar2=float(level_start[k] - level_start[k - 1]),
                     op0=ALU.is_ge, op1=ALU.mult,
                 )
                 nc.vector.tensor_scalar(
-                    out=step[:, 1, :], in0=span[:], scalar1=2.0 ** k - 1.0, scalar2=2.0 ** (k - 1), op0=ALU.is_ge, op1=ALU.mult
+                    out=step[:, 1], in0=span[:], scalar1=2.0 ** k - 1.0, scalar2=2.0 ** (k - 1), op0=ALU.is_ge, op1=ALU.mult
                 )
-                nc.vector.tensor_tensor(out=start[:], in0=start[:], in1=step[:, 0, :], op=ALU.add)
-                nc.vector.tensor_tensor(out=back[:], in0=back[:], in1=step[:, 1, :], op=ALU.add)
+                nc.vector.tensor_tensor(out=start[:], in0=start[:], in1=step[:, 0], op=ALU.add)
+                nc.vector.tensor_tensor(out=reach[:], in0=reach[:], in1=step[:, 1], op=ALU.add)
             entry = setup.tile([P, BATCH, 2], F32)
-            nc.vector.tensor_tensor(out=entry[:, :, 0], in0=start[:], in1=first, op=ALU.add)
-            nc.vector.tensor_tensor(out=span[:], in0=span[:], in1=back[:], op=ALU.subtract)
-            nc.vector.tensor_tensor(out=entry[:, :, 1], in0=entry[:, :, 0], in1=span[:], op=ALU.add)
+            nc.vector.tensor_tensor(out=entry[:], in0=start[:], in1=first, op=ALU.add)
+            nc.vector.tensor_tensor(out=span[:], in0=span[:], in1=reach[:], op=ALU.subtract)
+            nc.vector.scalar_tensor_tensor(out=entry[:], in0=span[:], scalar=side[:, 0:1], in1=entry[:], op0=ALU.mult, op1=ALU.add)
             entry_int = setup.tile([P, BATCH, 2], I32)
             nc.vector.tensor_copy(out=entry_int[:], in_=entry[:])
             tile_int = setup.tile([P, BATCH, 2], I32)
@@ -171,37 +163,42 @@ def tile_coarsepyramid_pb_kernel(
             tile_f = setup.tile([P, BATCH, 2], F32)
             nc.vector.tensor_copy(out=tile_f[:], in_=tile_int[:])
             row_f = setup.tile([P, BATCH, 2], F32)
-            nc.vector.tensor_scalar(
-                out=row_f[:], in0=entry[:], scalar1=2.0 * TABLE_TILES, scalar2=side[:, 0:1], op0=ALU.mult, op1=ALU.add
-            )
+            nc.vector.tensor_scalar(out=row_f[:], in0=entry[:], scalar1=float(TABLE_TILES), scalar2=None, op0=ALU.mult)
             nc.vector.scalar_tensor_tensor(
-                out=row_f[:], in0=tile_f[:], scalar=2.0 - 2.0 * TABLE_TILES * P, in1=row_f[:], op0=ALU.mult, op1=ALU.add
+                out=row_f[:], in0=tile_f[:], scalar=1.0 - float(TABLE_TILES * P), in1=row_f[:], op0=ALU.mult, op1=ALU.add
             )
-            region_int = setup.tile([P, BATCH], I32)
-            nc.gpsimd.iota(region_int[:], pattern=[[0, BATCH // REGIONS], [REGION_ROWS, REGIONS]], base=0, channel_multiplier=0)
-            region_f = setup.tile([P, BATCH], F32)
+            spare_rows = P - used_entries % P
+            spare = setup.tile([P, 1], F32)
+            nc.vector.tensor_scalar(out=spare[:], in0=partition_f[:], scalar1=float(spare_rows), scalar2=-float(spare_rows), op0=ALU.is_ge, op1=ALU.mult)
+            nc.vector.tensor_tensor(out=spare[:], in0=spare[:], in1=partition_f[:], op=ALU.add)
+            nc.vector.tensor_scalar(
+                out=spare[:], in0=spare[:], scalar1=float(TABLE_TILES), scalar2=float(TABLE_TILES * (used_entries % P) + TABLE_TILES - 1),
+                op0=ALU.mult, op1=ALU.add,
+            )
+            nc.vector.tensor_scalar(out=row_f[:], in0=row_f[:], scalar1=spare[:, 0:1], scalar2=None, op0=ALU.subtract)
+            nc.vector.tensor_tensor(out=row_f[:], in0=row_f[:], in1=filled[:], op=ALU.mult)
+            nc.vector.tensor_scalar(out=row_f[:], in0=row_f[:], scalar1=spare[:, 0:1], scalar2=None, op0=ALU.add)
+            region_int = setup.tile([P, BATCH, 2], I32)
+            nc.gpsimd.iota(
+                region_int[:].rearrange("p b h -> p (b h)"), pattern=[[0, 2 * BATCH // REGIONS], [REGION_ROWS, REGIONS]], base=0, channel_multiplier=0
+            )
+            region_f = setup.tile([P, BATCH, 2], F32)
             nc.vector.tensor_copy(out=region_f[:], in_=region_int[:])
-            nc.vector.tensor_tensor(out=row_f[:], in0=row_f[:], in1=region_f[:].unsqueeze(2).to_broadcast([P, BATCH, 2]), op=ALU.add)
+            nc.vector.tensor_tensor(out=row_f[:], in0=row_f[:], in1=region_f[:], op=ALU.add)
             nc.vector.tensor_copy(out=row_index[:], in_=row_f[:])
 
         table_ring = []
-        for s in range(REGIONS):
+        for s in range(RING):
             table = const.tile([P, 2, ENTRIES, 2], BF16, name="table%d" % s)
             nc.vector.memset(table[:, :, level_start[1] + FRAMES - 1 : level_start[2], :], 0.0)
             nc.vector.memset(table[:, :, used_entries:ENTRIES, :], 0.0)
             table_ring.append(table)
 
-        zero_rows = const.tile([P, 2 * ROW_WORDS], F32)
+        zero_rows = const.tile([P, ROW_WORDS], F32)
         nc.vector.memset(zero_rows[:], 0.0)
         for s in range(REGIONS):
-            unused = flat_out[s * REGION_ROWS * ROW_WORDS : (s + 1) * REGION_ROWS * ROW_WORDS].rearrange("(p a w) -> p a w", p=P, w=2 * ROW_WORDS)
+            unused = flat_out[s * REGION_ROWS * ROW_WORDS : (s + 1) * REGION_ROWS * ROW_WORDS].rearrange("(p a w) -> p a w", p=P, w=ROW_WORDS)
             nc.sync.dma_start(out=unused[used_entries % P : P, TABLE_TILES - 1, :], in_=zero_rows[used_entries % P : P, :])
-
-        best_ring = []
-        for s in range(3):
-            best = const.tile([P, 2, 2 * HALF], BF16, name="best%d" % s)
-            nc.vector.memset(best[:], 0.0)
-            best_ring.append(best)
 
         result = const.tile([P, CHUNKS, BATCH, PROPOSALS], F32)
 
@@ -221,48 +218,51 @@ def tile_coarsepyramid_pb_kernel(
                 raw_of[b] = raw
 
             def weave(b):
-                nc.vector.tensor_copy(out=table_ring[b % REGIONS][:, :, 0:FRAMES, :], in_=raw_of[b][:].rearrange("p h j t -> p h t j"))
+                nc.vector.tensor_copy(out=table_ring[b % RING][:, :, 0:FRAMES, :], in_=raw_of[b][:].rearrange("p h j t -> p h t j"))
 
             def build(b):
-                table = table_ring[b % REGIONS]
-                region = flat_out[(b % REGIONS) * REGION_ROWS * ROW_WORDS : (b % REGIONS + 1) * REGION_ROWS * ROW_WORDS].rearrange(
-                    "(p a w) -> p a w", p=P, w=2 * ROW_WORDS
-                )
-                turned = turned_pool.tile([P, TABLE_TILES, CHANNELS], BF16, name="turned")
-                turned_words = turned[:].rearrange("p a c -> p (a c)").bitcast(F32).rearrange("p (a w) -> p a w", w=2 * ROW_WORDS)
-                banks = (TABLE_TILES + BANK_TILES - 1) // BANK_TILES
-                landings = {}
+                table = table_ring[b % RING]
+                turned = [turned_pool.tile([P, TABLE_TILES, HALF], BF16, name="turned%d" % half) for half in range(2)]
 
-                def turn(bank):
-                    tiles = range(BANK_TILES * bank, min(BANK_TILES * (bank + 1), TABLE_TILES))
-                    landing = table_psum.tile([P, BANK_TILES, 2, P], F32, name="landing")
-                    for a in tiles:
-                        for half in range(2):
-                            nc.tensor.transpose(
-                                landing[:, a - tiles[0], half, :],
-                                table[:, half, P * a : P * (a + 1), :].rearrange("p e j -> p (e j)").bitcast(F32),
-                                identity_words[:],
-                            )
-                    landings[bank] = landing
-                    if bank not in VECTOR_BANKS:
-                        count = len(tiles)
-                        nc.scalar.copy(
-                            out=turned[:, tiles[0] : tiles[0] + count, :].rearrange("p a c -> p (a c)"),
-                            in_=landing[:, 0:count].rearrange("p a h m -> p (a h m)").bitcast(BF16),
-                        )
-                        write(bank)
+                def write(half, partitions, tiles):
+                    place = (2 * b + half) % REGIONS
+                    region = flat_out[place * REGION_ROWS * ROW_WORDS : (place + 1) * REGION_ROWS * ROW_WORDS].rearrange(
+                        "(p a w) -> p a w", p=P, w=ROW_WORDS
+                    )
+                    words = turned[half][:].rearrange("p a c -> p (a c)").bitcast(F32).rearrange("p (a w) -> p a w", w=ROW_WORDS)
+                    nc.sync.dma_start(out=region[partitions, tiles, :], in_=words[partitions, tiles, :])
 
                 emptied_banks = set()
 
-                def write(bank):
-                    emptied_banks.add(bank)
-                    pair = bank - bank % 2
-                    if pair in emptied_banks and pair + 1 in emptied_banks:
-                        whole_tiles = slice(BANK_TILES * pair, min(BANK_TILES * (pair + 2), used_entries // P))
-                        nc.sync.dma_start(out=region[:, whole_tiles, :], in_=turned_words[:, whole_tiles, :])
+                def emptied(half, bank):
+                    emptied_banks.add((half, bank))
+                    if bank < EARLY_BANKS and all((half, other) in emptied_banks for other in range(EARLY_BANKS)):
+                        write(half, slice(0, P), slice(0, BANK_TILES * EARLY_BANKS))
+                    if bank == (TABLE_TILES - 1) // BANK_TILES:
+                        write(half, slice(0, P), slice(BANK_TILES * EARLY_BANKS, used_entries // P))
+                        write(half, slice(0, used_entries % P), slice(used_entries // P, used_entries // P + 1))
 
-                turned_banks = 0
-                emptied_tiles = 0
+                landings = {}
+
+                def turn(half, a):
+                    bank = a // BANK_TILES
+                    if a % BANK_TILES == 0:
+                        landings[(half, bank)] = table_psum.tile([P, BANK_TILES, P], F32, name="landing")
+                    landing = landings[(half, bank)]
+                    nc.tensor.transpose(
+                        landing[:, a % BANK_TILES, :],
+                        table[:, half, P * a : P * (a + 1), :].rearrange("p e j -> p (e j)").bitcast(F32),
+                        identity_words[:],
+                    )
+                    if (a % BANK_TILES == BANK_TILES - 1 or a == TABLE_TILES - 1) and bank not in VECTOR_BANKS:
+                        nc.scalar.copy(
+                            out=turned[half][:, BANK_TILES * bank : a + 1, :].rearrange("p a c -> p (a c)"),
+                            in_=landing[:, 0 : a % BANK_TILES + 1, :].rearrange("p a m -> p (a m)").bitcast(BF16),
+                        )
+                        emptied(half, bank)
+
+                pieces = [(half, bank, piece) for bank in VECTOR_BANKS for piece in range(2) for half in range(2)]
+                turned_tiles = 0
                 for k in range(LEVELS):
                     if k > 0:
                         width = level_size[k] if k > 1 else FRAMES - 1
@@ -274,54 +274,46 @@ def tile_coarsepyramid_pb_kernel(
                                 in1=table[:, half, lower + 2 ** (k - 1) : lower + 2 ** (k - 1) + width, :],
                                 op=ALU.max,
                             )
-                        if emptied_tiles < BANK_TILES * len(VECTOR_BANKS):
-                            bank = emptied_tiles // BANK_TILES
+                        if pieces:
+                            half, bank, piece = pieces[0]
+                            pieces = pieces[1:]
+                            two = slice(2 * piece, 2 * piece + 2)
                             nc.vector.tensor_copy(
-                                out=turned[:, emptied_tiles, :], in_=landings[bank][:, emptied_tiles % BANK_TILES].rearrange("p h m -> p (h m)").bitcast(BF16)
+                                out=turned[half][:, BANK_TILES * bank + 2 * piece : BANK_TILES * bank + 2 * piece + 2, :].rearrange("p a c -> p (a c)"),
+                                in_=landings[(half, bank)][:, two, :].rearrange("p a m -> p (a m)").bitcast(BF16),
                             )
-                            emptied_tiles += 1
-                            if emptied_tiles % BANK_TILES == 0:
-                                write(bank)
+                            if piece == 1:
+                                emptied(half, bank)
                     built = level_start[k] + level_size[k] if k < LEVELS - 1 else ENTRIES
-                    while turned_banks < banks and min(BANK_TILES * P * (turned_banks + 1), ENTRIES) <= built:
-                        turn(turned_banks)
-                        turned_banks += 1
-                rest = used_entries % P
-                last = slice(used_entries // P, used_entries // P + 1)
-                nc.sync.dma_start(out=region[0:rest, last, :], in_=turned_words[0:rest, last, :])
+                    while turned_tiles < TABLE_TILES and P * (turned_tiles + 1) <= built:
+                        for half in range(2):
+                            turn(half, turned_tiles)
+                        turned_tiles += 1
 
             def fetch(b, fetched):
-                region_rows = out_rows[0 : (b % REGIONS + 1) * REGION_ROWS, :]
-                for s in range(2):
+                for half in range(2):
                     nc.gpsimd.indirect_dma_start(
-                        out=fetched[:, b % 2, s, :],
+                        out=fetched[:, b % 2, ROW_WORDS * half : ROW_WORDS * (half + 1)],
                         out_offset=None,
-                        in_=region_rows,
-                        in_offset=bass.IndirectOffsetOnAxis(ap=row_index[:, b, s : s + 1], axis=0),
+                        in_=out_rows[0 : ((2 * b + half) % REGIONS + 1) * REGION_ROWS, :],
+                        in_offset=bass.IndirectOffsetOnAxis(ap=row_index[:, b, half : half + 1], axis=0),
                     )
 
             def pool_pair(b, fetched, pooled):
-                values = fetched[:].rearrange("p b s w -> p (b s w)").bitcast(BF16).rearrange("p (b s c) -> p b s c", b=2, s=2)
-                best = best_ring[(b // 2) % len(best_ring)]
-                for half in range(2):
-                    lanes = slice(64 * half, 64 * half + 64)
-                    nc.vector.tensor_tensor(
-                        out=best[lanes, :, HALF * half : HALF * (half + 1)], in0=values[lanes, :, 0, :], in1=values[lanes, :, 1, :], op=ALU.max
-                    )
+                values = fetch_pool.tile([P, 2, CHANNELS], BF16, name="values")
+                nc.vector.tensor_copy(out=values[:].rearrange("p i c -> p (i c)"), in_=fetched[:].rearrange("p i w -> p (i w)").bitcast(BF16))
                 back = small_psum.tile([P, 2, PACK, P], BF16, name="back", tag="small")
                 for i in range(2):
                     for t in range(PACK):
-                        nc.tensor.transpose(
-                            back[:, i, t, :],
-                            best[:, i, t : t + PACK * (P - 1) + 1 : PACK],
-                            keep[:, b + i, :],
-                        )
-                for half in range(2):
-                    lanes = slice(64 * half, 64 * half + 64)
-                    nc.scalar.copy(
-                        out=pooled[lanes, b % ROUND : b % ROUND + 2, :, :],
-                        in_=back[lanes, :, :, 64 * half : 64 * half + 64].rearrange("p b t n -> p b n t"),
-                    )
+                        nc.tensor.transpose(back[:, i, t, :], values[:, i, t : t + PACK * (P - 1) + 1 : PACK], identity[:])
+                second = fetch_pool.tile([P, 2, PROPOSALS, PACK], BF16, name="second")
+                nc.scalar.copy(out=second[:], in_=back[:, :, :, PROPOSALS : 2 * PROPOSALS].rearrange("p i t n -> p i n t"))
+                nc.vector.tensor_tensor(
+                    out=pooled[:, b % ROUND : b % ROUND + 2, :, :],
+                    in0=back[:, :, :, 0:PROPOSALS].rearrange("p i t n -> p i n t"),
+                    in1=second[:],
+                    op=ALU.max,
+                )
 
             def finish_round(r, pooled):
                 batches = slice(ROUND * r, ROUND * (r + 1))
@@ -394,7 +386,7 @@ def tile_coarsepyramid_pb_kernel(
                 b = i - FETCH_LAG
                 if 0 <= b < BATCH:
                     if b % 2 == 0:
-                        fetched_of[b // 2] = fetch_pool.tile([P, 2, 2, ROW_WORDS], F32, name="fetched")
+                        fetched_of[b // 2] = fetch_pool.tile([P, 2, 2 * ROW_WORDS], F32, name="fetched")
                     fetch(b, fetched_of[b // 2])
                 if i < BATCH:
                     build(i)

@@ -23,9 +23,9 @@ FRAMES = 256
 PROPOSALS = 64
 GROUP_CHANNELS = 16
 GROUP_SIZE = GROUP_CHANNELS * PROPOSALS
+GROUP_PARTITIONS = 4
 EPS = 1e-5
 ROUND = 8
-ROUNDS = BATCH // ROUND
 CHUNKS = CHANNELS // P
 LEVELS = 8
 TABLE_TILES = 15
@@ -52,7 +52,21 @@ def tile_coarsepyramid_pb_kernel(
     out_rows = flat_out.rearrange("(r w) -> r w", w=ROW_WORDS)
     assert REGIONS * REGION_ROWS <= BATCH * CHANNELS * PROPOSALS // ROW_WORDS
 
-    with tc.tile_pool(name="const", bufs=1) as const:
+    with tc.tile_pool(name="const", bufs=1) as const, tc.tile_pool(name="raw", bufs=3) as raw_pool:
+        raw_of = {}
+
+        def load(b):
+            raw = raw_pool.tile([P, 2, 2, FRAMES], BF16, name="raw")
+            for half in range(2):
+                nc.sync.dma_start(
+                    out=raw[:, half],
+                    in_=frame_level_feature[b, HALF * half : HALF * (half + 1), :].rearrange("(m j) t -> m j t", j=2),
+                )
+            raw_of[b] = raw
+
+        load(0)
+        load(1)
+
         w_words = const.tile([P, CHANNELS], U32, align_bytes=64)
         nc.sync.dma_start(
             out=w_words[:].bitcast(I32),
@@ -66,17 +80,24 @@ def tile_coarsepyramid_pb_kernel(
                 in_=w_roi_scales[0, 4 * quadrant : 4 * quadrant + 4, :].bitcast(I32),
             )
 
+        w_sorted = const.tile([P, CHANNELS], U32, align_bytes=64)
+        nc.gpsimd.tensor_copy(
+            out=w_sorted[:].bitcast(I32).rearrange("p (q m) -> p q m", q=CHUNKS), in_=w_words[:].bitcast(I32).rearrange("p (m q) -> p q m", q=CHUNKS)
+        )
+        s_sorted = const.tile([P, CHANNELS], U8, align_bytes=64)
+        nc.vector.tensor_copy(out=s_sorted[:].rearrange("p (q m) -> p m q", q=CHUNKS), in_=w_scales[:].rearrange("p (m q) -> p m q", q=CHUNKS))
+
         identity = const.tile([P, P], BF16)
         make_identity(nc, identity[:])
         identity_words = const.tile([P, P], F32)
         make_identity(nc, identity_words[:])
 
         column_group = const.tile([P, P], I32)
-        nc.gpsimd.iota(column_group[:], pattern=[[1, P // GROUP_CHANNELS], [0, GROUP_CHANNELS]], base=0, channel_multiplier=0)
+        nc.gpsimd.iota(column_group[:], pattern=[[1, P // GROUP_PARTITIONS], [0, GROUP_PARTITIONS]], base=0, channel_multiplier=0)
         partition_index = const.tile([P, 1], I32)
         nc.gpsimd.iota(partition_index[:], pattern=[[0, 1]], base=0, channel_multiplier=1)
         partition_group = const.tile([P, 1], I32)
-        nc.vector.tensor_single_scalar(out=partition_group[:], in_=partition_index[:], scalar=4, op=ALU.arith_shift_right)
+        nc.vector.tensor_single_scalar(out=partition_group[:], in_=partition_index[:], scalar=2, op=ALU.arith_shift_right)
         column_group_f = const.tile([P, P], F32)
         nc.vector.tensor_copy(out=column_group_f[:], in_=column_group[:])
         partition_group_f = const.tile([P, 1], F32)
@@ -91,24 +112,20 @@ def tile_coarsepyramid_pb_kernel(
         side = const.tile([P, 1], F32)
         nc.vector.tensor_scalar(out=side[:], in0=partition_f[:], scalar1=float(PROPOSALS), scalar2=None, op0=ALU.is_ge)
 
-        rows = const.tile([P, P], BF16)
-        nc.vector.memset(rows[:], 0.0)
-        for i, vector in enumerate((b_roi, g_roi, be_roi)):
-            nc.sync.dma_start(
-                out=rows[CHUNKS * i : CHUNKS * (i + 1), :],
-                in_=vector.rearrange("(q p) -> q p", p=P),
-            )
         columns = const.tile([P, 3 * CHUNKS], F32)
+        for i, vector in enumerate((b_roi, g_roi, be_roi)):
+            four = const.tile([P, CHUNKS], BF16, name="four%d" % i)
+            nc.sync.dma_start(out=four[:], in_=vector.rearrange("(p q) -> p q", q=CHUNKS))
+            nc.vector.tensor_copy(out=columns[:, CHUNKS * i : CHUNKS * (i + 1)], in_=four[:])
         bias_centred = const.tile([P, CHUNKS], F32)
         with tc.psum_pool(name="setup_psum", bufs=1) as setup_psum:
-            rows_turned = setup_psum.tile([P, P], BF16)
-            nc.tensor.transpose(rows_turned[:], rows[:], identity[:])
-            nc.vector.tensor_copy(out=columns[:], in_=rows_turned[:, 0 : 3 * CHUNKS])
             bias_rows = const.tile([P, CHUNKS], F32)
             nc.vector.tensor_scalar(out=bias_rows[:], in0=columns[:, 0:CHUNKS], scalar1=float(PROPOSALS), scalar2=None, op0=ALU.mult)
-            bias_mean = setup_psum.tile([P, CHUNKS], F32)
-            nc.tensor.matmul(out=bias_mean[:], lhsT=group_average[:], rhs=bias_rows[:], start=True, stop=True)
-            nc.vector.tensor_tensor(out=bias_centred[:], in0=columns[:, 0:CHUNKS], in1=bias_mean[:], op=ALU.subtract)
+            bias_parts = setup_psum.tile([P, CHUNKS], F32)
+            nc.tensor.matmul(out=bias_parts[:], lhsT=group_average[:], rhs=bias_rows[:], start=True, stop=True)
+            bias_mean = const.tile([P, 1], F32)
+            nc.vector.tensor_reduce(out=bias_mean[:], in_=bias_parts[:], axis=AXIS.X, op=ALU.add)
+            nc.vector.tensor_scalar(out=bias_centred[:], in0=columns[:, 0:CHUNKS], scalar1=bias_mean[:, 0:1], scalar2=None, op0=ALU.subtract)
         gain_col = columns[:, CHUNKS : 2 * CHUNKS]
         shift_col = columns[:, 2 * CHUNKS : 3 * CHUNKS]
         eps_col = const.tile([P, 1], F32)
@@ -200,22 +217,13 @@ def tile_coarsepyramid_pb_kernel(
             unused = flat_out[s * REGION_ROWS * ROW_WORDS : (s + 1) * REGION_ROWS * ROW_WORDS].rearrange("(p a w) -> p a w", p=P, w=ROW_WORDS)
             nc.sync.dma_start(out=unused[used_entries % P : P, TABLE_TILES - 1, :], in_=zero_rows[used_entries % P : P, :])
 
-        result = const.tile([P, CHUNKS, BATCH, PROPOSALS], F32)
+        result = const.tile([P, BATCH, CHUNKS, PROPOSALS], F32)
 
-        with tc.tile_pool(name="raw", bufs=3) as raw_pool, tc.tile_pool(name="turned", bufs=3) as turned_pool, tc.tile_pool(name="fetch", bufs=4) as fetch_pool, tc.tile_pool(
+        with tc.tile_pool(name="turned", bufs=3) as turned_pool, tc.tile_pool(name="fetch", bufs=4) as fetch_pool, tc.tile_pool(
             name="operands", bufs=2
         ) as operand_pool, tc.tile_pool(name="norm", bufs=2) as norm_pool, tc.psum_pool(name="table_psum", bufs=3) as table_psum, tc.psum_pool(
             name="small_psum", bufs=1
         ) as small_psum, tc.psum_pool(name="product_psum", bufs=CHUNKS) as product_psum:
-
-            def load(b):
-                raw = raw_pool.tile([P, 2, 2, FRAMES], BF16, name="raw")
-                for half in range(2):
-                    nc.sync.dma_start(
-                        out=raw[:, half],
-                        in_=frame_level_feature[b, HALF * half : HALF * (half + 1), :].rearrange("(m j) t -> m j t", j=2),
-                    )
-                raw_of[b] = raw
 
             def weave(b):
                 nc.vector.tensor_copy(out=table_ring[b % RING][:, :, 0:FRAMES, :], in_=raw_of[b][:].rearrange("p h j t -> p h t j"))
@@ -299,7 +307,7 @@ def tile_coarsepyramid_pb_kernel(
                         in_offset=bass.IndirectOffsetOnAxis(ap=row_index[:, b, half : half + 1], axis=0),
                     )
 
-            def pool_pair(b, fetched, pooled):
+            def pool_pair(b, fetched, pooled, place):
                 values = fetch_pool.tile([P, 2, CHANNELS], BF16, name="values")
                 nc.vector.tensor_copy(out=values[:].rearrange("p i c -> p (i c)"), in_=fetched[:].rearrange("p i w -> p (i w)").bitcast(BF16))
                 back = small_psum.tile([P, 2, PACK, P], BF16, name="back", tag="small")
@@ -309,27 +317,26 @@ def tile_coarsepyramid_pb_kernel(
                 second = fetch_pool.tile([P, 2, PROPOSALS, PACK], BF16, name="second")
                 nc.scalar.copy(out=second[:], in_=back[:, :, :, PROPOSALS : 2 * PROPOSALS].rearrange("p i t n -> p i n t"))
                 nc.vector.tensor_tensor(
-                    out=pooled[:, b % ROUND : b % ROUND + 2, :, :],
+                    out=pooled[:, place : place + 2, :, :],
                     in0=back[:, :, :, 0:PROPOSALS].rearrange("p i t n -> p i n t"),
                     in1=second[:],
                     op=ALU.max,
                 )
 
-            def finish_round(r, pooled):
-                batches = slice(ROUND * r, ROUND * (r + 1))
-                codes = operand_pool.tile([P, ROUND * PROPOSALS], U32, align_bytes=64, name="codes")
-                scales = operand_pool.tile([P, ROUND * PROPOSALS], U8, align_bytes=64, name="scales")
+            def finish_round(first_batch, count, pooled):
+                codes = operand_pool.tile([P, count * PROPOSALS], U32, align_bytes=64, name="codes")
+                scales = operand_pool.tile([P, count * PROPOSALS], U8, align_bytes=64, name="scales")
                 nc.vector.quantize_mx(out=codes[:].bitcast(FP8X4), scales=scales[:], in_=pooled[:].rearrange("p b n j -> p (b n j)"))
-                stats = CHUNKS * ROUND
+                stats = CHUNKS * count
                 products = []
-                row_sum = norm_pool.tile([P, CHUNKS, ROUND], F32, name="row_sum")
+                row_sum = norm_pool.tile([P, CHUNKS, count], F32, name="row_sum")
                 for q in range(CHUNKS):
                     cols = slice(P * q, P * (q + 1))
-                    product = product_psum.tile([P, ROUND, PROPOSALS], F32, name="product")
+                    product = product_psum.tile([P, count, PROPOSALS], F32, name="product")
                     nc.tensor.matmul_mx(
                         out=product[:].rearrange("p b n -> p (b n)"),
-                        lhsT=w_words[:, cols].bitcast(FP8X4),
-                        lhsT_scale=w_scales[:, cols],
+                        lhsT=w_sorted[:, cols].bitcast(FP8X4),
+                        lhsT_scale=s_sorted[:, cols],
                         rhs=codes[:].bitcast(FP8X4),
                         rhs_scale=scales[:],
                         start=True,
@@ -337,48 +344,63 @@ def tile_coarsepyramid_pb_kernel(
                     )
                     nc.vector.tensor_reduce(out=row_sum[:, q, :], in_=product[:], axis=AXIS.X, op=ALU.add)
                     products.append(product)
-                group_mean = small_psum.tile([P, CHUNKS, ROUND], F32, name="group_mean", tag="small")
+                mean_parts = small_psum.tile([P, CHUNKS, count], F32, name="mean_parts", tag="small")
                 nc.tensor.matmul(
-                    out=group_mean[:].rearrange("p q b -> p (q b)"), lhsT=group_average[:], rhs=row_sum[:].rearrange("p q b -> p (q b)"), start=True, stop=True
+                    out=mean_parts[:].rearrange("p q b -> p (q b)"), lhsT=group_average[:], rhs=row_sum[:].rearrange("p q b -> p (q b)"), start=True, stop=True
                 )
-                to_centre = norm_pool.tile([P, CHUNKS, ROUND], F32, name="to_centre")
-                nc.vector.scalar_tensor_tensor(
-                    out=to_centre[:], in0=group_mean[:], scalar=-1.0, in1=bias_centred[:].unsqueeze(2).to_broadcast([P, CHUNKS, ROUND]),
-                    op0=ALU.mult, op1=ALU.add,
+                group_mean = norm_pool.tile([P, count], F32, name="group_mean")
+                nc.vector.tensor_reduce(out=group_mean[:], in_=mean_parts[:].rearrange("p q b -> p b q"), axis=AXIS.X, op=ALU.add)
+                to_centre = norm_pool.tile([P, CHUNKS, count], F32, name="to_centre")
+                nc.vector.tensor_tensor(
+                    out=to_centre[:],
+                    in0=bias_centred[:].unsqueeze(2).to_broadcast([P, CHUNKS, count]),
+                    in1=group_mean[:].unsqueeze(1).to_broadcast([P, CHUNKS, count]),
+                    op=ALU.subtract,
                 )
                 squares = norm_pool.tile([P, stats, PROPOSALS], F32, name="squares")
                 row_squares = norm_pool.tile([P, stats], F32, name="row_squares")
                 for q in range(CHUNKS):
-                    for i in range(ROUND):
-                        s = ROUND * q + i
+                    for i in range(count):
+                        s = count * q + i
                         nc.scalar.activation(
                             out=squares[:, s, :], in_=products[q][:, i, :], func=ACT.Square, bias=to_centre[:, q, i : i + 1], scale=1.0,
                             accum_out=row_squares[:, s : s + 1],
                         )
-                group_var = small_psum.tile([P, stats], F32, name="group_var", tag="small")
-                nc.tensor.matmul(out=group_var[:], lhsT=group_average[:], rhs=row_squares[:], start=True, stop=True)
-                deviation = norm_pool.tile([P, stats], F32, name="deviation")
+                var_parts = small_psum.tile([P, CHUNKS, count], F32, name="var_parts", tag="small")
+                nc.tensor.matmul(out=var_parts[:].rearrange("p q b -> p (q b)"), lhsT=group_average[:], rhs=row_squares[:], start=True, stop=True)
+                group_var = norm_pool.tile([P, count], F32, name="group_var")
+                nc.vector.tensor_reduce(out=group_var[:], in_=var_parts[:].rearrange("p q b -> p b q"), axis=AXIS.X, op=ALU.add)
+                deviation = norm_pool.tile([P, count], F32, name="deviation")
                 nc.scalar.activation(out=deviation[:], in_=group_var[:], func=ACT.Sqrt, bias=eps_col[:, 0:1], scale=1.0)
-                factor = norm_pool.tile([P, CHUNKS, ROUND], F32, name="factor")
-                nc.vector.reciprocal(out=factor[:].rearrange("p q b -> p (q b)"), in_=deviation[:])
-                nc.vector.tensor_tensor(out=factor[:], in0=factor[:], in1=gain_col.unsqueeze(2).to_broadcast([P, CHUNKS, ROUND]), op=ALU.mult)
-                offset = norm_pool.tile([P, CHUNKS, ROUND], F32, name="offset")
+                inverse = norm_pool.tile([P, count], F32, name="inverse")
+                nc.vector.reciprocal(out=inverse[:], in_=deviation[:])
+                factor = norm_pool.tile([P, CHUNKS, count], F32, name="factor")
+                nc.vector.tensor_tensor(
+                    out=factor[:],
+                    in0=gain_col.unsqueeze(2).to_broadcast([P, CHUNKS, count]),
+                    in1=inverse[:].unsqueeze(1).to_broadcast([P, CHUNKS, count]),
+                    op=ALU.mult,
+                )
+                offset = norm_pool.tile([P, CHUNKS, count], F32, name="offset")
                 nc.vector.tensor_tensor(out=offset[:], in0=factor[:], in1=to_centre[:], op=ALU.mult)
-                nc.vector.tensor_tensor(out=offset[:], in0=offset[:], in1=shift_col.unsqueeze(2).to_broadcast([P, CHUNKS, ROUND]), op=ALU.add)
+                nc.vector.tensor_tensor(out=offset[:], in0=offset[:], in1=shift_col.unsqueeze(2).to_broadcast([P, CHUNKS, count]), op=ALU.add)
                 for q in range(CHUNKS):
-                    for i in range(ROUND):
+                    for i in range(count):
                         nc.scalar.activation(
-                            out=result[:, q, ROUND * r + i, :], in_=products[q][:, i, :], func=ACT.Relu,
+                            out=result[:, first_batch + i, q, :], in_=products[q][:, i, :], func=ACT.Relu,
                             bias=offset[:, q, i : i + 1], scale=factor[:, q, i : i + 1],
                         )
 
+            rounds = [(first_batch, ROUND) for first_batch in range(0, BATCH - ROUND, ROUND)]
+            rounds.extend([(BATCH - 8, 4), (BATCH - 4, 2), (BATCH - 2, 2)])
+            round_of = {}
+            for first_batch, count in rounds:
+                for b in range(first_batch, first_batch + count):
+                    round_of[b] = (first_batch, count)
             FETCH_LAG = 1
             POOL_LAG = 3
             fetched_of = {}
             pooled_of = {}
-            raw_of = {}
-            load(0)
-            load(1)
             weave(0)
             for i in range(BATCH + POOL_LAG):
                 if i + 2 < BATCH:
@@ -394,13 +416,15 @@ def tile_coarsepyramid_pb_kernel(
                     weave(i + 1)
                 b = i - POOL_LAG
                 if b >= 0 and b % 2 == 1:
-                    if (b - 1) % ROUND == 0:
-                        pooled_of[b // ROUND] = operand_pool.tile([P, ROUND, PROPOSALS, PACK], BF16, align_bytes=64, name="pooled")
-                    pool_pair(b - 1, fetched_of[b // 2], pooled_of[b // ROUND])
-                    if b % ROUND == ROUND - 1:
-                        finish_round(b // ROUND, pooled_of[b // ROUND])
+                    first_batch, count = round_of[b]
+                    if b - 1 == first_batch:
+                        pooled_of[first_batch] = operand_pool.tile([P, count, PROPOSALS, PACK], BF16, align_bytes=64, name="pooled")
+                    pool_pair(b - 1, fetched_of[b // 2], pooled_of[first_batch], b - 1 - first_batch)
+                    if b == first_batch + count - 1:
+                        finish_round(first_batch, count, pooled_of[first_batch])
 
-            for r in range(ROUNDS):
-                batches = slice(ROUND * r, ROUND * (r + 1))
-                for q in range(CHUNKS):
-                    nc.sync.dma_start(out=out[batches, P * q : P * (q + 1), :].rearrange("b p n -> p b n"), in_=result[:, q, batches, :])
+            for first_batch, count in rounds:
+                batches = slice(first_batch, first_batch + count)
+                nc.sync.dma_start(
+                    out=out[batches].rearrange("b (p q) n -> p b (q n)", q=CHUNKS), in_=result[:, batches].rearrange("p b q n -> p b (q n)")
+                )

@@ -27,12 +27,13 @@ GROUP_PARTITIONS = 4
 EPS = 1e-5
 ROUND = 8
 CHUNKS = CHANNELS // P
-LEVELS = 8
-TABLE_TILES = 15
+RUNS = (1, 3, 7, 14, 28, 56, 112, 224)
+LEVELS = len(RUNS)
+TABLE_TILES = 13
 ENTRIES = TABLE_TILES * P
 ROW_WORDS = HALF // 2
 RING = 3
-REGIONS = 6
+REGIONS = 7
 REGION_ROWS = ENTRIES
 BANK_TILES = 4
 EARLY_BANKS = 2
@@ -43,7 +44,7 @@ def tile_coarsepyramid_pb_kernel(
     tc, frame_level_feature, frame_segments, w_roi_words, w_roi_scales, b_roi, g_roi, be_roi, out
 ):
     nc = tc.nc
-    level_size = [FRAMES] + [FRAMES + 2 - 2 ** k for k in range(1, LEVELS)]
+    level_size = [FRAMES + 1 - run for run in RUNS]
     level_start = [sum(level_size[0:k]) for k in range(LEVELS)]
     used_entries = level_start[LEVELS - 1] + level_size[LEVELS - 1]
     assert used_entries <= ENTRIES and used_entries // P == TABLE_TILES - 1
@@ -80,146 +81,149 @@ def tile_coarsepyramid_pb_kernel(
                 in_=w_roi_scales[0, 4 * quadrant : 4 * quadrant + 4, :].bitcast(I32),
             )
 
-        w_sorted = const.tile([P, CHANNELS], U32, align_bytes=64)
-        nc.gpsimd.tensor_copy(
-            out=w_sorted[:].bitcast(I32).rearrange("p (q m) -> p q m", q=CHUNKS), in_=w_words[:].bitcast(I32).rearrange("p (m q) -> p q m", q=CHUNKS)
-        )
-        s_sorted = const.tile([P, CHANNELS], U8, align_bytes=64)
-        nc.vector.tensor_copy(out=s_sorted[:].rearrange("p (q m) -> p m q", q=CHUNKS), in_=w_scales[:].rearrange("p (m q) -> p m q", q=CHUNKS))
+        fours = []
+        for i, vector in enumerate((b_roi, g_roi, be_roi)):
+            four = const.tile([P, CHUNKS], BF16, name="four%d" % i)
+            nc.sync.dma_start(out=four[:], in_=vector.rearrange("(p q) -> p q", q=CHUNKS))
+            fours.append(four)
+        segments = const.tile([P, BATCH, 4], BF16)
+        for s in range(2):
+            nc.sync.dma_start(out=segments[64 * s : 64 * s + 64], in_=frame_segments.rearrange("b n s -> n b s"))
 
         identity = const.tile([P, P], BF16)
         make_identity(nc, identity[:])
         identity_words = const.tile([P, P], F32)
         make_identity(nc, identity_words[:])
 
-        column_group = const.tile([P, P], I32)
-        nc.gpsimd.iota(column_group[:], pattern=[[1, P // GROUP_PARTITIONS], [0, GROUP_PARTITIONS]], base=0, channel_multiplier=0)
-        partition_index = const.tile([P, 1], I32)
-        nc.gpsimd.iota(partition_index[:], pattern=[[0, 1]], base=0, channel_multiplier=1)
-        partition_group = const.tile([P, 1], I32)
-        nc.vector.tensor_single_scalar(out=partition_group[:], in_=partition_index[:], scalar=2, op=ALU.arith_shift_right)
-        column_group_f = const.tile([P, P], F32)
-        nc.vector.tensor_copy(out=column_group_f[:], in_=column_group[:])
-        partition_group_f = const.tile([P, 1], F32)
-        nc.vector.tensor_copy(out=partition_group_f[:], in_=partition_group[:])
-        group_average = const.tile([P, P], F32)
-        nc.vector.tensor_scalar(
-            out=group_average[:], in0=column_group_f[:], scalar1=partition_group_f[:, 0:1], scalar2=1.0 / GROUP_SIZE,
-            op0=ALU.is_equal, op1=ALU.mult,
-        )
-        partition_f = const.tile([P, 1], F32)
-        nc.vector.tensor_copy(out=partition_f[:], in_=partition_index[:])
-        side = const.tile([P, 1], F32)
-        nc.vector.tensor_scalar(out=side[:], in0=partition_f[:], scalar1=float(PROPOSALS), scalar2=None, op0=ALU.is_ge)
-
-        columns = const.tile([P, 3 * CHUNKS], F32)
-        for i, vector in enumerate((b_roi, g_roi, be_roi)):
-            four = const.tile([P, CHUNKS], BF16, name="four%d" % i)
-            nc.sync.dma_start(out=four[:], in_=vector.rearrange("(p q) -> p q", q=CHUNKS))
-            nc.vector.tensor_copy(out=columns[:, CHUNKS * i : CHUNKS * (i + 1)], in_=four[:])
-        bias_centred = const.tile([P, CHUNKS], F32)
-        with tc.psum_pool(name="setup_psum", bufs=1) as setup_psum:
-            bias_rows = const.tile([P, CHUNKS], F32)
-            nc.vector.tensor_scalar(out=bias_rows[:], in0=columns[:, 0:CHUNKS], scalar1=float(PROPOSALS), scalar2=None, op0=ALU.mult)
-            bias_parts = setup_psum.tile([P, CHUNKS], F32)
-            nc.tensor.matmul(out=bias_parts[:], lhsT=group_average[:], rhs=bias_rows[:], start=True, stop=True)
-            bias_mean = const.tile([P, 1], F32)
-            nc.vector.tensor_reduce(out=bias_mean[:], in_=bias_parts[:], axis=AXIS.X, op=ALU.add)
-            nc.vector.tensor_scalar(out=bias_centred[:], in0=columns[:, 0:CHUNKS], scalar1=bias_mean[:, 0:1], scalar2=None, op0=ALU.subtract)
-        gain_col = columns[:, CHUNKS : 2 * CHUNKS]
-        shift_col = columns[:, 2 * CHUNKS : 3 * CHUNKS]
-        eps_col = const.tile([P, 1], F32)
-        nc.vector.memset(eps_col[:], EPS)
-
-        row_index = const.tile([P, BATCH, 2], I32)
-        with tc.tile_pool(name="setup", bufs=1) as setup:
-            segments = setup.tile([P, BATCH, 4], BF16)
-            for s in range(2):
-                nc.sync.dma_start(out=segments[64 * s : 64 * s + 64], in_=frame_segments.rearrange("b n s -> n b s"))
-            ends = setup.tile([P, 2, BATCH, 2], F32)
-            nc.vector.tensor_scalar(
-                out=ends[:], in0=segments[:].rearrange("p b (h e) -> p e b h", e=2), scalar1=0.0, scalar2=FRAMES - 1.0, op0=ALU.max, op1=ALU.min
-            )
-            as_int = setup.tile([P, 2, BATCH, 2], I32)
-            nc.vector.tensor_copy(out=as_int[:], in_=ends[:])
-            near = setup.tile([P, 2, BATCH, 2], F32)
-            nc.vector.tensor_copy(out=near[:], in_=as_int[:])
-            above = setup.tile([P, 2, BATCH, 2], F32)
-            nc.vector.tensor_tensor(out=above[:], in0=near[:], in1=ends[:], op=ALU.is_gt)
-            whole = setup.tile([P, 2, BATCH, 2], F32)
-            nc.vector.tensor_tensor(out=whole[:], in0=near[:], in1=above[:], op=ALU.subtract)
-            first = whole[:, 0]
-            span = setup.tile([P, BATCH, 2], F32)
-            nc.vector.tensor_tensor(out=span[:], in0=whole[:, 1], in1=first, op=ALU.subtract)
-            filled = setup.tile([P, BATCH, 2], F32)
-            nc.vector.tensor_scalar(out=filled[:], in0=span[:], scalar1=0.0, scalar2=None, op0=ALU.is_ge)
-            nc.vector.tensor_scalar(out=span[:], in0=span[:], scalar1=0.0, scalar2=None, op0=ALU.max)
-            start = setup.tile([P, BATCH, 2], F32)
-            nc.vector.memset(start[:], 0.0)
-            reach = setup.tile([P, BATCH, 2], F32)
-            nc.vector.memset(reach[:], 0.0)
-            step = setup.tile([P, 2, BATCH, 2], F32)
-            for k in range(1, LEVELS):
-                nc.vector.tensor_scalar(
-                    out=step[:, 0], in0=span[:], scalar1=2.0 ** k - 1.0, scalar2=float(level_start[k] - level_start[k - 1]),
-                    op0=ALU.is_ge, op1=ALU.mult,
-                )
-                nc.vector.tensor_scalar(
-                    out=step[:, 1], in0=span[:], scalar1=2.0 ** k - 1.0, scalar2=2.0 ** (k - 1), op0=ALU.is_ge, op1=ALU.mult
-                )
-                nc.vector.tensor_tensor(out=start[:], in0=start[:], in1=step[:, 0], op=ALU.add)
-                nc.vector.tensor_tensor(out=reach[:], in0=reach[:], in1=step[:, 1], op=ALU.add)
-            entry = setup.tile([P, BATCH, 2], F32)
-            nc.vector.tensor_tensor(out=entry[:], in0=start[:], in1=first, op=ALU.add)
-            nc.vector.tensor_tensor(out=span[:], in0=span[:], in1=reach[:], op=ALU.subtract)
-            nc.vector.scalar_tensor_tensor(out=entry[:], in0=span[:], scalar=side[:, 0:1], in1=entry[:], op0=ALU.mult, op1=ALU.add)
-            entry_int = setup.tile([P, BATCH, 2], I32)
-            nc.vector.tensor_copy(out=entry_int[:], in_=entry[:])
-            tile_int = setup.tile([P, BATCH, 2], I32)
-            nc.vector.tensor_single_scalar(out=tile_int[:], in_=entry_int[:], scalar=7, op=ALU.arith_shift_right)
-            tile_f = setup.tile([P, BATCH, 2], F32)
-            nc.vector.tensor_copy(out=tile_f[:], in_=tile_int[:])
-            row_f = setup.tile([P, BATCH, 2], F32)
-            nc.vector.tensor_scalar(out=row_f[:], in0=entry[:], scalar1=float(TABLE_TILES), scalar2=None, op0=ALU.mult)
-            nc.vector.scalar_tensor_tensor(
-                out=row_f[:], in0=tile_f[:], scalar=1.0 - float(TABLE_TILES * P), in1=row_f[:], op0=ALU.mult, op1=ALU.add
-            )
-            spare_rows = P - used_entries % P
-            spare = setup.tile([P, 1], F32)
-            nc.vector.tensor_scalar(out=spare[:], in0=partition_f[:], scalar1=float(spare_rows), scalar2=-float(spare_rows), op0=ALU.is_ge, op1=ALU.mult)
-            nc.vector.tensor_tensor(out=spare[:], in0=spare[:], in1=partition_f[:], op=ALU.add)
-            nc.vector.tensor_scalar(
-                out=spare[:], in0=spare[:], scalar1=float(TABLE_TILES), scalar2=float(TABLE_TILES * (used_entries % P) + TABLE_TILES - 1),
-                op0=ALU.mult, op1=ALU.add,
-            )
-            nc.vector.tensor_scalar(out=row_f[:], in0=row_f[:], scalar1=spare[:, 0:1], scalar2=None, op0=ALU.subtract)
-            nc.vector.tensor_tensor(out=row_f[:], in0=row_f[:], in1=filled[:], op=ALU.mult)
-            nc.vector.tensor_scalar(out=row_f[:], in0=row_f[:], scalar1=spare[:, 0:1], scalar2=None, op0=ALU.add)
-            region_int = setup.tile([P, BATCH, 2], I32)
-            nc.gpsimd.iota(
-                region_int[:].rearrange("p b h -> p (b h)"), pattern=[[0, 2 * BATCH // REGIONS], [REGION_ROWS, REGIONS]], base=0, channel_multiplier=0
-            )
-            region_f = setup.tile([P, BATCH, 2], F32)
-            nc.vector.tensor_copy(out=region_f[:], in_=region_int[:])
-            nc.vector.tensor_tensor(out=row_f[:], in0=row_f[:], in1=region_f[:], op=ALU.add)
-            nc.vector.tensor_copy(out=row_index[:], in_=row_f[:])
-
         table_ring = []
         for s in range(RING):
             table = const.tile([P, 2, ENTRIES, 2], BF16, name="table%d" % s)
-            nc.vector.memset(table[:, :, level_start[1] + FRAMES - 1 : level_start[2], :], 0.0)
             nc.vector.memset(table[:, :, used_entries:ENTRIES, :], 0.0)
             table_ring.append(table)
 
-        zero_rows = const.tile([P, ROW_WORDS], F32)
-        nc.vector.memset(zero_rows[:], 0.0)
-        for s in range(REGIONS):
-            unused = flat_out[s * REGION_ROWS * ROW_WORDS : (s + 1) * REGION_ROWS * ROW_WORDS].rearrange("(p a w) -> p a w", p=P, w=ROW_WORDS)
-            nc.sync.dma_start(out=unused[used_entries % P : P, TABLE_TILES - 1, :], in_=zero_rows[used_entries % P : P, :])
+        w_sorted = const.tile([P, CHANNELS], U32, align_bytes=64)
+        s_sorted = const.tile([P, CHANNELS], U8, align_bytes=64)
+        group_average = const.tile([P, P], F32)
+        columns = const.tile([P, 3 * CHUNKS], F32)
+        gain_col = columns[:, CHUNKS : 2 * CHUNKS]
+        shift_col = columns[:, 2 * CHUNKS : 3 * CHUNKS]
+        bias_centred = const.tile([P, CHUNKS], F32)
+        eps_col = const.tile([P, 1], F32)
+        row_index = const.tile([P, BATCH, 2], I32)
+
+        column_group = const.tile([P, P], I32)
+        partition_index = const.tile([P, 1], I32)
+        partition_group = const.tile([P, 1], I32)
+        column_group_f = const.tile([P, P], F32)
+        partition_group_f = const.tile([P, 1], F32)
+        partition_f = const.tile([P, 1], F32)
+        side = const.tile([P, 1], F32)
+        bias_rows = const.tile([P, CHUNKS], F32)
+        bias_mean = const.tile([P, 1], F32)
+
+        def prepare():
+            nc.gpsimd.tensor_copy(
+                out=w_sorted[:].bitcast(I32).rearrange("p (q m) -> p q m", q=CHUNKS), in_=w_words[:].bitcast(I32).rearrange("p (m q) -> p q m", q=CHUNKS)
+            )
+            nc.vector.tensor_copy(out=s_sorted[:].rearrange("p (q m) -> p m q", q=CHUNKS), in_=w_scales[:].rearrange("p (m q) -> p m q", q=CHUNKS))
+
+            nc.gpsimd.iota(column_group[:], pattern=[[1, P // GROUP_PARTITIONS], [0, GROUP_PARTITIONS]], base=0, channel_multiplier=0)
+            nc.gpsimd.iota(partition_index[:], pattern=[[0, 1]], base=0, channel_multiplier=1)
+            nc.vector.tensor_single_scalar(out=partition_group[:], in_=partition_index[:], scalar=2, op=ALU.arith_shift_right)
+            nc.vector.tensor_copy(out=column_group_f[:], in_=column_group[:])
+            nc.vector.tensor_copy(out=partition_group_f[:], in_=partition_group[:])
+            nc.vector.tensor_scalar(
+                out=group_average[:], in0=column_group_f[:], scalar1=partition_group_f[:, 0:1], scalar2=1.0 / GROUP_SIZE,
+                op0=ALU.is_equal, op1=ALU.mult,
+            )
+            nc.vector.tensor_copy(out=partition_f[:], in_=partition_index[:])
+            nc.vector.tensor_scalar(out=side[:], in0=partition_f[:], scalar1=float(PROPOSALS), scalar2=None, op0=ALU.is_ge)
+
+            for i in range(3):
+                nc.vector.tensor_copy(out=columns[:, CHUNKS * i : CHUNKS * (i + 1)], in_=fours[i][:])
+            nc.vector.tensor_scalar(out=bias_rows[:], in0=columns[:, 0:CHUNKS], scalar1=float(PROPOSALS), scalar2=None, op0=ALU.mult)
+            bias_parts = small_psum.tile([P, CHUNKS], F32, name="bias_parts", tag="small")
+            nc.tensor.matmul(out=bias_parts[:], lhsT=group_average[:], rhs=bias_rows[:], start=True, stop=True)
+            nc.vector.tensor_reduce(out=bias_mean[:], in_=bias_parts[:], axis=AXIS.X, op=ALU.add)
+            nc.vector.tensor_scalar(out=bias_centred[:], in0=columns[:, 0:CHUNKS], scalar1=bias_mean[:, 0:1], scalar2=None, op0=ALU.subtract)
+            nc.vector.memset(eps_col[:], EPS)
+
+            with tc.tile_pool(name="setup", bufs=1) as setup:
+                ends = setup.tile([P, 2, BATCH, 2], F32)
+                nc.vector.tensor_scalar(
+                    out=ends[:], in0=segments[:].rearrange("p b (h e) -> p e b h", e=2), scalar1=0.0, scalar2=FRAMES - 1.0, op0=ALU.max, op1=ALU.min
+                )
+                as_int = setup.tile([P, 2, BATCH, 2], I32)
+                nc.vector.tensor_copy(out=as_int[:], in_=ends[:])
+                near = setup.tile([P, 2, BATCH, 2], F32)
+                nc.vector.tensor_copy(out=near[:], in_=as_int[:])
+                above = setup.tile([P, 2, BATCH, 2], F32)
+                nc.vector.tensor_tensor(out=above[:], in0=near[:], in1=ends[:], op=ALU.is_gt)
+                whole = setup.tile([P, 2, BATCH, 2], F32)
+                nc.vector.tensor_tensor(out=whole[:], in0=near[:], in1=above[:], op=ALU.subtract)
+                first = whole[:, 0]
+                span = setup.tile([P, BATCH, 2], F32)
+                nc.vector.tensor_tensor(out=span[:], in0=whole[:, 1], in1=first, op=ALU.subtract)
+                filled = setup.tile([P, BATCH, 2], F32)
+                nc.vector.tensor_scalar(out=filled[:], in0=span[:], scalar1=0.0, scalar2=None, op0=ALU.is_ge)
+                nc.vector.tensor_scalar(out=span[:], in0=span[:], scalar1=0.0, scalar2=None, op0=ALU.max)
+                start = setup.tile([P, BATCH, 2], F32)
+                nc.vector.memset(start[:], 0.0)
+                reach = setup.tile([P, BATCH, 2], F32)
+                nc.vector.memset(reach[:], 0.0)
+                step = setup.tile([P, 2, BATCH, 2], F32)
+                for k in range(1, LEVELS):
+                    nc.vector.tensor_scalar(
+                        out=step[:, 0], in0=span[:], scalar1=RUNS[k] - 1.0, scalar2=float(level_start[k] - level_start[k - 1]),
+                        op0=ALU.is_ge, op1=ALU.mult,
+                    )
+                    nc.vector.tensor_scalar(
+                        out=step[:, 1], in0=span[:], scalar1=RUNS[k] - 1.0, scalar2=float(RUNS[k] - RUNS[k - 1]), op0=ALU.is_ge, op1=ALU.mult
+                    )
+                    nc.vector.tensor_tensor(out=start[:], in0=start[:], in1=step[:, 0], op=ALU.add)
+                    nc.vector.tensor_tensor(out=reach[:], in0=reach[:], in1=step[:, 1], op=ALU.add)
+                entry = setup.tile([P, BATCH, 2], F32)
+                nc.vector.tensor_tensor(out=entry[:], in0=start[:], in1=first, op=ALU.add)
+                nc.vector.tensor_tensor(out=span[:], in0=span[:], in1=reach[:], op=ALU.subtract)
+                nc.vector.scalar_tensor_tensor(out=entry[:], in0=span[:], scalar=side[:, 0:1], in1=entry[:], op0=ALU.mult, op1=ALU.add)
+                entry_int = setup.tile([P, BATCH, 2], I32)
+                nc.vector.tensor_copy(out=entry_int[:], in_=entry[:])
+                tile_int = setup.tile([P, BATCH, 2], I32)
+                nc.vector.tensor_single_scalar(out=tile_int[:], in_=entry_int[:], scalar=7, op=ALU.arith_shift_right)
+                tile_f = setup.tile([P, BATCH, 2], F32)
+                nc.vector.tensor_copy(out=tile_f[:], in_=tile_int[:])
+                row_f = setup.tile([P, BATCH, 2], F32)
+                nc.vector.tensor_scalar(out=row_f[:], in0=entry[:], scalar1=float(TABLE_TILES), scalar2=None, op0=ALU.mult)
+                nc.vector.scalar_tensor_tensor(
+                    out=row_f[:], in0=tile_f[:], scalar=1.0 - float(TABLE_TILES * P), in1=row_f[:], op0=ALU.mult, op1=ALU.add
+                )
+                spare_rows = P - used_entries % P
+                spare = setup.tile([P, 1], F32)
+                nc.vector.tensor_copy(out=spare[:], in_=partition_f[:])
+                wrap = setup.tile([P, 1], F32)
+                for multiple in range(1, (P - 1) // spare_rows + 1):
+                    nc.vector.tensor_scalar(
+                        out=wrap[:], in0=partition_f[:], scalar1=float(multiple * spare_rows), scalar2=-float(spare_rows), op0=ALU.is_ge, op1=ALU.mult
+                    )
+                    nc.vector.tensor_tensor(out=spare[:], in0=spare[:], in1=wrap[:], op=ALU.add)
+                nc.vector.tensor_scalar(
+                    out=spare[:], in0=spare[:], scalar1=float(TABLE_TILES), scalar2=float(TABLE_TILES * (used_entries % P) + TABLE_TILES - 1),
+                    op0=ALU.mult, op1=ALU.add,
+                )
+                nc.vector.tensor_scalar(out=row_f[:], in0=row_f[:], scalar1=spare[:, 0:1], scalar2=None, op0=ALU.subtract)
+                nc.vector.tensor_tensor(out=row_f[:], in0=row_f[:], in1=filled[:], op=ALU.mult)
+                nc.vector.tensor_scalar(out=row_f[:], in0=row_f[:], scalar1=spare[:, 0:1], scalar2=None, op0=ALU.add)
+                cycles = (2 * BATCH + REGIONS - 1) // REGIONS
+                region_int = setup.tile([P, cycles * REGIONS], I32)
+                nc.gpsimd.iota(region_int[:], pattern=[[0, cycles], [REGION_ROWS, REGIONS]], base=0, channel_multiplier=0)
+                region_f = setup.tile([P, BATCH, 2], F32)
+                nc.vector.tensor_copy(out=region_f[:].rearrange("p b h -> p (b h)"), in_=region_int[:, 0 : 2 * BATCH])
+                nc.vector.tensor_tensor(out=row_f[:], in0=row_f[:], in1=region_f[:], op=ALU.add)
+                nc.vector.tensor_copy(out=row_index[:], in_=row_f[:])
 
         result = const.tile([P, BATCH, CHUNKS, PROPOSALS], F32)
 
-        with tc.tile_pool(name="turned", bufs=3) as turned_pool, tc.tile_pool(name="fetch", bufs=4) as fetch_pool, tc.tile_pool(
+        with tc.tile_pool(name="work", bufs=2) as work_pool, tc.tile_pool(name="turned", bufs=3) as turned_pool, tc.tile_pool(name="fetch", bufs=4) as fetch_pool, tc.tile_pool(
             name="operands", bufs=2
         ) as operand_pool, tc.tile_pool(name="norm", bufs=2) as norm_pool, tc.psum_pool(name="table_psum", bufs=3) as table_psum, tc.psum_pool(
             name="small_psum", bufs=1
@@ -247,8 +251,7 @@ def tile_coarsepyramid_pb_kernel(
                     if bank < EARLY_BANKS and all((half, other) in emptied_banks for other in range(EARLY_BANKS)):
                         write(half, slice(0, P), slice(0, BANK_TILES * EARLY_BANKS))
                     if bank == (TABLE_TILES - 1) // BANK_TILES:
-                        write(half, slice(0, P), slice(BANK_TILES * EARLY_BANKS, used_entries // P))
-                        write(half, slice(0, used_entries % P), slice(used_entries // P, used_entries // P + 1))
+                        write(half, slice(0, P), slice(BANK_TILES * EARLY_BANKS, TABLE_TILES))
 
                 landings = {}
 
@@ -273,13 +276,25 @@ def tile_coarsepyramid_pb_kernel(
                 turned_tiles = 0
                 for k in range(LEVELS):
                     if k > 0:
-                        width = level_size[k] if k > 1 else FRAMES - 1
                         lower = level_start[k - 1]
+                        if RUNS[k] == 2 * RUNS[k - 1]:
+                            longer = None
+                        else:
+                            longer = work_pool.tile([P, 2, FRAMES, 2], BF16, name="longer")
+                            for half in range(2):
+                                nc.vector.tensor_tensor(
+                                    out=longer[:, half, 0 : level_size[k - 1] - 1, :],
+                                    in0=table[:, half, lower : lower + level_size[k - 1] - 1, :],
+                                    in1=table[:, half, lower + 1 : lower + level_size[k - 1], :],
+                                    op=ALU.max,
+                                )
+                        width = level_size[k]
+                        further = RUNS[k] - RUNS[k - 1]
                         for half in range(2):
                             nc.vector.tensor_tensor(
                                 out=table[:, half, level_start[k] : level_start[k] + width, :],
-                                in0=table[:, half, lower : lower + width, :],
-                                in1=table[:, half, lower + 2 ** (k - 1) : lower + 2 ** (k - 1) + width, :],
+                                in0=table[:, half, lower : lower + width, :] if longer is None else longer[:, half, 0:width, :],
+                                in1=table[:, half, lower + further : lower + further + width, :],
                                 op=ALU.max,
                             )
                         if pieces:
@@ -414,6 +429,8 @@ def tile_coarsepyramid_pb_kernel(
                     build(i)
                 if i + 1 < BATCH:
                     weave(i + 1)
+                if i == 0:
+                    prepare()
                 b = i - POOL_LAG
                 if b >= 0 and b % 2 == 1:
                     first_batch, count = round_of[b]

@@ -37,7 +37,7 @@ REGIONS = 7
 REGION_ROWS = ENTRIES
 BANK_TILES = 4
 EARLY_BANKS = 2
-VECTOR_BANKS = (0,)
+VECTOR_BANKS = ((0, 0),)
 
 
 def tile_coarsepyramid_pb_kernel(
@@ -230,7 +230,7 @@ def tile_coarsepyramid_pb_kernel(
         ) as small_psum, tc.psum_pool(name="product_psum", bufs=CHUNKS) as product_psum:
 
             def weave(b):
-                nc.vector.tensor_copy(out=table_ring[b % RING][:, :, 0:FRAMES, :], in_=raw_of[b][:].rearrange("p h j t -> p h t j"))
+                nc.scalar.copy(out=table_ring[b % RING][:, :, 0:FRAMES, :], in_=raw_of[b][:].rearrange("p h j t -> p h t j"))
 
             def build(b):
                 table = table_ring[b % RING]
@@ -265,14 +265,14 @@ def tile_coarsepyramid_pb_kernel(
                         table[:, half, P * a : P * (a + 1), :].rearrange("p e j -> p (e j)").bitcast(F32),
                         identity_words[:],
                     )
-                    if (a % BANK_TILES == BANK_TILES - 1 or a == TABLE_TILES - 1) and bank not in VECTOR_BANKS:
+                    if (a % BANK_TILES == BANK_TILES - 1 or a == TABLE_TILES - 1) and (half, bank) not in VECTOR_BANKS:
                         nc.scalar.copy(
-                            out=turned[half][:, BANK_TILES * bank : a + 1, :].rearrange("p a c -> p (a c)"),
-                            in_=landing[:, 0 : a % BANK_TILES + 1, :].rearrange("p a m -> p (a m)").bitcast(BF16),
+                            out=turned[half][:, BANK_TILES * bank : a + 1, :].rearrange("p a c -> p (a c)").bitcast(F32),
+                            in_=landing[:, 0 : a % BANK_TILES + 1, :].rearrange("p a m -> p (a m)"),
                         )
                         emptied(half, bank)
 
-                pieces = [(half, bank, piece) for bank in VECTOR_BANKS for piece in range(2) for half in range(2)]
+                pieces = {2 * piece + 1: (half, bank, piece) for half, bank in VECTOR_BANKS for piece in range(2)}
                 turned_tiles = 0
                 for k in range(LEVELS):
                     if k > 0:
@@ -297,9 +297,8 @@ def tile_coarsepyramid_pb_kernel(
                                 in1=table[:, half, lower + further : lower + further + width, :],
                                 op=ALU.max,
                             )
-                        if pieces:
-                            half, bank, piece = pieces[0]
-                            pieces = pieces[1:]
+                        if k in pieces:
+                            half, bank, piece = pieces[k]
                             two = slice(2 * piece, 2 * piece + 2)
                             nc.vector.tensor_copy(
                                 out=turned[half][:, BANK_TILES * bank + 2 * piece : BANK_TILES * bank + 2 * piece + 2, :].rearrange("p a c -> p (a c)"),

@@ -17,6 +17,7 @@ AXIS = mybir.AxisListType
 P = 128
 PACK = 4
 BATCH = 48
+PAIRS = BATCH // 2
 CHANNELS = 512
 HALF = CHANNELS // 2
 FRAMES = 256
@@ -25,48 +26,38 @@ GROUP_CHANNELS = 16
 GROUP_SIZE = GROUP_CHANNELS * PROPOSALS
 GROUP_PARTITIONS = 4
 EPS = 1e-5
-ROUND = 8
 CHUNKS = CHANNELS // P
-RUNS = (1, 3, 7, 14, 28, 56, 112, 224)
-LEVELS = len(RUNS)
-TABLE_TILES = 13
-ENTRIES = TABLE_TILES * P
+ROUND = 8
+LARGEST = 3.3895313892515355e38
+ZONES = 3
+SLOTS = 4
+ZONE_ROWS = FRAMES
 ROW_WORDS = HALF // 2
-RING = 3
-REGIONS = 7
-REGION_ROWS = ENTRIES
-BANK_TILES = 4
-EARLY_BANKS = 2
-VECTOR_BANKS = ((0, 0),)
+TABLE_ROWS = ZONES * ZONE_ROWS
+UNIT_ROWS = 2 * TABLE_ROWS
+SPARE_ROWS = 4
+UNIT_PITCH = UNIT_ROWS + SPARE_ROWS
+UNITS = 7
+PAD = 4
 
 
 def tile_coarsepyramid_pb_kernel(
     tc, frame_level_feature, frame_segments, w_roi_words, w_roi_scales, b_roi, g_roi, be_roi, out
 ):
     nc = tc.nc
-    level_size = [FRAMES + 1 - run for run in RUNS]
-    level_start = [sum(level_size[0:k]) for k in range(LEVELS)]
-    used_entries = level_start[LEVELS - 1] + level_size[LEVELS - 1]
-    assert used_entries <= ENTRIES and used_entries // P == TABLE_TILES - 1
-
     flat_out = out.rearrange("b c n -> (b c n)")
     out_rows = flat_out.rearrange("(r w) -> r w", w=ROW_WORDS)
-    assert REGIONS * REGION_ROWS <= BATCH * CHANNELS * PROPOSALS // ROW_WORDS
+    assert UNITS * UNIT_PITCH <= BATCH * CHANNELS * PROPOSALS // ROW_WORDS
 
     with tc.tile_pool(name="const", bufs=1) as const, tc.tile_pool(name="raw", bufs=3) as raw_pool:
         raw_of = {}
 
-        def load(b):
-            raw = raw_pool.tile([P, 2, 2, FRAMES], BF16, name="raw")
-            for half in range(2):
-                nc.sync.dma_start(
-                    out=raw[:, half],
-                    in_=frame_level_feature[b, HALF * half : HALF * (half + 1), :].rearrange("(m j) t -> m j t", j=2),
-                )
-            raw_of[b] = raw
+        def load(i):
+            raw = raw_pool.tile([P, 2, PACK * FRAMES], BF16, name="raw")
+            nc.sync.dma_start(out=raw[:], in_=frame_level_feature[2 * i : 2 * i + 2].rearrange("b (m j) t -> m b (j t)", j=PACK))
+            raw_of[i] = raw
 
         load(0)
-        load(1)
 
         w_words = const.tile([P, CHANNELS], U32, align_bytes=64)
         nc.sync.dma_start(
@@ -86,20 +77,32 @@ def tile_coarsepyramid_pb_kernel(
             four = const.tile([P, CHUNKS], BF16, name="four%d" % i)
             nc.sync.dma_start(out=four[:], in_=vector.rearrange("(p q) -> p q", q=CHUNKS))
             fours.append(four)
-        segments = const.tile([P, BATCH, 4], BF16)
+        segments = const.tile([P, PAIRS, 4], BF16)
         for s in range(2):
-            nc.sync.dma_start(out=segments[64 * s : 64 * s + 64], in_=frame_segments.rearrange("b n s -> n b s"))
+            nc.sync.dma_start(out=segments[64 * s : 64 * s + 64], in_=frame_segments.rearrange("(i s) n e -> s n i e", s=2)[s])
 
         identity = const.tile([P, P], BF16)
         make_identity(nc, identity[:])
         identity_words = const.tile([P, P], F32)
         make_identity(nc, identity_words[:])
 
-        table_ring = []
-        for s in range(RING):
-            table = const.tile([P, 2, ENTRIES, 2], BF16, name="table%d" % s)
-            nc.vector.memset(table[:, :, used_entries:ENTRIES, :], 0.0)
-            table_ring.append(table)
+        zeros = const.tile([UNITS, SPARE_ROWS * ROW_WORDS], F32)
+        nc.vector.memset(zeros[:], 0.0)
+        nc.sync.dma_start(
+            out=out_rows[0 : UNITS * UNIT_PITCH].rearrange("(u r) w -> u (r w)", u=UNITS)[:, UNIT_ROWS * ROW_WORDS : UNIT_PITCH * ROW_WORDS],
+            in_=zeros[:],
+        )
+
+        frames_ring = [const.tile([P, 2, FRAMES, PACK], BF16, name="frames%d" % s) for s in range(3)]
+        run2 = const.tile([P, 2, FRAMES, PACK], BF16)
+        run4 = const.tile([P, 2, 2, FRAMES // 2 + PAD, PACK], BF16)
+        run8_ring = [const.tile([P, 2, FRAMES, PACK], BF16, name="run8_%d" % s) for s in range(2)]
+        run16 = const.tile([P, 2, FRAMES + PAD, PACK], BF16)
+        run32 = const.tile([P, 2, FRAMES + PAD, PACK], BF16)
+        run64_ring = [const.tile([P, 2, FRAMES, PACK], BF16, name="run64_%d" % s) for s in range(2)]
+        nc.vector.memset(run4[:, :, :, FRAMES // 2 - 2 : FRAMES // 2 + PAD, :], 0.0)
+        nc.vector.memset(run16[:, :, FRAMES : FRAMES + PAD, :], 0.0)
+        nc.vector.memset(run32[:, :, FRAMES : FRAMES + PAD, :], 0.0)
 
         w_sorted = const.tile([P, CHANNELS], U32, align_bytes=64)
         s_sorted = const.tile([P, CHANNELS], U8, align_bytes=64)
@@ -109,7 +112,9 @@ def tile_coarsepyramid_pb_kernel(
         shift_col = columns[:, 2 * CHUNKS : 3 * CHUNKS]
         bias_centred = const.tile([P, CHUNKS], F32)
         eps_col = const.tile([P, 1], F32)
-        row_index = const.tile([P, BATCH, 2], I32)
+        row_index = const.tile([P, PAIRS, 2, 2], I32)
+        filled = const.tile([P, PAIRS, 2], F32)
+        slot_limit = const.tile([P, PAIRS, 2, SLOTS - 1], F32)
 
         column_group = const.tile([P, P], I32)
         partition_index = const.tile([P, 1], I32)
@@ -122,13 +127,93 @@ def tile_coarsepyramid_pb_kernel(
         bias_mean = const.tile([P, 1], F32)
 
         def prepare():
+            nc.gpsimd.iota(partition_index[:], pattern=[[0, 1]], base=0, channel_multiplier=1)
+            nc.vector.tensor_copy(out=partition_f[:], in_=partition_index[:])
+            nc.vector.tensor_scalar(out=side[:], in0=partition_f[:], scalar1=float(PROPOSALS), scalar2=None, op0=ALU.is_ge)
+            with tc.tile_pool(name="setup", bufs=1) as setup:
+                shape = [P, PAIRS, 2]
+                both = [P, 2, PAIRS, 2]
+                tt = nc.vector.tensor_tensor
+                ts = nc.vector.tensor_scalar
+
+                def whole_of(shift, source_int, dims, name):
+                    shifted = setup.tile(dims, I32, name=name + "_int")
+                    nc.vector.tensor_single_scalar(out=shifted[:], in_=source_int[:], scalar=shift, op=ALU.arith_shift_right)
+                    value = setup.tile(dims, F32, name=name)
+                    nc.vector.tensor_copy(out=value[:], in_=shifted[:])
+                    return value
+
+                ends = setup.tile(both, F32, name="ends")
+                ts(out=ends[:], in0=segments[:].rearrange("p i (h e) -> p e i h", e=2), scalar1=0.0, scalar2=FRAMES - 1.0, op0=ALU.max, op1=ALU.min)
+                as_int = setup.tile(both, I32, name="as_int")
+                nc.vector.tensor_copy(out=as_int[:], in_=ends[:])
+                near = setup.tile(both, F32, name="near")
+                nc.vector.tensor_copy(out=near[:], in_=as_int[:])
+                above = setup.tile(both, F32, name="above")
+                tt(out=above[:], in0=near[:], in1=ends[:], op=ALU.is_gt)
+                start = setup.tile(both, F32, name="start")
+                tt(out=start[:], in0=near[:], in1=above[:], op=ALU.subtract)
+                span = setup.tile(shape, F32, name="span")
+                tt(out=span[:], in0=start[:, 1], in1=start[:, 0], op=ALU.subtract)
+                ts(out=filled[:], in0=span[:], scalar1=0.0, scalar2=None, op0=ALU.is_ge)
+                ts(out=span[:], in0=span[:], scalar1=0.0, scalar2=None, op0=ALU.max)
+                level1 = setup.tile(shape, F32, name="level1")
+                ts(out=level1[:], in0=span[:], scalar1=8.0, scalar2=None, op0=ALU.is_ge)
+                level2 = setup.tile(shape, F32, name="level2")
+                ts(out=level2[:], in0=span[:], scalar1=64.0, scalar2=None, op0=ALU.is_ge)
+                run = setup.tile(shape, F32, name="run")
+                ts(out=run[:], in0=level1[:], scalar1=7.0, scalar2=1.0, op0=ALU.mult, op1=ALU.add)
+                nc.vector.scalar_tensor_tensor(out=run[:], in0=level2[:], scalar=56.0, in1=run[:], op0=ALU.mult, op1=ALU.add)
+                span_int = setup.tile(shape, I32, name="span_int")
+                nc.vector.tensor_copy(out=span_int[:], in_=span[:])
+                more = whole_of(1, span_int, shape, "more")
+                more1 = whole_of(4, span_int, shape, "more1")
+                more2 = whole_of(7, span_int, shape, "more2")
+                tt(out=more2[:], in0=more2[:], in1=more1[:], op=ALU.subtract)
+                tt(out=more1[:], in0=more1[:], in1=more[:], op=ALU.subtract)
+                tt(out=more1[:], in0=more1[:], in1=level1[:], op=ALU.mult)
+                tt(out=more2[:], in0=more2[:], in1=level2[:], op=ALU.mult)
+                tt(out=more[:], in0=more[:], in1=more1[:], op=ALU.add)
+                tt(out=more[:], in0=more[:], in1=more2[:], op=ALU.add)
+                for slot in range(1, SLOTS):
+                    limit = slot_limit[:, :, :, slot - 1]
+                    ts(out=limit, in0=more[:], scalar1=float(slot), scalar2=2.0, op0=ALU.is_ge, op1=ALU.mult)
+                    ts(out=limit, in0=limit, scalar1=1.0, scalar2=LARGEST, op0=ALU.subtract, op1=ALU.mult)
+                tt(out=more[:], in0=more[:], in1=run[:], op=ALU.mult)
+                tt(out=more[:], in0=more[:], in1=run[:], op=ALU.add)
+                nc.vector.scalar_tensor_tensor(out=start[:, 1], in0=start[:, 1], scalar=1.0, in1=more[:], op0=ALU.add, op1=ALU.subtract)
+                start_int = setup.tile(both, I32, name="start_int")
+                nc.vector.tensor_copy(out=start_int[:], in_=start[:])
+                eighth = whole_of(3, start_int, both, "eighth")
+                ts(out=eighth[:], in0=eighth[:], scalar1=float(1 - 32 * 8), scalar2=float(ZONE_ROWS), op0=ALU.mult, op1=ALU.add)
+                sixty_fourth = whole_of(6, start_int, both, "sixty_fourth")
+                ts(out=sixty_fourth[:], in0=sixty_fourth[:], scalar1=float(1 - 4 * 64), scalar2=float(2 * ZONE_ROWS), op0=ALU.mult, op1=ALU.add)
+                tt(out=sixty_fourth[:], in0=sixty_fourth[:], in1=eighth[:], op=ALU.subtract)
+                nc.vector.scalar_tensor_tensor(out=eighth[:], in0=start[:], scalar=31.0, in1=eighth[:], op0=ALU.mult, op1=ALU.add)
+                nc.vector.scalar_tensor_tensor(out=sixty_fourth[:], in0=start[:], scalar=-28.0, in1=sixty_fourth[:], op0=ALU.mult, op1=ALU.add)
+                for end in range(2):
+                    tt(out=eighth[:, end], in0=eighth[:, end], in1=level1[:], op=ALU.mult)
+                    tt(out=sixty_fourth[:, end], in0=sixty_fourth[:, end], in1=level2[:], op=ALU.mult)
+                tt(out=start[:], in0=start[:], in1=eighth[:], op=ALU.add)
+                tt(out=start[:], in0=start[:], in1=sixty_fourth[:], op=ALU.add)
+                cycles = (2 * PAIRS + UNITS - 1) // UNITS
+                unit_int = setup.tile([P, cycles * UNITS], I32, name="unit_int")
+                nc.gpsimd.iota(unit_int[:], pattern=[[0, cycles], [UNIT_PITCH, UNITS]], base=0, channel_multiplier=0)
+                base = setup.tile(shape, F32, name="base")
+                nc.vector.tensor_copy(out=base[:].rearrange("p i h -> p (i h)"), in_=unit_int[:, 0 : 2 * PAIRS])
+                behind = setup.tile([P, 1], F32, name="behind")
+                ts(out=behind[:], in0=side[:], scalar1=float(TABLE_ROWS), scalar2=None, op0=ALU.mult)
+                ts(out=base[:], in0=base[:], scalar1=behind[:, 0:1], scalar2=None, op0=ALU.add)
+                for end in range(2):
+                    tt(out=start[:, end], in0=start[:, end], in1=base[:], op=ALU.add)
+                    nc.vector.tensor_copy(out=row_index[:, :, :, end], in_=start[:, end])
+
             nc.gpsimd.tensor_copy(
                 out=w_sorted[:].bitcast(I32).rearrange("p (q m) -> p q m", q=CHUNKS), in_=w_words[:].bitcast(I32).rearrange("p (m q) -> p q m", q=CHUNKS)
             )
             nc.vector.tensor_copy(out=s_sorted[:].rearrange("p (q m) -> p m q", q=CHUNKS), in_=w_scales[:].rearrange("p (m q) -> p m q", q=CHUNKS))
 
             nc.gpsimd.iota(column_group[:], pattern=[[1, P // GROUP_PARTITIONS], [0, GROUP_PARTITIONS]], base=0, channel_multiplier=0)
-            nc.gpsimd.iota(partition_index[:], pattern=[[0, 1]], base=0, channel_multiplier=1)
             nc.vector.tensor_single_scalar(out=partition_group[:], in_=partition_index[:], scalar=2, op=ALU.arith_shift_right)
             nc.vector.tensor_copy(out=column_group_f[:], in_=column_group[:])
             nc.vector.tensor_copy(out=partition_group_f[:], in_=partition_group[:])
@@ -136,8 +221,6 @@ def tile_coarsepyramid_pb_kernel(
                 out=group_average[:], in0=column_group_f[:], scalar1=partition_group_f[:, 0:1], scalar2=1.0 / GROUP_SIZE,
                 op0=ALU.is_equal, op1=ALU.mult,
             )
-            nc.vector.tensor_copy(out=partition_f[:], in_=partition_index[:])
-            nc.vector.tensor_scalar(out=side[:], in0=partition_f[:], scalar1=float(PROPOSALS), scalar2=None, op0=ALU.is_ge)
 
             for i in range(3):
                 nc.vector.tensor_copy(out=columns[:, CHUNKS * i : CHUNKS * (i + 1)], in_=fours[i][:])
@@ -148,193 +231,119 @@ def tile_coarsepyramid_pb_kernel(
             nc.vector.tensor_scalar(out=bias_centred[:], in0=columns[:, 0:CHUNKS], scalar1=bias_mean[:, 0:1], scalar2=None, op0=ALU.subtract)
             nc.vector.memset(eps_col[:], EPS)
 
-            with tc.tile_pool(name="setup", bufs=1) as setup:
-                ends = setup.tile([P, 2, BATCH, 2], F32)
-                nc.vector.tensor_scalar(
-                    out=ends[:], in0=segments[:].rearrange("p b (h e) -> p e b h", e=2), scalar1=0.0, scalar2=FRAMES - 1.0, op0=ALU.max, op1=ALU.min
-                )
-                as_int = setup.tile([P, 2, BATCH, 2], I32)
-                nc.vector.tensor_copy(out=as_int[:], in_=ends[:])
-                near = setup.tile([P, 2, BATCH, 2], F32)
-                nc.vector.tensor_copy(out=near[:], in_=as_int[:])
-                above = setup.tile([P, 2, BATCH, 2], F32)
-                nc.vector.tensor_tensor(out=above[:], in0=near[:], in1=ends[:], op=ALU.is_gt)
-                whole = setup.tile([P, 2, BATCH, 2], F32)
-                nc.vector.tensor_tensor(out=whole[:], in0=near[:], in1=above[:], op=ALU.subtract)
-                first = whole[:, 0]
-                span = setup.tile([P, BATCH, 2], F32)
-                nc.vector.tensor_tensor(out=span[:], in0=whole[:, 1], in1=first, op=ALU.subtract)
-                filled = setup.tile([P, BATCH, 2], F32)
-                nc.vector.tensor_scalar(out=filled[:], in0=span[:], scalar1=0.0, scalar2=None, op0=ALU.is_ge)
-                nc.vector.tensor_scalar(out=span[:], in0=span[:], scalar1=0.0, scalar2=None, op0=ALU.max)
-                start = setup.tile([P, BATCH, 2], F32)
-                nc.vector.memset(start[:], 0.0)
-                reach = setup.tile([P, BATCH, 2], F32)
-                nc.vector.memset(reach[:], 0.0)
-                step = setup.tile([P, 2, BATCH, 2], F32)
-                for k in range(1, LEVELS):
-                    nc.vector.tensor_scalar(
-                        out=step[:, 0], in0=span[:], scalar1=RUNS[k] - 1.0, scalar2=float(level_start[k] - level_start[k - 1]),
-                        op0=ALU.is_ge, op1=ALU.mult,
-                    )
-                    nc.vector.tensor_scalar(
-                        out=step[:, 1], in0=span[:], scalar1=RUNS[k] - 1.0, scalar2=float(RUNS[k] - RUNS[k - 1]), op0=ALU.is_ge, op1=ALU.mult
-                    )
-                    nc.vector.tensor_tensor(out=start[:], in0=start[:], in1=step[:, 0], op=ALU.add)
-                    nc.vector.tensor_tensor(out=reach[:], in0=reach[:], in1=step[:, 1], op=ALU.add)
-                entry = setup.tile([P, BATCH, 2], F32)
-                nc.vector.tensor_tensor(out=entry[:], in0=start[:], in1=first, op=ALU.add)
-                nc.vector.tensor_tensor(out=span[:], in0=span[:], in1=reach[:], op=ALU.subtract)
-                nc.vector.scalar_tensor_tensor(out=entry[:], in0=span[:], scalar=side[:, 0:1], in1=entry[:], op0=ALU.mult, op1=ALU.add)
-                entry_int = setup.tile([P, BATCH, 2], I32)
-                nc.vector.tensor_copy(out=entry_int[:], in_=entry[:])
-                tile_int = setup.tile([P, BATCH, 2], I32)
-                nc.vector.tensor_single_scalar(out=tile_int[:], in_=entry_int[:], scalar=7, op=ALU.arith_shift_right)
-                tile_f = setup.tile([P, BATCH, 2], F32)
-                nc.vector.tensor_copy(out=tile_f[:], in_=tile_int[:])
-                row_f = setup.tile([P, BATCH, 2], F32)
-                nc.vector.tensor_scalar(out=row_f[:], in0=entry[:], scalar1=float(TABLE_TILES), scalar2=None, op0=ALU.mult)
-                nc.vector.scalar_tensor_tensor(
-                    out=row_f[:], in0=tile_f[:], scalar=1.0 - float(TABLE_TILES * P), in1=row_f[:], op0=ALU.mult, op1=ALU.add
-                )
-                spare_rows = P - used_entries % P
-                spare = setup.tile([P, 1], F32)
-                nc.vector.tensor_copy(out=spare[:], in_=partition_f[:])
-                wrap = setup.tile([P, 1], F32)
-                for multiple in range(1, (P - 1) // spare_rows + 1):
-                    nc.vector.tensor_scalar(
-                        out=wrap[:], in0=partition_f[:], scalar1=float(multiple * spare_rows), scalar2=-float(spare_rows), op0=ALU.is_ge, op1=ALU.mult
-                    )
-                    nc.vector.tensor_tensor(out=spare[:], in0=spare[:], in1=wrap[:], op=ALU.add)
-                nc.vector.tensor_scalar(
-                    out=spare[:], in0=spare[:], scalar1=float(TABLE_TILES), scalar2=float(TABLE_TILES * (used_entries % P) + TABLE_TILES - 1),
-                    op0=ALU.mult, op1=ALU.add,
-                )
-                nc.vector.tensor_scalar(out=row_f[:], in0=row_f[:], scalar1=spare[:, 0:1], scalar2=None, op0=ALU.subtract)
-                nc.vector.tensor_tensor(out=row_f[:], in0=row_f[:], in1=filled[:], op=ALU.mult)
-                nc.vector.tensor_scalar(out=row_f[:], in0=row_f[:], scalar1=spare[:, 0:1], scalar2=None, op0=ALU.add)
-                cycles = (2 * BATCH + REGIONS - 1) // REGIONS
-                region_int = setup.tile([P, cycles * REGIONS], I32)
-                nc.gpsimd.iota(region_int[:], pattern=[[0, cycles], [REGION_ROWS, REGIONS]], base=0, channel_multiplier=0)
-                region_f = setup.tile([P, BATCH, 2], F32)
-                nc.vector.tensor_copy(out=region_f[:].rearrange("p b h -> p (b h)"), in_=region_int[:, 0 : 2 * BATCH])
-                nc.vector.tensor_tensor(out=row_f[:], in0=row_f[:], in1=region_f[:], op=ALU.add)
-                nc.vector.tensor_copy(out=row_index[:], in_=row_f[:])
-
         result = const.tile([P, BATCH, CHUNKS, PROPOSALS], F32)
 
-        with tc.tile_pool(name="work", bufs=2) as work_pool, tc.tile_pool(name="turned", bufs=3) as turned_pool, tc.tile_pool(name="fetch", bufs=4) as fetch_pool, tc.tile_pool(
-            name="operands", bufs=2
-        ) as operand_pool, tc.tile_pool(name="norm", bufs=2) as norm_pool, tc.psum_pool(name="table_psum", bufs=3) as table_psum, tc.psum_pool(
-            name="small_psum", bufs=1
-        ) as small_psum, tc.psum_pool(name="product_psum", bufs=CHUNKS) as product_psum:
+        with tc.tile_pool(name="turned", bufs=3) as turned_pool, tc.tile_pool(name="fetch", bufs=3) as fetch_pool, tc.tile_pool(
+            name="merge", bufs=2
+        ) as merge_pool, tc.tile_pool(name="operands", bufs=2) as operand_pool, tc.tile_pool(name="norm", bufs=2) as norm_pool, tc.psum_pool(
+            name="table_psum", bufs=3
+        ) as table_psum, tc.psum_pool(name="small_psum", bufs=1) as small_psum, tc.psum_pool(name="product_psum", bufs=CHUNKS) as product_psum:
 
-            def weave(b):
-                nc.scalar.copy(out=table_ring[b % RING][:, :, 0:FRAMES, :], in_=raw_of[b][:].rearrange("p h j t -> p h t j"))
-
-            def build(b):
-                table = table_ring[b % RING]
-                turned = [turned_pool.tile([P, TABLE_TILES, HALF], BF16, name="turned%d" % half) for half in range(2)]
-
-                def write(half, partitions, tiles):
-                    place = (2 * b + half) % REGIONS
-                    region = flat_out[place * REGION_ROWS * ROW_WORDS : (place + 1) * REGION_ROWS * ROW_WORDS].rearrange(
-                        "(p a w) -> p a w", p=P, w=ROW_WORDS
+            def weave(i):
+                frames = frames_ring[i % 3]
+                for b in range(2):
+                    nc.scalar.copy(
+                        out=frames[:, b].rearrange("p (r q) j -> p r q j", r=2), in_=raw_of[i][:, b].rearrange("p (j q r) -> p r q j", j=PACK, r=2)
                     )
-                    words = turned[half][:].rearrange("p a c -> p (a c)").bitcast(F32).rearrange("p (a w) -> p a w", w=ROW_WORDS)
-                    nc.sync.dma_start(out=region[partitions, tiles, :], in_=words[partitions, tiles, :])
 
-                emptied_banks = set()
+            def turn(level, b, zone, turned):
+                words = level.rearrange("p e j -> p (e j)").bitcast(F32)
+                landing = table_psum.tile([P, 2, 2, P], F32, name="landing")
+                for a in range(2):
+                    for k in range(2):
+                        nc.tensor.transpose(landing[:, a, k, :], words[:, 2 * P * a + k : 2 * P * a + k + 2 * P - 1 : 2], identity_words[:])
+                nc.scalar.copy(
+                    out=turned[:, :, b].rearrange("p h (x m) -> p h x m", x=4),
+                    in_=landing[:].rearrange("p a k (h m) -> p h (a k) m", h=2),
+                )
 
-                def emptied(half, bank):
-                    emptied_banks.add((half, bank))
-                    if bank < EARLY_BANKS and all((half, other) in emptied_banks for other in range(EARLY_BANKS)):
-                        write(half, slice(0, P), slice(0, BANK_TILES * EARLY_BANKS))
-                    if bank == (TABLE_TILES - 1) // BANK_TILES:
-                        write(half, slice(0, P), slice(BANK_TILES * EARLY_BANKS, TABLE_TILES))
+            def build(i):
+                frames = frames_ring[i % 3]
+                run8 = run8_ring[i % 2]
+                run64 = run64_ring[i % 2]
+                turned = [turned_pool.tile([P, 2, 2, 2 * ROW_WORDS], F32, name="turned%d" % zone) for zone in range(ZONES)]
+                half = FRAMES // 2
 
-                landings = {}
+                def larger(result_view, one, other):
+                    nc.vector.tensor_tensor(out=result_view, in0=one, in1=other, op=ALU.max)
 
-                def turn(half, a):
-                    bank = a // BANK_TILES
-                    if a % BANK_TILES == 0:
-                        landings[(half, bank)] = table_psum.tile([P, BANK_TILES, P], F32, name="landing")
-                    landing = landings[(half, bank)]
-                    nc.tensor.transpose(
-                        landing[:, a % BANK_TILES, :],
-                        table[:, half, P * a : P * (a + 1), :].rearrange("p e j -> p (e j)").bitcast(F32),
-                        identity_words[:],
-                    )
-                    if (a % BANK_TILES == BANK_TILES - 1 or a == TABLE_TILES - 1) and (half, bank) not in VECTOR_BANKS:
-                        nc.scalar.copy(
-                            out=turned[half][:, BANK_TILES * bank : a + 1, :].rearrange("p a c -> p (a c)").bitcast(F32),
-                            in_=landing[:, 0 : a % BANK_TILES + 1, :].rearrange("p a m -> p (a m)"),
+                for b in range(2):
+                    turn(frames[:, b], b, 0, turned[0])
+                larger(run2[:, :, 0:half], frames[:, :, 0:half], frames[:, :, half:FRAMES])
+                larger(run2[:, :, half:FRAMES], frames[:, :, half:FRAMES], frames[:, :, 1 : half + 1])
+                larger(run4[:, :, 0, 0 : half - 1], run2[:, :, 0 : half - 1], run2[:, :, 1:half])
+                larger(run4[:, :, 1, 0 : half - 2], run2[:, :, half : FRAMES - 2], run2[:, :, half + 1 : FRAMES - 1])
+                for b in range(2):
+                    for r in range(2):
+                        larger(
+                            run8[:, b].rearrange("p (g r q) j -> p r g q j", r=2, q=16)[:, r],
+                            run4[:, b, r, 0:half].rearrange("p (q g) j -> p g q j", g=8),
+                            run4[:, b, r, 2 : half + 2].rearrange("p (q g) j -> p g q j", g=8),
                         )
-                        emptied(half, bank)
+                for b in range(2):
+                    larger(run16[:, b, 0:half], run8[:, b, 0:half], run8[:, b, half:FRAMES])
+                    larger(run16[:, b, half:FRAMES], run8[:, b, half:FRAMES], run8[:, b, 1 : half + 1])
+                for b in range(2):
+                    turn(run8[:, b], b, 1, turned[1])
+                for b in range(2):
+                    larger(run32[:, b, 0:FRAMES], run16[:, b, 0:FRAMES], run16[:, b, 1 : FRAMES + 1])
+                for b in range(2):
+                    for r in range(2):
+                        larger(
+                            run64[:, b].rearrange("p (g r k) j -> p r g k j", r=2, k=16)[:, r],
+                            run32[:, b, half * r : half * (r + 1)].rearrange("p (k g) j -> p g k j", g=8),
+                            run32[:, b, half * r + 2 : half * (r + 1) + 2].rearrange("p (k g) j -> p g k j", g=8),
+                        )
+                for b in range(2):
+                    turn(run64[:, b], b, 2, turned[2])
+                return turned
 
-                pieces = {2 * piece + 1: (half, bank, piece) for half, bank in VECTOR_BANKS for piece in range(2)}
-                turned_tiles = 0
-                for k in range(LEVELS):
-                    if k > 0:
-                        lower = level_start[k - 1]
-                        if RUNS[k] == 2 * RUNS[k - 1]:
-                            longer = None
-                        else:
-                            longer = work_pool.tile([P, 2, FRAMES, 2], BF16, name="longer")
-                            for half in range(2):
-                                nc.vector.tensor_tensor(
-                                    out=longer[:, half, 0 : level_size[k - 1] - 1, :],
-                                    in0=table[:, half, lower : lower + level_size[k - 1] - 1, :],
-                                    in1=table[:, half, lower + 1 : lower + level_size[k - 1], :],
-                                    op=ALU.max,
-                                )
-                        width = level_size[k]
-                        further = RUNS[k] - RUNS[k - 1]
-                        for half in range(2):
-                            nc.vector.tensor_tensor(
-                                out=table[:, half, level_start[k] : level_start[k] + width, :],
-                                in0=table[:, half, lower : lower + width, :] if longer is None else longer[:, half, 0:width, :],
-                                in1=table[:, half, lower + further : lower + further + width, :],
-                                op=ALU.max,
-                            )
-                        if k in pieces:
-                            half, bank, piece = pieces[k]
-                            two = slice(2 * piece, 2 * piece + 2)
-                            nc.vector.tensor_copy(
-                                out=turned[half][:, BANK_TILES * bank + 2 * piece : BANK_TILES * bank + 2 * piece + 2, :].rearrange("p a c -> p (a c)"),
-                                in_=landings[(half, bank)][:, two, :].rearrange("p a m -> p (a m)").bitcast(BF16),
-                            )
-                            if piece == 1:
-                                emptied(half, bank)
-                    built = level_start[k] + level_size[k] if k < LEVELS - 1 else ENTRIES
-                    while turned_tiles < TABLE_TILES and P * (turned_tiles + 1) <= built:
-                        for half in range(2):
-                            turn(half, turned_tiles)
-                        turned_tiles += 1
-
-            def fetch(b, fetched):
+            def publish(i, turned, fetched):
                 for half in range(2):
-                    nc.gpsimd.indirect_dma_start(
-                        out=fetched[:, b % 2, ROW_WORDS * half : ROW_WORDS * (half + 1)],
-                        out_offset=None,
-                        in_=out_rows[0 : ((2 * b + half) % REGIONS + 1) * REGION_ROWS, :],
-                        in_offset=bass.IndirectOffsetOnAxis(ap=row_index[:, b, half : half + 1], axis=0),
-                    )
+                    unit = (2 * i + half) % UNITS
+                    rows = out_rows[unit * UNIT_PITCH : unit * UNIT_PITCH + UNIT_ROWS].rearrange("(b z p a) w -> z p b (a w)", b=2, z=ZONES, p=P)
+                    for zone in range(ZONES):
+                        nc.sync.dma_start(out=rows[zone], in_=turned[zone][:, half])
+                    for end in range(2):
+                        nc.gpsimd.indirect_dma_start(
+                            out=fetched[:, half, end, :],
+                            out_offset=None,
+                            in_=out_rows[0 : (unit + 1) * UNIT_PITCH, :],
+                            in_offset=bass.IndirectOffsetOnAxis(ap=row_index[:, i, half, end : end + 1], axis=0),
+                        )
 
-            def pool_pair(b, fetched, pooled, place):
-                values = fetch_pool.tile([P, 2, CHANNELS], BF16, name="values")
-                nc.vector.tensor_copy(out=values[:].rearrange("p i c -> p (i c)"), in_=fetched[:].rearrange("p i w -> p (i w)").bitcast(BF16))
-                back = small_psum.tile([P, 2, PACK, P], BF16, name="back", tag="small")
-                for i in range(2):
-                    for t in range(PACK):
-                        nc.tensor.transpose(back[:, i, t, :], values[:, i, t : t + PACK * (P - 1) + 1 : PACK], identity[:])
-                second = fetch_pool.tile([P, 2, PROPOSALS, PACK], BF16, name="second")
-                nc.scalar.copy(out=second[:], in_=back[:, :, :, PROPOSALS : 2 * PROPOSALS].rearrange("p i t n -> p i n t"))
-                nc.vector.tensor_tensor(
-                    out=pooled[:, place : place + 2, :, :],
-                    in0=back[:, :, :, 0:PROPOSALS].rearrange("p i t n -> p i n t"),
-                    in1=second[:],
-                    op=ALU.max,
+            def merge(i, fetched, pooled, place):
+                runs = merge_pool.tile([P, 2, SLOTS, HALF], BF16, name="runs")
+                twos = merge_pool.tile([P, 2, 2, HALF], BF16, name="twos")
+                values = merge_pool.tile([P, 2, 2, HALF // 2], BF16, name="values")
+                for half in range(2):
+                    nc.vector.tensor_tensor(
+                        out=runs[:, half].rearrange("p s c -> p (s c)"), in0=fetched[:, half, 0].bitcast(BF16), in1=fetched[:, half, 1].bitcast(BF16), op=ALU.max
+                    )
+                for half in range(2):
+                    full = filled[:, i, half : half + 1]
+                    nc.vector.tensor_scalar(out=runs[:, half, 0, :], in0=runs[:, half, 0, :], scalar1=full, scalar2=None, op0=ALU.mult)
+                    for slot in range(1, SLOTS):
+                        nc.vector.tensor_scalar(
+                            out=runs[:, half, slot, :], in0=runs[:, half, slot, :], scalar1=slot_limit[:, i, half, slot - 1 : slot], scalar2=full,
+                            op0=ALU.min, op1=ALU.mult,
+                        )
+                for half in range(2):
+                    nc.vector.tensor_tensor(out=twos[:, half], in0=runs[:, half, 0:2, :], in1=runs[:, half, 2:4, :], op=ALU.max)
+                for half in range(2):
+                    nc.vector.tensor_tensor(
+                        out=values[:, :, half, :],
+                        in0=twos[:, half, 0, :].rearrange("p (k c) -> p k c", k=2),
+                        in1=twos[:, half, 1, :].rearrange("p (k c) -> p k c", k=2),
+                        op=ALU.max,
+                    )
+                flat = values[:].rearrange("p k h c -> p (k h c)")
+                back = small_psum.tile([P, PACK, P], BF16, name="back", tag="small")
+                for t in range(PACK):
+                    first = HALF * (t // 2) + t % 2
+                    nc.tensor.transpose(back[:, t, :], flat[:, first : first + HALF - 1 : 2], identity[:])
+                nc.scalar.copy(
+                    out=pooled[:, place : place + 2, :, :].rearrange("p b n t -> p (b n) t"), in_=back[:].rearrange("p t c -> p c t")
                 )
 
             def finish_round(first_batch, count, pooled):
@@ -371,13 +380,13 @@ def tile_coarsepyramid_pb_kernel(
                     in1=group_mean[:].unsqueeze(1).to_broadcast([P, CHUNKS, count]),
                     op=ALU.subtract,
                 )
-                squares = norm_pool.tile([P, stats, PROPOSALS], F32, name="squares")
                 row_squares = norm_pool.tile([P, stats], F32, name="row_squares")
                 for q in range(CHUNKS):
+                    squares = norm_pool.tile([P, count, PROPOSALS], F32, name="squares")
                     for i in range(count):
                         s = count * q + i
                         nc.scalar.activation(
-                            out=squares[:, s, :], in_=products[q][:, i, :], func=ACT.Square, bias=to_centre[:, q, i : i + 1], scale=1.0,
+                            out=squares[:, i, :], in_=products[q][:, i, :], func=ACT.Square, bias=to_centre[:, q, i : i + 1], scale=1.0,
                             accum_out=row_squares[:, s : s + 1],
                         )
                 var_parts = small_psum.tile([P, CHUNKS, count], F32, name="var_parts", tag="small")
@@ -411,32 +420,30 @@ def tile_coarsepyramid_pb_kernel(
             for first_batch, count in rounds:
                 for b in range(first_batch, first_batch + count):
                     round_of[b] = (first_batch, count)
-            FETCH_LAG = 1
-            POOL_LAG = 3
+            MERGE_LAG = 2
             fetched_of = {}
             pooled_of = {}
+            load(1)
             weave(0)
-            for i in range(BATCH + POOL_LAG):
-                if i + 2 < BATCH:
+            for i in range(PAIRS + MERGE_LAG):
+                if i + 2 < PAIRS:
                     load(i + 2)
-                b = i - FETCH_LAG
-                if 0 <= b < BATCH:
-                    if b % 2 == 0:
-                        fetched_of[b // 2] = fetch_pool.tile([P, 2, 2 * ROW_WORDS], F32, name="fetched")
-                    fetch(b, fetched_of[b // 2])
-                if i < BATCH:
-                    build(i)
-                if i + 1 < BATCH:
-                    weave(i + 1)
+                if i < PAIRS:
+                    turned = build(i)
                 if i == 0:
                     prepare()
-                b = i - POOL_LAG
-                if b >= 0 and b % 2 == 1:
-                    first_batch, count = round_of[b]
-                    if b - 1 == first_batch:
+                if i < PAIRS:
+                    fetched_of[i] = fetch_pool.tile([P, 2, 2, SLOTS * ROW_WORDS], F32, name="fetched")
+                    publish(i, turned, fetched_of[i])
+                if i + 1 < PAIRS:
+                    weave(i + 1)
+                done = i - MERGE_LAG
+                if done >= 0:
+                    first_batch, count = round_of[2 * done]
+                    if 2 * done == first_batch:
                         pooled_of[first_batch] = operand_pool.tile([P, count, PROPOSALS, PACK], BF16, align_bytes=64, name="pooled")
-                    pool_pair(b - 1, fetched_of[b // 2], pooled_of[first_batch], b - 1 - first_batch)
-                    if b == first_batch + count - 1:
+                    merge(done, fetched_of[done], pooled_of[first_batch], 2 * done - first_batch)
+                    if 2 * done + 2 == first_batch + count:
                         finish_round(first_batch, count, pooled_of[first_batch])
 
             for first_batch, count in rounds:

@@ -98,11 +98,9 @@ def tile_coarsepyramid_pb_kernel(
         run4 = const.tile([P, 2, 2, FRAMES // 2 + PAD, PACK], BF16)
         run8_ring = [const.tile([P, 2, FRAMES, PACK], BF16, name="run8_%d" % s) for s in range(2)]
         run16 = const.tile([P, 2, FRAMES + PAD, PACK], BF16)
-        run32 = const.tile([P, 2, FRAMES + PAD, PACK], BF16)
-        run64_ring = [const.tile([P, 2, FRAMES, PACK], BF16, name="run64_%d" % s) for s in range(2)]
+        run32_ring = [const.tile([P, 2, FRAMES, PACK], BF16, name="run32_%d" % s) for s in range(2)]
         nc.vector.memset(run4[:, :, :, FRAMES // 2 - 2 : FRAMES // 2 + PAD, :], 0.0)
         nc.vector.memset(run16[:, :, FRAMES : FRAMES + PAD, :], 0.0)
-        nc.vector.memset(run32[:, :, FRAMES : FRAMES + PAD, :], 0.0)
 
         w_sorted = const.tile([P, CHANNELS], U32, align_bytes=64)
         s_sorted = const.tile([P, CHANNELS], U8, align_bytes=64)
@@ -114,7 +112,8 @@ def tile_coarsepyramid_pb_kernel(
         eps_col = const.tile([P, 1], F32)
         row_index = const.tile([P, PAIRS, 2, 2], I32)
         filled = const.tile([P, PAIRS, 2], F32)
-        slot_limit = const.tile([P, PAIRS, 2, SLOTS - 1], F32)
+        slot_scale = const.tile([P, PAIRS, 2, SLOTS], F32)
+        slot_bias = const.tile([P, PAIRS, 2, SLOTS], F32)
 
         column_group = const.tile([P, P], I32)
         partition_index = const.tile([P, 1], I32)
@@ -163,22 +162,24 @@ def tile_coarsepyramid_pb_kernel(
                 ts(out=level2[:], in0=span[:], scalar1=64.0, scalar2=None, op0=ALU.is_ge)
                 run = setup.tile(shape, F32, name="run")
                 ts(out=run[:], in0=level1[:], scalar1=7.0, scalar2=1.0, op0=ALU.mult, op1=ALU.add)
-                nc.vector.scalar_tensor_tensor(out=run[:], in0=level2[:], scalar=56.0, in1=run[:], op0=ALU.mult, op1=ALU.add)
+                nc.vector.scalar_tensor_tensor(out=run[:], in0=level2[:], scalar=24.0, in1=run[:], op0=ALU.mult, op1=ALU.add)
                 span_int = setup.tile(shape, I32, name="span_int")
                 nc.vector.tensor_copy(out=span_int[:], in_=span[:])
                 more = whole_of(1, span_int, shape, "more")
                 more1 = whole_of(4, span_int, shape, "more1")
-                more2 = whole_of(7, span_int, shape, "more2")
+                more2 = whole_of(6, span_int, shape, "more2")
                 tt(out=more2[:], in0=more2[:], in1=more1[:], op=ALU.subtract)
                 tt(out=more1[:], in0=more1[:], in1=more[:], op=ALU.subtract)
                 tt(out=more1[:], in0=more1[:], in1=level1[:], op=ALU.mult)
                 tt(out=more2[:], in0=more2[:], in1=level2[:], op=ALU.mult)
                 tt(out=more[:], in0=more[:], in1=more1[:], op=ALU.add)
                 tt(out=more[:], in0=more[:], in1=more2[:], op=ALU.add)
-                for slot in range(1, SLOTS):
-                    limit = slot_limit[:, :, :, slot - 1]
-                    ts(out=limit, in0=more[:], scalar1=float(slot), scalar2=2.0, op0=ALU.is_ge, op1=ALU.mult)
-                    ts(out=limit, in0=limit, scalar1=1.0, scalar2=LARGEST, op0=ALU.subtract, op1=ALU.mult)
+                for slot in range(SLOTS):
+                    scale = slot_scale[:, :, :, slot]
+                    ts(out=scale, in0=more[:], scalar1=float(slot), scalar2=None, op0=ALU.is_ge)
+                    tt(out=scale, in0=scale, in1=filled[:], op=ALU.mult)
+                    tt(out=slot_bias[:, :, :, slot], in0=scale, in1=filled[:], op=ALU.subtract)
+                    ts(out=slot_bias[:, :, :, slot], in0=slot_bias[:, :, :, slot], scalar1=LARGEST, scalar2=None, op0=ALU.mult)
                 tt(out=more[:], in0=more[:], in1=run[:], op=ALU.mult)
                 tt(out=more[:], in0=more[:], in1=run[:], op=ALU.add)
                 nc.vector.scalar_tensor_tensor(out=start[:, 1], in0=start[:, 1], scalar=1.0, in1=more[:], op0=ALU.add, op1=ALU.subtract)
@@ -186,16 +187,16 @@ def tile_coarsepyramid_pb_kernel(
                 nc.vector.tensor_copy(out=start_int[:], in_=start[:])
                 eighth = whole_of(3, start_int, both, "eighth")
                 ts(out=eighth[:], in0=eighth[:], scalar1=float(1 - 32 * 8), scalar2=float(ZONE_ROWS), op0=ALU.mult, op1=ALU.add)
-                sixty_fourth = whole_of(6, start_int, both, "sixty_fourth")
-                ts(out=sixty_fourth[:], in0=sixty_fourth[:], scalar1=float(1 - 4 * 64), scalar2=float(2 * ZONE_ROWS), op0=ALU.mult, op1=ALU.add)
-                tt(out=sixty_fourth[:], in0=sixty_fourth[:], in1=eighth[:], op=ALU.subtract)
+                thirty_second = whole_of(5, start_int, both, "thirty_second")
+                ts(out=thirty_second[:], in0=thirty_second[:], scalar1=float(1 - 8 * 32), scalar2=float(2 * ZONE_ROWS), op0=ALU.mult, op1=ALU.add)
+                tt(out=thirty_second[:], in0=thirty_second[:], in1=eighth[:], op=ALU.subtract)
                 nc.vector.scalar_tensor_tensor(out=eighth[:], in0=start[:], scalar=31.0, in1=eighth[:], op0=ALU.mult, op1=ALU.add)
-                nc.vector.scalar_tensor_tensor(out=sixty_fourth[:], in0=start[:], scalar=-28.0, in1=sixty_fourth[:], op0=ALU.mult, op1=ALU.add)
+                nc.vector.scalar_tensor_tensor(out=thirty_second[:], in0=start[:], scalar=-24.0, in1=thirty_second[:], op0=ALU.mult, op1=ALU.add)
                 for end in range(2):
                     tt(out=eighth[:, end], in0=eighth[:, end], in1=level1[:], op=ALU.mult)
-                    tt(out=sixty_fourth[:, end], in0=sixty_fourth[:, end], in1=level2[:], op=ALU.mult)
+                    tt(out=thirty_second[:, end], in0=thirty_second[:, end], in1=level2[:], op=ALU.mult)
                 tt(out=start[:], in0=start[:], in1=eighth[:], op=ALU.add)
-                tt(out=start[:], in0=start[:], in1=sixty_fourth[:], op=ALU.add)
+                tt(out=start[:], in0=start[:], in1=thirty_second[:], op=ALU.add)
                 cycles = (2 * PAIRS + UNITS - 1) // UNITS
                 unit_int = setup.tile([P, cycles * UNITS], I32, name="unit_int")
                 nc.gpsimd.iota(unit_int[:], pattern=[[0, cycles], [UNIT_PITCH, UNITS]], base=0, channel_multiplier=0)
@@ -260,7 +261,7 @@ def tile_coarsepyramid_pb_kernel(
             def build(i):
                 frames = frames_ring[i % 3]
                 run8 = run8_ring[i % 2]
-                run64 = run64_ring[i % 2]
+                run32 = run32_ring[i % 2]
                 turned = [turned_pool.tile([P, 2, 2, 2 * ROW_WORDS], F32, name="turned%d" % zone) for zone in range(ZONES)]
                 half = FRAMES // 2
 
@@ -286,16 +287,14 @@ def tile_coarsepyramid_pb_kernel(
                 for b in range(2):
                     turn(run8[:, b], b, 1, turned[1])
                 for b in range(2):
-                    larger(run32[:, b, 0:FRAMES], run16[:, b, 0:FRAMES], run16[:, b, 1 : FRAMES + 1])
-                for b in range(2):
-                    for r in range(2):
+                    for part in range(2):
                         larger(
-                            run64[:, b].rearrange("p (g r k) j -> p r g k j", r=2, k=16)[:, r],
-                            run32[:, b, half * r : half * (r + 1)].rearrange("p (k g) j -> p g k j", g=8),
-                            run32[:, b, half * r + 2 : half * (r + 1) + 2].rearrange("p (k g) j -> p g k j", g=8),
+                            run32[:, b].rearrange("p (g r x) j -> p r g x j", r=2, x=32)[:, part],
+                            run16[:, b, half * part : half * (part + 1)].rearrange("p (x g) j -> p g x j", g=4),
+                            run16[:, b, half * part + 1 : half * (part + 1) + 1].rearrange("p (x g) j -> p g x j", g=4),
                         )
                 for b in range(2):
-                    turn(run64[:, b], b, 2, turned[2])
+                    turn(run32[:, b], b, 2, turned[2])
                 return turned
 
             def publish(i, turned, fetched):
@@ -314,6 +313,7 @@ def tile_coarsepyramid_pb_kernel(
 
             def merge(i, fetched, pooled, place):
                 runs = merge_pool.tile([P, 2, SLOTS, HALF], BF16, name="runs")
+                counted = merge_pool.tile([P, 2, SLOTS, HALF], BF16, name="counted")
                 twos = merge_pool.tile([P, 2, 2, HALF], BF16, name="twos")
                 values = merge_pool.tile([P, 2, 2, HALF // 2], BF16, name="values")
                 for half in range(2):
@@ -321,15 +321,13 @@ def tile_coarsepyramid_pb_kernel(
                         out=runs[:, half].rearrange("p s c -> p (s c)"), in0=fetched[:, half, 0].bitcast(BF16), in1=fetched[:, half, 1].bitcast(BF16), op=ALU.max
                     )
                 for half in range(2):
-                    full = filled[:, i, half : half + 1]
-                    nc.vector.tensor_scalar(out=runs[:, half, 0, :], in0=runs[:, half, 0, :], scalar1=full, scalar2=None, op0=ALU.mult)
-                    for slot in range(1, SLOTS):
-                        nc.vector.tensor_scalar(
-                            out=runs[:, half, slot, :], in0=runs[:, half, slot, :], scalar1=slot_limit[:, i, half, slot - 1 : slot], scalar2=full,
-                            op0=ALU.min, op1=ALU.mult,
+                    for slot in range(SLOTS):
+                        nc.scalar.activation(
+                            out=counted[:, half, slot, :], in_=runs[:, half, slot, :], func=ACT.Identity,
+                            scale=slot_scale[:, i, half, slot : slot + 1], bias=slot_bias[:, i, half, slot : slot + 1],
                         )
                 for half in range(2):
-                    nc.vector.tensor_tensor(out=twos[:, half], in0=runs[:, half, 0:2, :], in1=runs[:, half, 2:4, :], op=ALU.max)
+                    nc.vector.tensor_tensor(out=twos[:, half], in0=counted[:, half, 0:2, :], in1=counted[:, half, 2:4, :], op=ALU.max)
                 for half in range(2):
                     nc.vector.tensor_tensor(
                         out=values[:, :, half, :],

@@ -54,7 +54,11 @@ def tile_coarsepyramid_pb_kernel(
 
         def load(i):
             raw = raw_pool.tile([P, 2, PACK * FRAMES], BF16, name="raw")
-            nc.sync.dma_start(out=raw[:], in_=frame_level_feature[2 * i : 2 * i + 2].rearrange("b (m j) t -> m b (j t)", j=PACK))
+            for half in range(2):
+                nc.sync.dma_start(
+                    out=raw[:, :, half * 2 * FRAMES : (half + 1) * 2 * FRAMES],
+                    in_=frame_level_feature[2 * i : 2 * i + 2, HALF * half : HALF * (half + 1)].rearrange("b (m j) t -> m b (j t)", j=2),
+                )
             raw_of[i] = raw
 
         load(0)
@@ -93,14 +97,9 @@ def tile_coarsepyramid_pb_kernel(
             in_=zeros[:],
         )
 
-        frames_ring = [const.tile([P, 2, FRAMES, PACK], BF16, name="frames%d" % s) for s in range(3)]
-        run2 = const.tile([P, 2, FRAMES, PACK], BF16)
-        run4 = const.tile([P, 2, 2, FRAMES // 2 + PAD, PACK], BF16)
-        run8_ring = [const.tile([P, 2, FRAMES, PACK], BF16, name="run8_%d" % s) for s in range(2)]
-        run16 = const.tile([P, 2, FRAMES + PAD, PACK], BF16)
-        run32_ring = [const.tile([P, 2, FRAMES, PACK], BF16, name="run32_%d" % s) for s in range(2)]
-        nc.vector.memset(run4[:, :, :, FRAMES // 2 - 2 : FRAMES // 2 + PAD, :], 0.0)
-        nc.vector.memset(run16[:, :, FRAMES : FRAMES + PAD, :], 0.0)
+        run2_ring = [const.tile([P, 2, FRAMES // 2 + PAD, PACK], BF16, name="run2_%d" % s) for s in range(2)]
+        for run2 in run2_ring:
+            nc.vector.memset(run2[:, :, FRAMES // 2 : FRAMES // 2 + PAD, :], 0.0)
 
         w_sorted = const.tile([P, CHANNELS], U32, align_bytes=64)
         s_sorted = const.tile([P, CHANNELS], U8, align_bytes=64)
@@ -234,75 +233,100 @@ def tile_coarsepyramid_pb_kernel(
 
         result = const.tile([P, BATCH, CHUNKS, PROPOSALS], F32)
 
-        with tc.tile_pool(name="turned", bufs=3) as turned_pool, tc.tile_pool(name="fetch", bufs=3) as fetch_pool, tc.tile_pool(
+        with tc.tile_pool(name="turned", bufs=3) as turned_pool, tc.tile_pool(name="step", bufs=3) as step_pool, tc.tile_pool(name="fetch", bufs=4) as fetch_pool, tc.tile_pool(
             name="merge", bufs=2
         ) as merge_pool, tc.tile_pool(name="operands", bufs=2) as operand_pool, tc.tile_pool(name="norm", bufs=2) as norm_pool, tc.psum_pool(
             name="table_psum", bufs=3
         ) as table_psum, tc.psum_pool(name="small_psum", bufs=1) as small_psum, tc.psum_pool(name="product_psum", bufs=CHUNKS) as product_psum:
 
-            def weave(i):
-                frames = frames_ring[i % 3]
-                for b in range(2):
-                    nc.scalar.copy(
-                        out=frames[:, b].rearrange("p (r q) j -> p r q j", r=2), in_=raw_of[i][:, b].rearrange("p (j q r) -> p r q j", j=PACK, r=2)
-                    )
+            frames_of, run4_of, run16_of, turned_of = {}, {}, {}, {}
 
-            def turn(level, b, zone, turned):
-                words = level.rearrange("p e j -> p (e j)").bitcast(F32)
+            def weave(b):
+                frames = step_pool.tile([P, FRAMES, PACK], BF16, name="frames")
+                nc.scalar.copy(
+                    out=frames[:].rearrange("p (r q) c -> p r q c", r=2), in_=raw_of[b // 2][:, b % 2].rearrange("p (c q r) -> p r q c", c=PACK, r=2)
+                )
+                frames_of[b] = frames
+
+            def turn(words, first):
                 landing = table_psum.tile([P, 2, 2, P], F32, name="landing")
                 for a in range(2):
-                    for k in range(2):
-                        nc.tensor.transpose(landing[:, a, k, :], words[:, 2 * P * a + k : 2 * P * a + k + 2 * P - 1 : 2], identity_words[:])
+                    for half in range(2):
+                        nc.tensor.transpose(landing[:, a, half, :], words(half, first + P * a), identity_words[:])
+                return landing
+
+            def side_by_side(level):
+                words = level.rearrange("p e c -> p (e c)").bitcast(F32)
+                return lambda half, first: words[:, 2 * first + half : 2 * first + half + 2 * P - 1 : 2]
+
+            def swapped(view):
+                return view.rearrange("p x y m -> p y x m")
+
+            def larger(result_view, one, other):
+                nc.vector.tensor_tensor(out=result_view, in0=one, in1=other, op=ALU.max)
+
+            def first_level(b):
+                if b % 2 == 0:
+                    turned_of[b // 2] = [turned_pool.tile([P, 2, 2, 2, ROW_WORDS], F32, name="turned%d" % zone) for zone in range(ZONES)]
+                frames = frames_of[b]
+                landing = turn(side_by_side(frames[:]), 0)
+                nc.scalar.copy(out=turned_of[b // 2][0][:, :, b % 2], in_=swapped(landing[:]))
+                run2 = run2_ring[b % 2]
+                many = FRAMES // 2
+                larger(run2[:, 0, 0:many], frames[:, 0:many], frames[:, many:FRAMES])
+                larger(run2[:, 1, 0:many], frames[:, many:FRAMES], frames[:, 1 : many + 1])
+                run4 = step_pool.tile([P, FRAMES + 64, PACK], BF16, name="run4")
+                for r in range(2):
+                    larger(
+                        run4[:, 0:FRAMES].rearrange("p (g r q) c -> p r g q c", r=2, q=16)[:, r],
+                        run2[:, r, 0:many].rearrange("p (q g) c -> p g q c", g=8),
+                        run2[:, r, 1 : many + 1].rearrange("p (q g) c -> p g q c", g=8),
+                    )
+                words = run4[:].rearrange("p e c -> p (e c)").bitcast(F32)
+                nc.scalar.copy(out=words[:, 2 * FRAMES : 2 * FRAMES + 128], in_=words[:, 2 : 2 + 128])
+                run4_of[b] = run4
+
+            def turned_maximum(words, b, zone):
+                landing = turn(words, 0)
+                shifted = turn(words, 64)
+                here = step_pool.tile([P, 2, 2, P], F32, name="here")
+                nc.scalar.copy(out=here[:], in_=landing[:])
+                larger(swapped(turned_of[b // 2][zone][:, :, b % 2].bitcast(BF16)), shifted[:].bitcast(BF16), here[:].bitcast(BF16))
+
+            def second_level(b):
+                turned_maximum(side_by_side(run4_of[b][:]), b, 1)
+
+            def back_again(b):
+                back8 = table_psum.tile([P, 2, 2, P], F32, name="landing")
+                for half in range(2):
+                    for a in range(2):
+                        nc.tensor.transpose(back8[:, half, a, :], turned_of[b // 2][1][:, half, b % 2, a, :], identity_words[:])
+                ordered = back8[:].rearrange("p h a e -> p h (a e)")
+                run8 = step_pool.tile([P, 2, FRAMES + 32], F32, name="run8")
                 nc.scalar.copy(
-                    out=turned[:, :, b].rearrange("p h (x m) -> p h x m", x=4),
-                    in_=landing[:].rearrange("p a k (h m) -> p h (a k) m", h=2),
+                    out=run8[:, :, 0:FRAMES].rearrange("p h (g x) -> p h g x", g=4), in_=ordered.rearrange("p h (x g) -> p h g x", g=4)
                 )
+                nc.scalar.copy(out=run8[:, :, FRAMES : FRAMES + 32], in_=ordered[:, :, 4 : 4 * 32 + 1 : 4])
+                run16 = step_pool.tile([P, 2, FRAMES + 64], F32, name="run16")
+                for half in range(2):
+                    larger(
+                        run16[:, half, 0:FRAMES].bitcast(BF16).rearrange("p (g x j) -> p g x j", g=4, j=2),
+                        back8[:, half].rearrange("p a e -> p (a e)").bitcast(BF16).rearrange("p (x g j) -> p g x j", g=4, j=2),
+                        run8[:, half, 32 : FRAMES + 32].bitcast(BF16).rearrange("p (g x j) -> p g x j", g=4, j=2),
+                    )
+                nc.scalar.copy(out=run16[:, :, FRAMES : FRAMES + 64], in_=run16[:, :, 1 : 1 + 64])
+                run16_of[b] = run16
 
-            def build(i):
-                frames = frames_ring[i % 3]
-                run8 = run8_ring[i % 2]
-                run32 = run32_ring[i % 2]
-                turned = [turned_pool.tile([P, 2, 2, 2 * ROW_WORDS], F32, name="turned%d" % zone) for zone in range(ZONES)]
-                half = FRAMES // 2
-
-                def larger(result_view, one, other):
-                    nc.vector.tensor_tensor(out=result_view, in0=one, in1=other, op=ALU.max)
-
-                for b in range(2):
-                    turn(frames[:, b], b, 0, turned[0])
-                larger(run2[:, :, 0:half], frames[:, :, 0:half], frames[:, :, half:FRAMES])
-                larger(run2[:, :, half:FRAMES], frames[:, :, half:FRAMES], frames[:, :, 1 : half + 1])
-                larger(run4[:, :, 0, 0 : half - 1], run2[:, :, 0 : half - 1], run2[:, :, 1:half])
-                larger(run4[:, :, 1, 0 : half - 2], run2[:, :, half : FRAMES - 2], run2[:, :, half + 1 : FRAMES - 1])
-                for b in range(2):
-                    for r in range(2):
-                        larger(
-                            run8[:, b].rearrange("p (g r q) j -> p r g q j", r=2, q=16)[:, r],
-                            run4[:, b, r, 0:half].rearrange("p (q g) j -> p g q j", g=8),
-                            run4[:, b, r, 2 : half + 2].rearrange("p (q g) j -> p g q j", g=8),
-                        )
-                for b in range(2):
-                    larger(run16[:, b, 0:half], run8[:, b, 0:half], run8[:, b, half:FRAMES])
-                    larger(run16[:, b, half:FRAMES], run8[:, b, half:FRAMES], run8[:, b, 1 : half + 1])
-                for b in range(2):
-                    turn(run8[:, b], b, 1, turned[1])
-                for b in range(2):
-                    for part in range(2):
-                        larger(
-                            run32[:, b].rearrange("p (g r x) j -> p r g x j", r=2, x=32)[:, part],
-                            run16[:, b, half * part : half * (part + 1)].rearrange("p (x g) j -> p g x j", g=4),
-                            run16[:, b, half * part + 1 : half * (part + 1) + 1].rearrange("p (x g) j -> p g x j", g=4),
-                        )
-                for b in range(2):
-                    turn(run32[:, b], b, 2, turned[2])
-                return turned
+            def third_level(b):
+                run16 = run16_of[b]
+                turned_maximum(lambda half, first: run16[:, half, first : first + P], b, 2)
 
             def publish(i, turned, fetched):
                 for half in range(2):
                     unit = (2 * i + half) % UNITS
                     rows = out_rows[unit * UNIT_PITCH : unit * UNIT_PITCH + UNIT_ROWS].rearrange("(b z p a) w -> z p b (a w)", b=2, z=ZONES, p=P)
                     for zone in range(ZONES):
-                        nc.sync.dma_start(out=rows[zone], in_=turned[zone][:, half])
+                        nc.sync.dma_start(out=rows[zone], in_=turned[zone][:, half].rearrange("p b a w -> p b (a w)"))
                     for end in range(2):
                         nc.gpsimd.indirect_dma_start(
                             out=fetched[:, half, end, :],
@@ -315,7 +339,7 @@ def tile_coarsepyramid_pb_kernel(
                 runs = merge_pool.tile([P, 2, SLOTS, HALF], BF16, name="runs")
                 counted = merge_pool.tile([P, 2, SLOTS, HALF], BF16, name="counted")
                 twos = merge_pool.tile([P, 2, 2, HALF], BF16, name="twos")
-                values = merge_pool.tile([P, 2, 2, HALF // 2], BF16, name="values")
+                values = merge_pool.tile([P, 2, HALF], BF16, name="values")
                 for half in range(2):
                     nc.vector.tensor_tensor(
                         out=runs[:, half].rearrange("p s c -> p (s c)"), in0=fetched[:, half, 0].bitcast(BF16), in1=fetched[:, half, 1].bitcast(BF16), op=ALU.max
@@ -329,17 +353,11 @@ def tile_coarsepyramid_pb_kernel(
                 for half in range(2):
                     nc.vector.tensor_tensor(out=twos[:, half], in0=counted[:, half, 0:2, :], in1=counted[:, half, 2:4, :], op=ALU.max)
                 for half in range(2):
-                    nc.vector.tensor_tensor(
-                        out=values[:, :, half, :],
-                        in0=twos[:, half, 0, :].rearrange("p (k c) -> p k c", k=2),
-                        in1=twos[:, half, 1, :].rearrange("p (k c) -> p k c", k=2),
-                        op=ALU.max,
-                    )
-                flat = values[:].rearrange("p k h c -> p (k h c)")
+                    nc.vector.tensor_tensor(out=values[:, half], in0=twos[:, half, 0, :], in1=twos[:, half, 1, :], op=ALU.max)
+                flat = values[:].rearrange("p h c -> p (h c)")
                 back = small_psum.tile([P, PACK, P], BF16, name="back", tag="small")
                 for t in range(PACK):
-                    first = HALF * (t // 2) + t % 2
-                    nc.tensor.transpose(back[:, t, :], flat[:, first : first + HALF - 1 : 2], identity[:])
+                    nc.tensor.transpose(back[:, t, :], flat[:, t : t + PACK * (P - 1) + 1 : PACK], identity[:])
                 nc.scalar.copy(
                     out=pooled[:, place : place + 2, :, :].rearrange("p b n t -> p (b n) t"), in_=back[:].rearrange("p t c -> p c t")
                 )
@@ -418,30 +436,37 @@ def tile_coarsepyramid_pb_kernel(
             for first_batch, count in rounds:
                 for b in range(first_batch, first_batch + count):
                     round_of[b] = (first_batch, count)
-            MERGE_LAG = 2
+            MERGE_LAG = 6
             fetched_of = {}
             pooled_of = {}
             load(1)
             weave(0)
-            for i in range(PAIRS + MERGE_LAG):
-                if i + 2 < PAIRS:
-                    load(i + 2)
-                if i < PAIRS:
-                    turned = build(i)
-                if i == 0:
+            for step in range(BATCH + 4 + MERGE_LAG):
+                if step % 2 == 0 and 4 <= step + 4 < BATCH:
+                    load(step // 2 + 2)
+                if 0 <= step - 3 < BATCH:
+                    third_level(step - 3)
+                if 0 <= step - 2 < BATCH:
+                    back_again(step - 2)
+                if 0 <= step - 1 < BATCH:
+                    second_level(step - 1)
+                if step < BATCH:
+                    first_level(step)
+                if step + 1 < BATCH:
+                    weave(step + 1)
+                if step == 1:
                     prepare()
-                if i < PAIRS:
+                if 0 <= step - 4 < BATCH and step % 2 == 0:
+                    i = (step - 4) // 2
                     fetched_of[i] = fetch_pool.tile([P, 2, 2, SLOTS * ROW_WORDS], F32, name="fetched")
-                    publish(i, turned, fetched_of[i])
-                if i + 1 < PAIRS:
-                    weave(i + 1)
-                done = i - MERGE_LAG
-                if done >= 0:
-                    first_batch, count = round_of[2 * done]
-                    if 2 * done == first_batch:
+                    publish(i, turned_of[i], fetched_of[i])
+                done = step - 4 - MERGE_LAG
+                if done >= 0 and done % 2 == 0:
+                    first_batch, count = round_of[done]
+                    if done == first_batch:
                         pooled_of[first_batch] = operand_pool.tile([P, count, PROPOSALS, PACK], BF16, align_bytes=64, name="pooled")
-                    merge(done, fetched_of[done], pooled_of[first_batch], 2 * done - first_batch)
-                    if 2 * done + 2 == first_batch + count:
+                    merge(done // 2, fetched_of[done // 2], pooled_of[first_batch], done - first_batch)
+                    if done + 2 == first_batch + count:
                         finish_round(first_batch, count, pooled_of[first_batch])
 
             for first_batch, count in rounds:

@@ -27,7 +27,7 @@ GROUP_SIZE = GROUP_CHANNELS * PROPOSALS
 GROUP_PARTITIONS = 4
 EPS = 1e-5
 CHUNKS = CHANNELS // P
-ROUND = 8
+ROUND = 4
 LARGEST = 3.3895313892515355e38
 ZONES = 3
 SLOTS = 4
@@ -62,6 +62,9 @@ def tile_coarsepyramid_pb_kernel(
             raw_of[i] = raw
 
         load(0)
+        warm = const.tile([P, 1], F32)
+        nc.vector.memset(warm[:], 0.0)
+        nc.scalar.activation(out=warm[:], in_=warm[:], func=ACT.Sqrt, scale=1.0)
 
         w_words = const.tile([P, CHANNELS], U32, align_bytes=64)
         nc.sync.dma_start(
@@ -111,8 +114,8 @@ def tile_coarsepyramid_pb_kernel(
         eps_col = const.tile([P, 1], F32)
         row_index = const.tile([P, PAIRS, 2, 2], I32)
         filled = const.tile([P, PAIRS, 2], F32)
-        slot_scale = const.tile([P, PAIRS, 2, SLOTS], F32)
-        slot_bias = const.tile([P, PAIRS, 2, SLOTS], F32)
+        slot_scale = const.tile([P, PAIRS, 2, SLOTS - 1], F32)
+        slot_bias = const.tile([P, PAIRS, 2, SLOTS - 1], F32)
 
         column_group = const.tile([P, P], I32)
         partition_index = const.tile([P, 1], I32)
@@ -124,7 +127,7 @@ def tile_coarsepyramid_pb_kernel(
         bias_rows = const.tile([P, CHUNKS], F32)
         bias_mean = const.tile([P, 1], F32)
 
-        def prepare():
+        def prepare_rows():
             nc.gpsimd.iota(partition_index[:], pattern=[[0, 1]], base=0, channel_multiplier=1)
             nc.vector.tensor_copy(out=partition_f[:], in_=partition_index[:])
             nc.vector.tensor_scalar(out=side[:], in0=partition_f[:], scalar1=float(PROPOSALS), scalar2=None, op0=ALU.is_ge)
@@ -173,12 +176,12 @@ def tile_coarsepyramid_pb_kernel(
                 tt(out=more2[:], in0=more2[:], in1=level2[:], op=ALU.mult)
                 tt(out=more[:], in0=more[:], in1=more1[:], op=ALU.add)
                 tt(out=more[:], in0=more[:], in1=more2[:], op=ALU.add)
-                for slot in range(SLOTS):
-                    scale = slot_scale[:, :, :, slot]
+                for slot in range(1, SLOTS):
+                    scale = slot_scale[:, :, :, slot - 1]
                     ts(out=scale, in0=more[:], scalar1=float(slot), scalar2=None, op0=ALU.is_ge)
                     tt(out=scale, in0=scale, in1=filled[:], op=ALU.mult)
-                    tt(out=slot_bias[:, :, :, slot], in0=scale, in1=filled[:], op=ALU.subtract)
-                    ts(out=slot_bias[:, :, :, slot], in0=slot_bias[:, :, :, slot], scalar1=LARGEST, scalar2=None, op0=ALU.mult)
+                    tt(out=slot_bias[:, :, :, slot - 1], in0=scale, in1=filled[:], op=ALU.subtract)
+                    ts(out=slot_bias[:, :, :, slot - 1], in0=slot_bias[:, :, :, slot - 1], scalar1=LARGEST, scalar2=None, op0=ALU.mult)
                 tt(out=more[:], in0=more[:], in1=run[:], op=ALU.mult)
                 tt(out=more[:], in0=more[:], in1=run[:], op=ALU.add)
                 nc.vector.scalar_tensor_tensor(out=start[:, 1], in0=start[:, 1], scalar=1.0, in1=more[:], op0=ALU.add, op1=ALU.subtract)
@@ -208,6 +211,7 @@ def tile_coarsepyramid_pb_kernel(
                     tt(out=start[:, end], in0=start[:, end], in1=base[:], op=ALU.add)
                     nc.vector.tensor_copy(out=row_index[:, :, :, end], in_=start[:, end])
 
+        def prepare_norm():
             nc.gpsimd.tensor_copy(
                 out=w_sorted[:].bitcast(I32).rearrange("p (q m) -> p q m", q=CHUNKS), in_=w_words[:].bitcast(I32).rearrange("p (m q) -> p q m", q=CHUNKS)
             )
@@ -236,8 +240,8 @@ def tile_coarsepyramid_pb_kernel(
         with tc.tile_pool(name="turned", bufs=3) as turned_pool, tc.tile_pool(name="step", bufs=3) as step_pool, tc.tile_pool(name="fetch", bufs=4) as fetch_pool, tc.tile_pool(
             name="merge", bufs=2
         ) as merge_pool, tc.tile_pool(name="operands", bufs=2) as operand_pool, tc.tile_pool(name="norm", bufs=2) as norm_pool, tc.psum_pool(
-            name="table_psum", bufs=3
-        ) as table_psum, tc.psum_pool(name="small_psum", bufs=1) as small_psum, tc.psum_pool(name="product_psum", bufs=CHUNKS) as product_psum:
+            name="table_psum", bufs=5
+        ) as table_psum, tc.psum_pool(name="small_psum", bufs=1) as small_psum, tc.psum_pool(name="product_psum", bufs=CHUNKS // 2) as product_psum:
 
             frames_of, run4_of, run16_of, turned_of = {}, {}, {}, {}
 
@@ -283,18 +287,18 @@ def tile_coarsepyramid_pb_kernel(
                         run2[:, r, 1 : many + 1].rearrange("p (q g) c -> p g q c", g=8),
                     )
                 words = run4[:].rearrange("p e c -> p (e c)").bitcast(F32)
-                nc.scalar.copy(out=words[:, 2 * FRAMES : 2 * FRAMES + 128], in_=words[:, 2 : 2 + 128])
+                nc.vector.tensor_copy(out=words[:, 2 * FRAMES : 2 * FRAMES + 128], in_=words[:, 2 : 2 + 128])
                 run4_of[b] = run4
 
-            def turned_maximum(words, b, zone):
+            def turned_maximum(words, b, zone, copy):
                 landing = turn(words, 0)
                 shifted = turn(words, 64)
                 here = step_pool.tile([P, 2, 2, P], F32, name="here")
-                nc.scalar.copy(out=here[:], in_=landing[:])
+                copy(out=here[:], in_=landing[:])
                 larger(swapped(turned_of[b // 2][zone][:, :, b % 2].bitcast(BF16)), shifted[:].bitcast(BF16), here[:].bitcast(BF16))
 
             def second_level(b):
-                turned_maximum(side_by_side(run4_of[b][:]), b, 1)
+                turned_maximum(side_by_side(run4_of[b][:]), b, 1, nc.scalar.copy)
 
             def back_again(b):
                 back8 = table_psum.tile([P, 2, 2, P], F32, name="landing")
@@ -319,7 +323,7 @@ def tile_coarsepyramid_pb_kernel(
 
             def third_level(b):
                 run16 = run16_of[b]
-                turned_maximum(lambda half, first: run16[:, half, first : first + P], b, 2)
+                turned_maximum(lambda half, first: run16[:, half, first : first + P], b, 2, nc.vector.tensor_copy)
 
             def publish(i, turned, fetched):
                 for half in range(2):
@@ -337,7 +341,6 @@ def tile_coarsepyramid_pb_kernel(
 
             def merge(i, fetched, pooled, place):
                 runs = merge_pool.tile([P, 2, SLOTS, HALF], BF16, name="runs")
-                counted = merge_pool.tile([P, 2, SLOTS, HALF], BF16, name="counted")
                 twos = merge_pool.tile([P, 2, 2, HALF], BF16, name="twos")
                 values = merge_pool.tile([P, 2, HALF], BF16, name="values")
                 for half in range(2):
@@ -345,15 +348,17 @@ def tile_coarsepyramid_pb_kernel(
                         out=runs[:, half].rearrange("p s c -> p (s c)"), in0=fetched[:, half, 0].bitcast(BF16), in1=fetched[:, half, 1].bitcast(BF16), op=ALU.max
                     )
                 for half in range(2):
-                    for slot in range(SLOTS):
+                    for slot in range(1, SLOTS):
                         nc.scalar.activation(
-                            out=counted[:, half, slot, :], in_=runs[:, half, slot, :], func=ACT.Identity,
-                            scale=slot_scale[:, i, half, slot : slot + 1], bias=slot_bias[:, i, half, slot : slot + 1],
+                            out=runs[:, half, slot, :], in_=runs[:, half, slot, :], func=ACT.Identity,
+                            scale=slot_scale[:, i, half, slot - 1 : slot], bias=slot_bias[:, i, half, slot - 1 : slot],
                         )
                 for half in range(2):
-                    nc.vector.tensor_tensor(out=twos[:, half], in0=counted[:, half, 0:2, :], in1=counted[:, half, 2:4, :], op=ALU.max)
+                    nc.vector.tensor_tensor(out=twos[:, half], in0=runs[:, half, 0:2, :], in1=runs[:, half, 2:4, :], op=ALU.max)
                 for half in range(2):
-                    nc.vector.tensor_tensor(out=values[:, half], in0=twos[:, half, 0, :], in1=twos[:, half, 1, :], op=ALU.max)
+                    nc.vector.scalar_tensor_tensor(
+                        out=values[:, half], in0=twos[:, half, 0, :], scalar=filled[:, i, half : half + 1], in1=twos[:, half, 1, :], op0=ALU.mult, op1=ALU.max
+                    )
                 flat = values[:].rearrange("p h c -> p (h c)")
                 back = small_psum.tile([P, PACK, P], BF16, name="back", tag="small")
                 for t in range(PACK):
@@ -371,9 +376,11 @@ def tile_coarsepyramid_pb_kernel(
                 row_sum = norm_pool.tile([P, CHUNKS, count], F32, name="row_sum")
                 for q in range(CHUNKS):
                     cols = slice(P * q, P * (q + 1))
-                    product = product_psum.tile([P, count, PROPOSALS], F32, name="product")
+                    if q % 2 == 0:
+                        bank = product_psum.tile([P, 2, count, PROPOSALS], F32, name="product")
+                    product = bank[:, q % 2]
                     nc.tensor.matmul_mx(
-                        out=product[:].rearrange("p b n -> p (b n)"),
+                        out=product.rearrange("p b n -> p (b n)"),
                         lhsT=w_sorted[:, cols].bitcast(FP8X4),
                         lhsT_scale=s_sorted[:, cols],
                         rhs=codes[:].bitcast(FP8X4),
@@ -381,8 +388,9 @@ def tile_coarsepyramid_pb_kernel(
                         start=True,
                         stop=True,
                     )
-                    nc.vector.tensor_reduce(out=row_sum[:, q, :], in_=product[:], axis=AXIS.X, op=ALU.add)
                     products.append(product)
+                    if q % 2 == 1:
+                        nc.vector.tensor_reduce(out=row_sum[:, q - 1 : q + 1, :], in_=bank[:], axis=AXIS.X, op=ALU.add)
                 mean_parts = small_psum.tile([P, CHUNKS, count], F32, name="mean_parts", tag="small")
                 nc.tensor.matmul(
                     out=mean_parts[:].rearrange("p q b -> p (q b)"), lhsT=group_average[:], rhs=row_sum[:].rearrange("p q b -> p (q b)"), start=True, stop=True
@@ -430,8 +438,7 @@ def tile_coarsepyramid_pb_kernel(
                             bias=offset[:, q, i : i + 1], scale=factor[:, q, i : i + 1],
                         )
 
-            rounds = [(first_batch, ROUND) for first_batch in range(0, BATCH - ROUND, ROUND)]
-            rounds.extend([(BATCH - 8, 4), (BATCH - 4, 2), (BATCH - 2, 2)])
+            rounds = [(first_batch, ROUND) for first_batch in range(0, BATCH, ROUND)]
             round_of = {}
             for first_batch, count in rounds:
                 for b in range(first_batch, first_batch + count):
@@ -455,11 +462,13 @@ def tile_coarsepyramid_pb_kernel(
                 if step + 1 < BATCH:
                     weave(step + 1)
                 if step == 1:
-                    prepare()
+                    prepare_rows()
                 if 0 <= step - 4 < BATCH and step % 2 == 0:
                     i = (step - 4) // 2
                     fetched_of[i] = fetch_pool.tile([P, 2, 2, SLOTS * ROW_WORDS], F32, name="fetched")
                     publish(i, turned_of[i], fetched_of[i])
+                    if i == 0:
+                        prepare_norm()
                 done = step - 4 - MERGE_LAG
                 if done >= 0 and done % 2 == 0:
                     first_batch, count = round_of[done]

@@ -35,7 +35,7 @@ ZONE_ROWS = FRAMES
 ROW_WORDS = HALF // 2
 TABLE_ROWS = ZONES * ZONE_ROWS
 UNIT_ROWS = 2 * TABLE_ROWS
-SPARE_ROWS = 4
+SPARE_ROWS = PROPOSALS + 4
 UNIT_PITCH = UNIT_ROWS + SPARE_ROWS
 UNITS = 7
 PAD = 4
@@ -54,11 +54,10 @@ def tile_coarsepyramid_pb_kernel(
 
         def load(i):
             raw = raw_pool.tile([P, 2, PACK * FRAMES], BF16, name="raw")
-            for half in range(2):
-                nc.sync.dma_start(
-                    out=raw[:, :, half * 2 * FRAMES : (half + 1) * 2 * FRAMES],
-                    in_=frame_level_feature[2 * i : 2 * i + 2, HALF * half : HALF * (half + 1)].rearrange("b (m j) t -> m b (j t)", j=2),
-                )
+            nc.sync.dma_start(
+                out=raw[:].rearrange("p b (h x) -> p (b h) x", h=2),
+                in_=frame_level_feature[2 * i : 2 * i + 2].rearrange("b (h m j) t -> m (b h) (j t)", h=2, j=2),
+            )
             raw_of[i] = raw
 
         load(0)
@@ -93,11 +92,10 @@ def tile_coarsepyramid_pb_kernel(
         identity_words = const.tile([P, P], F32)
         make_identity(nc, identity_words[:])
 
-        zeros = const.tile([UNITS, SPARE_ROWS * ROW_WORDS], F32)
+        zeros = const.tile([SPARE_ROWS, UNITS, ROW_WORDS], F32)
         nc.vector.memset(zeros[:], 0.0)
         nc.sync.dma_start(
-            out=out_rows[0 : UNITS * UNIT_PITCH].rearrange("(u r) w -> u (r w)", u=UNITS)[:, UNIT_ROWS * ROW_WORDS : UNIT_PITCH * ROW_WORDS],
-            in_=zeros[:],
+            out=out_rows[0 : UNITS * UNIT_PITCH].rearrange("(u r) w -> r u w", u=UNITS)[UNIT_ROWS:UNIT_PITCH], in_=zeros[:]
         )
 
         run2_ring = [const.tile([P, 2, FRAMES // 2 + PAD, PACK], BF16, name="run2_%d" % s) for s in range(2)]
@@ -112,13 +110,16 @@ def tile_coarsepyramid_pb_kernel(
         shift_col = columns[:, 2 * CHUNKS : 3 * CHUNKS]
         bias_centred = const.tile([P, CHUNKS], F32)
         eps_col = const.tile([P, 1], F32)
-        row_index = const.tile([P, PAIRS, 2, 2], I32)
-        filled = const.tile([P, PAIRS, 2], F32)
-        slot_scale = const.tile([P, PAIRS, 2, SLOTS - 1], F32)
-        slot_bias = const.tile([P, PAIRS, 2, SLOTS - 1], F32)
+        row_index = const.tile([P, 2, PAIRS, 2], I32)
+        slot_scale = const.tile([P, SLOTS - 1, PAIRS, 2], F32)
+        slot_bias = const.tile([P, SLOTS - 1, PAIRS, 2], F32)
 
         column_group = const.tile([P, P], I32)
         partition_index = const.tile([P, 1], I32)
+        nc.gpsimd.iota(partition_index[:], pattern=[[0, 1]], base=0, channel_multiplier=1)
+        cycles = (2 * PAIRS + UNITS - 1) // UNITS
+        unit_int = const.tile([P, cycles * UNITS], I32)
+        nc.gpsimd.iota(unit_int[:], pattern=[[0, cycles], [UNIT_PITCH, UNITS]], base=0, channel_multiplier=0)
         partition_group = const.tile([P, 1], I32)
         column_group_f = const.tile([P, P], F32)
         partition_group_f = const.tile([P, 1], F32)
@@ -127,89 +128,80 @@ def tile_coarsepyramid_pb_kernel(
         bias_rows = const.tile([P, CHUNKS], F32)
         bias_mean = const.tile([P, 1], F32)
 
-        def prepare_rows():
-            nc.gpsimd.iota(partition_index[:], pattern=[[0, 1]], base=0, channel_multiplier=1)
+        def prepare_rows(setup):
+            tt = nc.vector.tensor_tensor
+            ts = nc.vector.tensor_scalar
+            stt = nc.vector.scalar_tensor_tensor
+            shape = [P, PAIRS, 2]
+            both = [P, 2, PAIRS, 2]
+            start = setup.tile(both, F32, name="start")
+            level1 = setup.tile(shape, F32, name="level1")
+            level2 = setup.tile(shape, F32, name="level2")
+            filled = setup.tile(shape, F32, name="filled")
+
+            ends = setup.tile(both, F32, name="ends")
+            ts(out=ends[:], in0=segments[:].rearrange("p i (h e) -> p e i h", e=2), scalar1=0.0, scalar2=FRAMES - 1.0, op0=ALU.max, op1=ALU.min)
+            as_int = setup.tile(both, I32, name="as_int")
+            nc.vector.tensor_copy(out=as_int[:], in_=ends[:])
+            near = setup.tile(both, F32, name="near")
+            nc.vector.tensor_copy(out=near[:], in_=as_int[:])
+            above = setup.tile(both, F32, name="above")
+            tt(out=above[:], in0=near[:], in1=ends[:], op=ALU.is_gt)
+            tt(out=start[:], in0=near[:], in1=above[:], op=ALU.subtract)
+            span = setup.tile(shape, F32, name="span")
+            tt(out=span[:], in0=start[:, 1], in1=start[:, 0], op=ALU.subtract)
+            ts(out=filled[:], in0=span[:], scalar1=0.0, scalar2=None, op0=ALU.is_ge)
+            ts(out=span[:], in0=span[:], scalar1=0.0, scalar2=None, op0=ALU.max)
+            ts(out=level1[:], in0=span[:], scalar1=8.0, scalar2=None, op0=ALU.is_ge)
+            ts(out=level2[:], in0=span[:], scalar1=64.0, scalar2=None, op0=ALU.is_ge)
+            run = setup.tile(shape, F32, name="run")
+            ts(out=run[:], in0=level1[:], scalar1=7.0, scalar2=1.0, op0=ALU.mult, op1=ALU.add)
+            stt(out=run[:], in0=level2[:], scalar=24.0, in1=run[:], op0=ALU.mult, op1=ALU.add)
+            for slot in range(1, SLOTS):
+                stt(out=slot_scale[:, slot - 1], in0=run[:], scalar=2.0 * slot, in1=span[:], op0=ALU.mult, op1=ALU.is_le)
+            slots = setup.tile(shape, F32, name="slots")
+            stt(out=slots[:], in0=slot_scale[:, 0], scalar=1.0, in1=slot_scale[:, 1], op0=ALU.add, op1=ALU.add)
+            tt(out=slots[:], in0=slots[:], in1=slot_scale[:, 2], op=ALU.add)
+            tt(out=slots[:], in0=slots[:], in1=run[:], op=ALU.mult)
+            stt(out=start[:, 1], in0=start[:, 1], scalar=1.0, in1=slots[:], op0=ALU.add, op1=ALU.subtract)
+            ts(out=slot_bias[:], in0=slot_scale[:], scalar1=1.0, scalar2=LARGEST, op0=ALU.subtract, op1=ALU.mult)
+
             nc.vector.tensor_copy(out=partition_f[:], in_=partition_index[:])
-            nc.vector.tensor_scalar(out=side[:], in0=partition_f[:], scalar1=float(PROPOSALS), scalar2=None, op0=ALU.is_ge)
-            with tc.tile_pool(name="setup", bufs=1) as setup:
-                shape = [P, PAIRS, 2]
-                both = [P, 2, PAIRS, 2]
-                tt = nc.vector.tensor_tensor
-                ts = nc.vector.tensor_scalar
-
-                def whole_of(shift, source_int, dims, name):
-                    shifted = setup.tile(dims, I32, name=name + "_int")
-                    nc.vector.tensor_single_scalar(out=shifted[:], in_=source_int[:], scalar=shift, op=ALU.arith_shift_right)
-                    value = setup.tile(dims, F32, name=name)
-                    nc.vector.tensor_copy(out=value[:], in_=shifted[:])
-                    return value
-
-                ends = setup.tile(both, F32, name="ends")
-                ts(out=ends[:], in0=segments[:].rearrange("p i (h e) -> p e i h", e=2), scalar1=0.0, scalar2=FRAMES - 1.0, op0=ALU.max, op1=ALU.min)
-                as_int = setup.tile(both, I32, name="as_int")
-                nc.vector.tensor_copy(out=as_int[:], in_=ends[:])
-                near = setup.tile(both, F32, name="near")
-                nc.vector.tensor_copy(out=near[:], in_=as_int[:])
-                above = setup.tile(both, F32, name="above")
-                tt(out=above[:], in0=near[:], in1=ends[:], op=ALU.is_gt)
-                start = setup.tile(both, F32, name="start")
-                tt(out=start[:], in0=near[:], in1=above[:], op=ALU.subtract)
-                span = setup.tile(shape, F32, name="span")
-                tt(out=span[:], in0=start[:, 1], in1=start[:, 0], op=ALU.subtract)
-                ts(out=filled[:], in0=span[:], scalar1=0.0, scalar2=None, op0=ALU.is_ge)
-                ts(out=span[:], in0=span[:], scalar1=0.0, scalar2=None, op0=ALU.max)
-                level1 = setup.tile(shape, F32, name="level1")
-                ts(out=level1[:], in0=span[:], scalar1=8.0, scalar2=None, op0=ALU.is_ge)
-                level2 = setup.tile(shape, F32, name="level2")
-                ts(out=level2[:], in0=span[:], scalar1=64.0, scalar2=None, op0=ALU.is_ge)
-                run = setup.tile(shape, F32, name="run")
-                ts(out=run[:], in0=level1[:], scalar1=7.0, scalar2=1.0, op0=ALU.mult, op1=ALU.add)
-                nc.vector.scalar_tensor_tensor(out=run[:], in0=level2[:], scalar=24.0, in1=run[:], op0=ALU.mult, op1=ALU.add)
-                span_int = setup.tile(shape, I32, name="span_int")
-                nc.vector.tensor_copy(out=span_int[:], in_=span[:])
-                more = whole_of(1, span_int, shape, "more")
-                more1 = whole_of(4, span_int, shape, "more1")
-                more2 = whole_of(6, span_int, shape, "more2")
-                tt(out=more2[:], in0=more2[:], in1=more1[:], op=ALU.subtract)
-                tt(out=more1[:], in0=more1[:], in1=more[:], op=ALU.subtract)
-                tt(out=more1[:], in0=more1[:], in1=level1[:], op=ALU.mult)
-                tt(out=more2[:], in0=more2[:], in1=level2[:], op=ALU.mult)
-                tt(out=more[:], in0=more[:], in1=more1[:], op=ALU.add)
-                tt(out=more[:], in0=more[:], in1=more2[:], op=ALU.add)
-                for slot in range(1, SLOTS):
-                    scale = slot_scale[:, :, :, slot - 1]
-                    ts(out=scale, in0=more[:], scalar1=float(slot), scalar2=None, op0=ALU.is_ge)
-                    tt(out=scale, in0=scale, in1=filled[:], op=ALU.mult)
-                    tt(out=slot_bias[:, :, :, slot - 1], in0=scale, in1=filled[:], op=ALU.subtract)
-                    ts(out=slot_bias[:, :, :, slot - 1], in0=slot_bias[:, :, :, slot - 1], scalar1=LARGEST, scalar2=None, op0=ALU.mult)
-                tt(out=more[:], in0=more[:], in1=run[:], op=ALU.mult)
-                tt(out=more[:], in0=more[:], in1=run[:], op=ALU.add)
-                nc.vector.scalar_tensor_tensor(out=start[:, 1], in0=start[:, 1], scalar=1.0, in1=more[:], op0=ALU.add, op1=ALU.subtract)
-                start_int = setup.tile(both, I32, name="start_int")
-                nc.vector.tensor_copy(out=start_int[:], in_=start[:])
-                eighth = whole_of(3, start_int, both, "eighth")
-                ts(out=eighth[:], in0=eighth[:], scalar1=float(1 - 32 * 8), scalar2=float(ZONE_ROWS), op0=ALU.mult, op1=ALU.add)
-                thirty_second = whole_of(5, start_int, both, "thirty_second")
-                ts(out=thirty_second[:], in0=thirty_second[:], scalar1=float(1 - 8 * 32), scalar2=float(2 * ZONE_ROWS), op0=ALU.mult, op1=ALU.add)
-                tt(out=thirty_second[:], in0=thirty_second[:], in1=eighth[:], op=ALU.subtract)
-                nc.vector.scalar_tensor_tensor(out=eighth[:], in0=start[:], scalar=31.0, in1=eighth[:], op0=ALU.mult, op1=ALU.add)
-                nc.vector.scalar_tensor_tensor(out=thirty_second[:], in0=start[:], scalar=-24.0, in1=thirty_second[:], op0=ALU.mult, op1=ALU.add)
-                for end in range(2):
-                    tt(out=eighth[:, end], in0=eighth[:, end], in1=level1[:], op=ALU.mult)
-                    tt(out=thirty_second[:, end], in0=thirty_second[:, end], in1=level2[:], op=ALU.mult)
-                tt(out=start[:], in0=start[:], in1=eighth[:], op=ALU.add)
-                tt(out=start[:], in0=start[:], in1=thirty_second[:], op=ALU.add)
-                cycles = (2 * PAIRS + UNITS - 1) // UNITS
-                unit_int = setup.tile([P, cycles * UNITS], I32, name="unit_int")
-                nc.gpsimd.iota(unit_int[:], pattern=[[0, cycles], [UNIT_PITCH, UNITS]], base=0, channel_multiplier=0)
-                base = setup.tile(shape, F32, name="base")
-                nc.vector.tensor_copy(out=base[:].rearrange("p i h -> p (i h)"), in_=unit_int[:, 0 : 2 * PAIRS])
-                behind = setup.tile([P, 1], F32, name="behind")
-                ts(out=behind[:], in0=side[:], scalar1=float(TABLE_ROWS), scalar2=None, op0=ALU.mult)
-                ts(out=base[:], in0=base[:], scalar1=behind[:, 0:1], scalar2=None, op0=ALU.add)
-                for end in range(2):
-                    tt(out=start[:, end], in0=start[:, end], in1=base[:], op=ALU.add)
-                    nc.vector.tensor_copy(out=row_index[:, :, :, end], in_=start[:, end])
+            ts(out=side[:], in0=partition_f[:], scalar1=float(PROPOSALS), scalar2=None, op0=ALU.is_ge)
+            start_int = setup.tile(both, I32, name="start_int")
+            nc.vector.tensor_copy(out=start_int[:], in_=start[:])
+            shifted = setup.tile([P, 2] + both[1:], I32, name="shifted")
+            for s, shift in enumerate((3, 5)):
+                nc.vector.tensor_single_scalar(out=shifted[:, s], in_=start_int[:], scalar=shift, op=ALU.arith_shift_right)
+            whole = setup.tile([P, 2] + both[1:], F32, name="whole")
+            nc.vector.tensor_copy(out=whole[:], in_=shifted[:])
+            eighth, thirty_second = whole[:, 0], whole[:, 1]
+            tt(out=thirty_second, in0=eighth, in1=thirty_second, op=ALU.subtract)
+            ts(out=eighth, in0=eighth, scalar1=-255.0, scalar2=float(ZONE_ROWS), op0=ALU.mult, op1=ALU.add)
+            ts(out=thirty_second, in0=thirty_second, scalar1=255.0, scalar2=float(ZONE_ROWS), op0=ALU.mult, op1=ALU.add)
+            stt(out=eighth, in0=start[:], scalar=31.0, in1=eighth, op0=ALU.mult, op1=ALU.add)
+            stt(out=thirty_second, in0=start[:], scalar=-24.0, in1=thirty_second, op0=ALU.mult, op1=ALU.add)
+            for end in range(2):
+                tt(out=eighth[:, end], in0=eighth[:, end], in1=level1[:], op=ALU.mult)
+                tt(out=thirty_second[:, end], in0=thirty_second[:, end], in1=level2[:], op=ALU.mult)
+            tt(out=start[:], in0=start[:], in1=eighth, op=ALU.add)
+            tt(out=start[:], in0=start[:], in1=thirty_second, op=ALU.add)
+            empty = setup.tile([P, 1], F32, name="empty")
+            stt(out=empty[:], in0=side[:], scalar=-float(TABLE_ROWS + PROPOSALS), in1=partition_f[:], op0=ALU.mult, op1=ALU.add)
+            ts(out=empty[:], in0=empty[:], scalar1=float(UNIT_ROWS), scalar2=None, op0=ALU.add)
+            ts(out=start[:], in0=start[:], scalar1=empty[:, 0:1], scalar2=None, op0=ALU.subtract)
+            for end in range(2):
+                tt(out=start[:, end], in0=start[:, end], in1=filled[:], op=ALU.mult)
+            ts(out=start[:], in0=start[:], scalar1=empty[:, 0:1], scalar2=None, op0=ALU.add)
+            base = setup.tile(shape, F32, name="base")
+            nc.vector.tensor_copy(out=base[:].rearrange("p i h -> p (i h)"), in_=unit_int[:, 0 : 2 * PAIRS])
+            stt(
+                out=base[:].rearrange("p i h -> p (i h)"), in0=side[:, 0:1].to_broadcast([P, 2 * PAIRS]), scalar=float(TABLE_ROWS),
+                in1=base[:].rearrange("p i h -> p (i h)"), op0=ALU.mult, op1=ALU.add,
+            )
+            for end in range(2):
+                tt(out=start[:, end], in0=start[:, end], in1=base[:], op=ALU.add)
+            nc.vector.tensor_copy(out=row_index[:], in_=start[:])
 
         def prepare_norm():
             nc.gpsimd.tensor_copy(
@@ -271,10 +263,10 @@ def tile_coarsepyramid_pb_kernel(
 
             def first_level(b):
                 if b % 2 == 0:
-                    turned_of[b // 2] = [turned_pool.tile([P, 2, 2, 2, ROW_WORDS], F32, name="turned%d" % zone) for zone in range(ZONES)]
+                    turned_of[b // 2] = turned_pool.tile([P, 2, ZONES, 2, 2, ROW_WORDS], F32, name="turned")
                 frames = frames_of[b]
                 landing = turn(side_by_side(frames[:]), 0)
-                nc.scalar.copy(out=turned_of[b // 2][0][:, :, b % 2], in_=swapped(landing[:]))
+                nc.scalar.copy(out=turned_of[b // 2][:, b % 2, 0], in_=swapped(landing[:]))
                 run2 = run2_ring[b % 2]
                 many = FRAMES // 2
                 larger(run2[:, 0, 0:many], frames[:, 0:many], frames[:, many:FRAMES])
@@ -295,7 +287,7 @@ def tile_coarsepyramid_pb_kernel(
                 shifted = turn(words, 64)
                 here = step_pool.tile([P, 2, 2, P], F32, name="here")
                 copy(out=here[:], in_=landing[:])
-                larger(swapped(turned_of[b // 2][zone][:, :, b % 2].bitcast(BF16)), shifted[:].bitcast(BF16), here[:].bitcast(BF16))
+                larger(swapped(turned_of[b // 2][:, b % 2, zone].bitcast(BF16)), shifted[:].bitcast(BF16), here[:].bitcast(BF16))
 
             def second_level(b):
                 turned_maximum(side_by_side(run4_of[b][:]), b, 1, nc.scalar.copy)
@@ -304,7 +296,7 @@ def tile_coarsepyramid_pb_kernel(
                 back8 = table_psum.tile([P, 2, 2, P], F32, name="landing")
                 for half in range(2):
                     for a in range(2):
-                        nc.tensor.transpose(back8[:, half, a, :], turned_of[b // 2][1][:, half, b % 2, a, :], identity_words[:])
+                        nc.tensor.transpose(back8[:, half, a, :], turned_of[b // 2][:, b % 2, 1, half, a, :], identity_words[:])
                 ordered = back8[:].rearrange("p h a e -> p h (a e)")
                 run8 = step_pool.tile([P, 2, FRAMES + 32], F32, name="run8")
                 nc.scalar.copy(
@@ -328,15 +320,16 @@ def tile_coarsepyramid_pb_kernel(
             def publish(i, turned, fetched):
                 for half in range(2):
                     unit = (2 * i + half) % UNITS
-                    rows = out_rows[unit * UNIT_PITCH : unit * UNIT_PITCH + UNIT_ROWS].rearrange("(b z p a) w -> z p b (a w)", b=2, z=ZONES, p=P)
-                    for zone in range(ZONES):
-                        nc.sync.dma_start(out=rows[zone], in_=turned[zone][:, half].rearrange("p b a w -> p b (a w)"))
+                    rows = out_rows[unit * UNIT_PITCH : unit * UNIT_PITCH + UNIT_ROWS]
+                    nc.sync.dma_start(
+                        out=rows.rearrange("(b z p a) w -> p (b z) (a w)", b=2, z=ZONES, p=P), in_=turned[:, :, :, half].rearrange("p b z a w -> p (b z) (a w)")
+                    )
                     for end in range(2):
                         nc.gpsimd.indirect_dma_start(
                             out=fetched[:, half, end, :],
                             out_offset=None,
                             in_=out_rows[0 : (unit + 1) * UNIT_PITCH, :],
-                            in_offset=bass.IndirectOffsetOnAxis(ap=row_index[:, i, half, end : end + 1], axis=0),
+                            in_offset=bass.IndirectOffsetOnAxis(ap=row_index[:, end, i, half : half + 1], axis=0),
                         )
 
             def merge(i, fetched, pooled, place):
@@ -351,14 +344,12 @@ def tile_coarsepyramid_pb_kernel(
                     for slot in range(1, SLOTS):
                         nc.scalar.activation(
                             out=runs[:, half, slot, :], in_=runs[:, half, slot, :], func=ACT.Identity,
-                            scale=slot_scale[:, i, half, slot - 1 : slot], bias=slot_bias[:, i, half, slot - 1 : slot],
+                            scale=slot_scale[:, slot - 1, i, half : half + 1], bias=slot_bias[:, slot - 1, i, half : half + 1],
                         )
                 for half in range(2):
                     nc.vector.tensor_tensor(out=twos[:, half], in0=runs[:, half, 0:2, :], in1=runs[:, half, 2:4, :], op=ALU.max)
                 for half in range(2):
-                    nc.vector.scalar_tensor_tensor(
-                        out=values[:, half], in0=twos[:, half, 0, :], scalar=filled[:, i, half : half + 1], in1=twos[:, half, 1, :], op0=ALU.mult, op1=ALU.max
-                    )
+                    nc.vector.tensor_tensor(out=values[:, half], in0=twos[:, half, 0, :], in1=twos[:, half, 1, :], op=ALU.max)
                 flat = values[:].rearrange("p h c -> p (h c)")
                 back = small_psum.tile([P, PACK, P], BF16, name="back", tag="small")
                 for t in range(PACK):
@@ -462,7 +453,8 @@ def tile_coarsepyramid_pb_kernel(
                 if step + 1 < BATCH:
                     weave(step + 1)
                 if step == 1:
-                    prepare_rows()
+                    with tc.tile_pool(name="setup", bufs=1) as setup:
+                        prepare_rows(setup)
                 if 0 <= step - 4 < BATCH and step % 2 == 0:
                     i = (step - 4) // 2
                     fetched_of[i] = fetch_pool.tile([P, 2, 2, SLOTS * ROW_WORDS], F32, name="fetched")

import concourse.bass as bass
import concourse.mybir as mybir
from concourse.masks import make_identity

FLOPS = 2 * 48 * 512 * 512 * 64

BF16 = mybir.dt.bfloat16
F32 = mybir.dt.float32
I32 = mybir.dt.int32
U32 = mybir.dt.uint32
U8 = mybir.dt.uint8
FP8X4 = mybir.dt.float8_e4m3fn_x4
ALU = mybir.AluOpType
ACT = mybir.ActivationFunctionType
AXIS = mybir.AxisListType

P = 128
PACK = 4
BATCH = 48
PAIRS = BATCH // 2
CHANNELS = 512
HALF = CHANNELS // 2
FRAMES = 256
PROPOSALS = 64
GROUP_CHANNELS = 16
GROUP_SIZE = GROUP_CHANNELS * PROPOSALS
GROUP_PARTITIONS = 4
EPS = 1e-5
CHUNKS = CHANNELS // P
ROUND = 4
LARGEST = 3.3895313892515355e38
ZONES = 3
SLOTS = 4
ZONE_ROWS = FRAMES
ROW_WORDS = HALF // 2
TABLE_ROWS = ZONES * ZONE_ROWS
UNIT_ROWS = 2 * TABLE_ROWS
SPARE_ROWS = PROPOSALS + 4
UNIT_PITCH = UNIT_ROWS + SPARE_ROWS
UNITS = 7
PAD = 4


def tile_coarsepyramid_pb_kernel(
    tc, frame_level_feature, frame_segments, w_roi_words, w_roi_scales, b_roi, g_roi, be_roi, out
):
    nc = tc.nc
    flat_out = out.rearrange("b c n -> (b c n)")
    out_rows = flat_out.rearrange("(r w) -> r w", w=ROW_WORDS)
    assert UNITS * UNIT_PITCH <= BATCH * CHANNELS * PROPOSALS // ROW_WORDS

    with tc.tile_pool(name="const", bufs=1) as const, tc.tile_pool(name="raw", bufs=3) as raw_pool:
        raw_of = {}

        def load(i):
            raw = raw_pool.tile([P, 2, PACK * FRAMES], BF16, name="raw")
            nc.sync.dma_start(
                out=raw[:].rearrange("p b (h x) -> p (b h) x", h=2),
                in_=frame_level_feature[2 * i : 2 * i + 2].rearrange("b (h m j) t -> m (b h) (j t)", h=2, j=2),
            )
            raw_of[i] = raw

        load(0)
        warm = const.tile([P, 1], F32)
        nc.vector.memset(warm[:], 0.0)
        nc.scalar.activation(out=warm[:], in_=warm[:], func=ACT.Sqrt, scale=1.0)

        w_words = const.tile([P, CHANNELS], U32, align_bytes=64)
        nc.sync.dma_start(
            out=w_words[:].bitcast(I32),
            in_=w_roi_words[0].rearrange("p n t -> p (n t)").bitcast(I32),
        )
        w_scales = const.tile([P, CHANNELS], U8, align_bytes=64)
        nc.vector.memset(w_scales[:].bitcast(I32), 0)
        for quadrant in range(4):
            nc.sync.dma_start(
                out=w_scales[32 * quadrant : 32 * quadrant + 4, :].bitcast(I32),
                in_=w_roi_scales[0, 4 * quadrant : 4 * quadrant + 4, :].bitcast(I32),
            )

        fours = []
        for i, vector in enumerate((b_roi, g_roi, be_roi)):
            four = const.tile([P, CHUNKS], BF16, name="four%d" % i)
            nc.sync.dma_start(out=four[:], in_=vector.rearrange("(p q) -> p q", q=CHUNKS))
            fours.append(four)
        segments = const.tile([P, PAIRS, 4], BF16)
        for s in range(2):
            nc.sync.dma_start(out=segments[64 * s : 64 * s + 64], in_=frame_segments.rearrange("(i s) n e -> s n i e", s=2)[s])

        identity = const.tile([P, P], BF16)
        make_identity(nc, identity[:])
        identity_words = const.tile([P, P], F32)
        make_identity(nc, identity_words[:])

        zeros = const.tile([SPARE_ROWS, UNITS, ROW_WORDS], F32)
        nc.vector.memset(zeros[:], 0.0)
        nc.sync.dma_start(
            out=out_rows[0 : UNITS * UNIT_PITCH].rearrange("(u r) w -> r u w", u=UNITS)[UNIT_ROWS:UNIT_PITCH], in_=zeros[:]
        )

        run2_ring = [const.tile([P, 2, FRAMES // 2 + PAD, PACK], BF16, name="run2_%d" % s) for s in range(2)]
        for run2 in run2_ring:
            nc.vector.memset(run2[:, :, FRAMES // 2 : FRAMES // 2 + PAD, :], 0.0)

        w_sorted = const.tile([P, CHANNELS], U32, align_bytes=64)
        s_sorted = const.tile([P, CHANNELS], U8, align_bytes=64)
        group_average = const.tile([P, P], F32)
        columns = const.tile([P, 3 * CHUNKS], F32)
        gain_col = columns[:, CHUNKS : 2 * CHUNKS]
        shift_col = columns[:, 2 * CHUNKS : 3 * CHUNKS]
        bias_centred = const.tile([P, CHUNKS], F32)
        eps_col = const.tile([P, 1], F32)
        row_index = const.tile([P, 2, PAIRS, 2], I32)
        slot_scale = const.tile([P, SLOTS - 1, PAIRS, 2], F32)
        slot_bias = const.tile([P, SLOTS - 1, PAIRS, 2], F32)

        column_group = const.tile([P, P], I32)
        partition_index = const.tile([P, 1], I32)
        nc.gpsimd.iota(partition_index[:], pattern=[[0, 1]], base=0, channel_multiplier=1)
        cycles = (2 * PAIRS + UNITS - 1) // UNITS
        unit_int = const.tile([P, cycles * UNITS], I32)
        nc.gpsimd.iota(unit_int[:], pattern=[[0, cycles], [UNIT_PITCH, UNITS]], base=0, channel_multiplier=0)
        partition_group = const.tile([P, 1], I32)
        column_group_f = const.tile([P, P], F32)
        partition_group_f = const.tile([P, 1], F32)
        partition_f = const.tile([P, 1], F32)
        side = const.tile([P, 1], F32)
        bias_rows = const.tile([P, CHUNKS], F32)
        bias_mean = const.tile([P, 1], F32)

        def prepare_rows(setup):
            tt = nc.vector.tensor_tensor
            ts = nc.vector.tensor_scalar
            stt = nc.vector.scalar_tensor_tensor
            shape = [P, PAIRS, 2]
            both = [P, 2, PAIRS, 2]
            start = setup.tile(both, F32, name="start")
            level1 = setup.tile(shape, F32, name="level1")
            level2 = setup.tile(shape, F32, name="level2")
            filled = setup.tile(shape, F32, name="filled")

            ends = setup.tile(both, F32, name="ends")
            ts(out=ends[:], in0=segments[:].rearrange("p i (h e) -> p e i h", e=2), scalar1=0.0, scalar2=FRAMES - 1.0, op0=ALU.max, op1=ALU.min)
            as_int = setup.tile(both, I32, name="as_int")
            nc.vector.tensor_copy(out=as_int[:], in_=ends[:])
            near = setup.tile(both, F32, name="near")
            nc.vector.tensor_copy(out=near[:], in_=as_int[:])
            above = setup.tile(both, F32, name="above")
            tt(out=above[:], in0=near[:], in1=ends[:], op=ALU.is_gt)
            tt(out=start[:], in0=near[:], in1=above[:], op=ALU.subtract)
            span = setup.tile(shape, F32, name="span")
            tt(out=span[:], in0=start[:, 1], in1=start[:, 0], op=ALU.subtract)
            ts(out=filled[:], in0=span[:], scalar1=0.0, scalar2=None, op0=ALU.is_ge)
            ts(out=span[:], in0=span[:], scalar1=0.0, scalar2=None, op0=ALU.max)
            ts(out=level1[:], in0=span[:], scalar1=8.0, scalar2=None, op0=ALU.is_ge)
            ts(out=level2[:], in0=span[:], scalar1=64.0, scalar2=None, op0=ALU.is_ge)
            run = setup.tile(shape, F32, name="run")
            ts(out=run[:], in0=level1[:], scalar1=7.0, scalar2=1.0, op0=ALU.mult, op1=ALU.add)
            stt(out=run[:], in0=level2[:], scalar=24.0, in1=run[:], op0=ALU.mult, op1=ALU.add)
            for slot in range(1, SLOTS):
                stt(out=slot_scale[:, slot - 1], in0=run[:], scalar=2.0 * slot, in1=span[:], op0=ALU.mult, op1=ALU.is_le)
            slots = setup.tile(shape, F32, name="slots")
            stt(out=slots[:], in0=slot_scale[:, 0], scalar=1.0, in1=slot_scale[:, 1], op0=ALU.add, op1=ALU.add)
            tt(out=slots[:], in0=slots[:], in1=slot_scale[:, 2], op=ALU.add)
            tt(out=slots[:], in0=slots[:], in1=run[:], op=ALU.mult)
            stt(out=start[:, 1], in0=start[:, 1], scalar=1.0, in1=slots[:], op0=ALU.add, op1=ALU.subtract)
            ts(out=slot_bias[:], in0=slot_scale[:], scalar1=1.0, scalar2=LARGEST, op0=ALU.subtract, op1=ALU.mult)

            nc.vector.tensor_copy(out=partition_f[:], in_=partition_index[:])
            ts(out=side[:], in0=partition_f[:], scalar1=float(PROPOSALS), scalar2=None, op0=ALU.is_ge)
            start_int = setup.tile(both, I32, name="start_int")
            nc.vector.tensor_copy(out=start_int[:], in_=start[:])
            shifted = setup.tile([P, 2] + both[1:], I32, name="shifted")
            for s, shift in enumerate((3, 5)):
                nc.vector.tensor_single_scalar(out=shifted[:, s], in_=start_int[:], scalar=shift, op=ALU.arith_shift_right)
            whole = setup.tile([P, 2] + both[1:], F32, name="whole")
            nc.vector.tensor_copy(out=whole[:], in_=shifted[:])
            eighth, thirty_second = whole[:, 0], whole[:, 1]
            tt(out=thirty_second, in0=eighth, in1=thirty_second, op=ALU.subtract)
            ts(out=eighth, in0=eighth, scalar1=-255.0, scalar2=float(ZONE_ROWS), op0=ALU.mult, op1=ALU.add)
            ts(out=thirty_second, in0=thirty_second, scalar1=255.0, scalar2=float(ZONE_ROWS), op0=ALU.mult, op1=ALU.add)
            stt(out=eighth, in0=start[:], scalar=31.0, in1=eighth, op0=ALU.mult, op1=ALU.add)
            stt(out=thirty_second, in0=start[:], scalar=-24.0, in1=thirty_second, op0=ALU.mult, op1=ALU.add)
            for end in range(2):
                tt(out=eighth[:, end], in0=eighth[:, end], in1=level1[:], op=ALU.mult)
                tt(out=thirty_second[:, end], in0=thirty_second[:, end], in1=level2[:], op=ALU.mult)
            tt(out=start[:], in0=start[:], in1=eighth, op=ALU.add)
            tt(out=start[:], in0=start[:], in1=thirty_second, op=ALU.add)
            empty = setup.tile([P, 1], F32, name="empty")
            stt(out=empty[:], in0=side[:], scalar=-float(TABLE_ROWS + PROPOSALS), in1=partition_f[:], op0=ALU.mult, op1=ALU.add)
            ts(out=empty[:], in0=empty[:], scalar1=float(UNIT_ROWS), scalar2=None, op0=ALU.add)
            ts(out=start[:], in0=start[:], scalar1=empty[:, 0:1], scalar2=None, op0=ALU.subtract)
            for end in range(2):
                tt(out=start[:, end], in0=start[:, end], in1=filled[:], op=ALU.mult)
            ts(out=start[:], in0=start[:], scalar1=empty[:, 0:1], scalar2=None, op0=ALU.add)
            base = setup.tile(shape, F32, name="base")
            nc.vector.tensor_copy(out=base[:].rearrange("p i h -> p (i h)"), in_=unit_int[:, 0 : 2 * PAIRS])
            stt(
                out=base[:].rearrange("p i h -> p (i h)"), in0=side[:, 0:1].to_broadcast([P, 2 * PAIRS]), scalar=float(TABLE_ROWS),
                in1=base[:].rearrange("p i h -> p (i h)"), op0=ALU.mult, op1=ALU.add,
            )
            for end in range(2):
                tt(out=start[:, end], in0=start[:, end], in1=base[:], op=ALU.add)
            nc.vector.tensor_copy(out=row_index[:], in_=start[:])

        def prepare_norm():
            nc.gpsimd.tensor_copy(
                out=w_sorted[:].bitcast(I32).rearrange("p (q m) -> p q m", q=CHUNKS), in_=w_words[:].bitcast(I32).rearrange("p (m q) -> p q m", q=CHUNKS)
            )
            nc.vector.tensor_copy(out=s_sorted[:].rearrange("p (q m) -> p m q", q=CHUNKS), in_=w_scales[:].rearrange("p (m q) -> p m q", q=CHUNKS))

            nc.gpsimd.iota(column_group[:], pattern=[[1, P // GROUP_PARTITIONS], [0, GROUP_PARTITIONS]], base=0, channel_multiplier=0)
            nc.vector.tensor_single_scalar(out=partition_group[:], in_=partition_index[:], scalar=2, op=ALU.arith_shift_right)
            nc.vector.tensor_copy(out=column_group_f[:], in_=column_group[:])
            nc.vector.tensor_copy(out=partition_group_f[:], in_=partition_group[:])
            nc.vector.tensor_scalar(
                out=group_average[:], in0=column_group_f[:], scalar1=partition_group_f[:, 0:1], scalar2=1.0 / GROUP_SIZE,
                op0=ALU.is_equal, op1=ALU.mult,
            )

            for i in range(3):
                nc.vector.tensor_copy(out=columns[:, CHUNKS * i : CHUNKS * (i + 1)], in_=fours[i][:])
            nc.vector.tensor_scalar(out=bias_rows[:], in0=columns[:, 0:CHUNKS], scalar1=float(PROPOSALS), scalar2=None, op0=ALU.mult)
            bias_parts = small_psum.tile([P, CHUNKS], F32, name="bias_parts", tag="small")
            nc.tensor.matmul(out=bias_parts[:], lhsT=group_average[:], rhs=bias_rows[:], start=True, stop=True)
            nc.vector.tensor_reduce(out=bias_mean[:], in_=bias_parts[:], axis=AXIS.X, op=ALU.add)
            nc.vector.tensor_scalar(out=bias_centred[:], in0=columns[:, 0:CHUNKS], scalar1=bias_mean[:, 0:1], scalar2=None, op0=ALU.subtract)
            nc.vector.memset(eps_col[:], EPS)

        result = const.tile([P, BATCH, CHUNKS, PROPOSALS], F32)

        with tc.tile_pool(name="turned", bufs=3) as turned_pool, tc.tile_pool(name="step", bufs=3) as step_pool, tc.tile_pool(name="fetch", bufs=4) as fetch_pool, tc.tile_pool(
            name="merge", bufs=2
        ) as merge_pool, tc.tile_pool(name="operands", bufs=2) as operand_pool, tc.tile_pool(name="norm", bufs=2) as norm_pool, tc.psum_pool(
            name="table_psum", bufs=5
        ) as table_psum, tc.psum_pool(name="small_psum", bufs=1) as small_psum, tc.psum_pool(name="product_psum", bufs=CHUNKS // 2) as product_psum:

            frames_of, run4_of, run16_of, turned_of = {}, {}, {}, {}

            def weave(b):
                frames = step_pool.tile([P, FRAMES, PACK], BF16, name="frames")
                nc.scalar.copy(
                    out=frames[:].rearrange("p (r q) c -> p r q c", r=2), in_=raw_of[b // 2][:, b % 2].rearrange("p (c q r) -> p r q c", c=PACK, r=2)
                )
                frames_of[b] = frames

            def turn(words, first):
                landing = table_psum.tile([P, 2, 2, P], F32, name="landing")
                for a in range(2):
                    for half in range(2):
                        nc.tensor.transpose(landing[:, a, half, :], words(half, first + P * a), identity_words[:])
                return landing

            def side_by_side(level):
                words = level.rearrange("p e c -> p (e c)").bitcast(F32)
                return lambda half, first: words[:, 2 * first + half : 2 * first + half + 2 * P - 1 : 2]

            def swapped(view):
                return view.rearrange("p x y m -> p y x m")

            def larger(result_view, one, other):
                nc.vector.tensor_tensor(out=result_view, in0=one, in1=other, op=ALU.max)

            def first_level(b):
                if b % 2 == 0:
                    turned_of[b // 2] = turned_pool.tile([P, 2, ZONES, 2, 2, ROW_WORDS], F32, name="turned")
                frames = frames_of[b]
                landing = turn(side_by_side(frames[:]), 0)
                nc.scalar.copy(out=turned_of[b // 2][:, b % 2, 0], in_=swapped(landing[:]))
                run2 = run2_ring[b % 2]
                many = FRAMES // 2
                larger(run2[:, 0, 0:many], frames[:, 0:many], frames[:, many:FRAMES])
                larger(run2[:, 1, 0:many], frames[:, many:FRAMES], frames[:, 1 : many + 1])
                run4 = step_pool.tile([P, FRAMES + 64, PACK], BF16, name="run4")
                for r in range(2):
                    larger(
                        run4[:, 0:FRAMES].rearrange("p (g r q) c -> p r g q c", r=2, q=16)[:, r],
                        run2[:, r, 0:many].rearrange("p (q g) c -> p g q c", g=8),
                        run2[:, r, 1 : many + 1].rearrange("p (q g) c -> p g q c", g=8),
                    )
                words = run4[:].rearrange("p e c -> p (e c)").bitcast(F32)
                nc.vector.tensor_copy(out=words[:, 2 * FRAMES : 2 * FRAMES + 128], in_=words[:, 2 : 2 + 128])
                run4_of[b] = run4

            def turned_maximum(words, b, zone, copy):
                landing = turn(words, 0)
                shifted = turn(words, 64)
                here = step_pool.tile([P, 2, 2, P], F32, name="here")
                copy(out=here[:], in_=landing[:])
                larger(swapped(turned_of[b // 2][:, b % 2, zone].bitcast(BF16)), shifted[:].bitcast(BF16), here[:].bitcast(BF16))

            def second_level(b):
                turned_maximum(side_by_side(run4_of[b][:]), b, 1, nc.scalar.copy)

            def back_again(b):
                back8 = table_psum.tile([P, 2, 2, P], F32, name="landing")
                for half in range(2):
                    for a in range(2):
                        nc.tensor.transpose(back8[:, half, a, :], turned_of[b // 2][:, b % 2, 1, half, a, :], identity_words[:])
                ordered = back8[:].rearrange("p h a e -> p h (a e)")
                run8 = step_pool.tile([P, 2, FRAMES + 32], F32, name="run8")
                nc.scalar.copy(
                    out=run8[:, :, 0:FRAMES].rearrange("p h (g x) -> p h g x", g=4), in_=ordered.rearrange("p h (x g) -> p h g x", g=4)
                )
                nc.scalar.copy(out=run8[:, :, FRAMES : FRAMES + 32], in_=ordered[:, :, 4 : 4 * 32 + 1 : 4])
                run16 = step_pool.tile([P, 2, FRAMES + 64], F32, name="run16")
                for half in range(2):
                    larger(
                        run16[:, half, 0:FRAMES].bitcast(BF16).rearrange("p (g x j) -> p g x j", g=4, j=2),
                        back8[:, half].rearrange("p a e -> p (a e)").bitcast(BF16).rearrange("p (x g j) -> p g x j", g=4, j=2),
                        run8[:, half, 32 : FRAMES + 32].bitcast(BF16).rearrange("p (g x j) -> p g x j", g=4, j=2),
                    )
                nc.scalar.copy(out=run16[:, :, FRAMES : FRAMES + 64], in_=run16[:, :, 1 : 1 + 64])
                run16_of[b] = run16

            def third_level(b):
                run16 = run16_of[b]
                turned_maximum(lambda half, first: run16[:, half, first : first + P], b, 2, nc.vector.tensor_copy)

            def publish(i, turned, fetched):
                for half in range(2):
                    unit = (2 * i + half) % UNITS
                    rows = out_rows[unit * UNIT_PITCH : unit * UNIT_PITCH + UNIT_ROWS]
                    nc.sync.dma_start(
                        out=rows.rearrange("(b z p a) w -> p (b z) (a w)", b=2, z=ZONES, p=P), in_=turned[:, :, :, half].rearrange("p b z a w -> p (b z) (a w)")
                    )
                    for end in range(2):
                        nc.gpsimd.indirect_dma_start(
                            out=fetched[:, half, end, :],
                            out_offset=None,
                            in_=out_rows[0 : (unit + 1) * UNIT_PITCH, :],
                            in_offset=bass.IndirectOffsetOnAxis(ap=row_index[:, end, i, half : half + 1], axis=0),
                        )

            def merge(i, fetched, pooled, place):
                runs = merge_pool.tile([P, 2, SLOTS, HALF], BF16, name="runs")
                twos = merge_pool.tile([P, 2, 2, HALF], BF16, name="twos")
                values = merge_pool.tile([P, 2, HALF], BF16, name="values")
                for half in range(2):
                    nc.vector.tensor_tensor(
                        out=runs[:, half].rearrange("p s c -> p (s c)"), in0=fetched[:, half, 0].bitcast(BF16), in1=fetched[:, half, 1].bitcast(BF16), op=ALU.max
                    )
                for half in range(2):
                    for slot in range(1, SLOTS):
                        nc.scalar.activation(
                            out=runs[:, half, slot, :], in_=runs[:, half, slot, :], func=ACT.Identity,
                            scale=slot_scale[:, slot - 1, i, half : half + 1], bias=slot_bias[:, slot - 1, i, half : half + 1],
                        )
                for half in range(2):
                    nc.vector.tensor_tensor(out=twos[:, half], in0=runs[:, half, 0:2, :], in1=runs[:, half, 2:4, :], op=ALU.max)
                for half in range(2):
                    nc.vector.tensor_tensor(out=values[:, half], in0=twos[:, half, 0, :], in1=twos[:, half, 1, :], op=ALU.max)
                flat = values[:].rearrange("p h c -> p (h c)")
                back = small_psum.tile([P, PACK, P], BF16, name="back", tag="small")
                for t in range(PACK):
                    nc.tensor.transpose(back[:, t, :], flat[:, t : t + PACK * (P - 1) + 1 : PACK], identity[:])
                nc.scalar.copy(
                    out=pooled[:, place : place + 2, :, :].rearrange("p b n t -> p (b n) t"), in_=back[:].rearrange("p t c -> p c t")
                )

            def finish_round(first_batch, count, pooled):
                codes = operand_pool.tile([P, count * PROPOSALS], U32, align_bytes=64, name="codes")
                scales = operand_pool.tile([P, count * PROPOSALS], U8, align_bytes=64, name="scales")
                nc.vector.quantize_mx(out=codes[:].bitcast(FP8X4), scales=scales[:], in_=pooled[:].rearrange("p b n j -> p (b n j)"))
                stats = CHUNKS * count
                products = []
                row_sum = norm_pool.tile([P, CHUNKS, count], F32, name="row_sum")
                for q in range(CHUNKS):
                    cols = slice(P * q, P * (q + 1))
                    if q % 2 == 0:
                        bank = product_psum.tile([P, 2, count, PROPOSALS], F32, name="product")
                    product = bank[:, q % 2]
                    nc.tensor.matmul_mx(
                        out=product.rearrange("p b n -> p (b n)"),
                        lhsT=w_sorted[:, cols].bitcast(FP8X4),
                        lhsT_scale=s_sorted[:, cols],
                        rhs=codes[:].bitcast(FP8X4),
                        rhs_scale=scales[:],
                        start=True,
                        stop=True,
                    )
                    products.append(product)
                    if q % 2 == 1:
                        nc.vector.tensor_reduce(out=row_sum[:, q - 1 : q + 1, :], in_=bank[:], axis=AXIS.X, op=ALU.add)
                mean_parts = small_psum.tile([P, CHUNKS, count], F32, name="mean_parts", tag="small")
                nc.tensor.matmul(
                    out=mean_parts[:].rearrange("p q b -> p (q b)"), lhsT=group_average[:], rhs=row_sum[:].rearrange("p q b -> p (q b)"), start=True, stop=True
                )
                group_mean = norm_pool.tile([P, count], F32, name="group_mean")
                nc.vector.tensor_reduce(out=group_mean[:], in_=mean_parts[:].rearrange("p q b -> p b q"), axis=AXIS.X, op=ALU.add)
                to_centre = norm_pool.tile([P, CHUNKS, count], F32, name="to_centre")
                nc.vector.tensor_tensor(
                    out=to_centre[:],
                    in0=bias_centred[:].unsqueeze(2).to_broadcast([P, CHUNKS, count]),
                    in1=group_mean[:].unsqueeze(1).to_broadcast([P, CHUNKS, count]),
                    op=ALU.subtract,
                )
                row_squares = norm_pool.tile([P, stats], F32, name="row_squares")
                for q in range(CHUNKS):
                    squares = norm_pool.tile([P, count, PROPOSALS], F32, name="squares")
                    for i in range(count):
                        s = count * q + i
                        nc.scalar.activation(
                            out=squares[:, i, :], in_=products[q][:, i, :], func=ACT.Square, bias=to_centre[:, q, i : i + 1], scale=1.0,
                            accum_out=row_squares[:, s : s + 1],
                        )
                var_parts = small_psum.tile([P, CHUNKS, count], F32, name="var_parts", tag="small")
                nc.tensor.matmul(out=var_parts[:].rearrange("p q b -> p (q b)"), lhsT=group_average[:], rhs=row_squares[:], start=True, stop=True)
                group_var = norm_pool.tile([P, count], F32, name="group_var")
                nc.vector.tensor_reduce(out=group_var[:], in_=var_parts[:].rearrange("p q b -> p b q"), axis=AXIS.X, op=ALU.add)
                deviation = norm_pool.tile([P, count], F32, name="deviation")
                nc.scalar.activation(out=deviation[:], in_=group_var[:], func=ACT.Sqrt, bias=eps_col[:, 0:1], scale=1.0)
                inverse = norm_pool.tile([P, count], F32, name="inverse")
                nc.vector.reciprocal(out=inverse[:], in_=deviation[:])
                factor = norm_pool.tile([P, CHUNKS, count], F32, name="factor")
                nc.vector.tensor_tensor(
                    out=factor[:],
                    in0=gain_col.unsqueeze(2).to_broadcast([P, CHUNKS, count]),
                    in1=inverse[:].unsqueeze(1).to_broadcast([P, CHUNKS, count]),
                    op=ALU.mult,
                )
                offset = norm_pool.tile([P, CHUNKS, count], F32, name="offset")
                nc.vector.tensor_tensor(out=offset[:], in0=factor[:], in1=to_centre[:], op=ALU.mult)
                nc.vector.tensor_tensor(out=offset[:], in0=offset[:], in1=shift_col.unsqueeze(2).to_broadcast([P, CHUNKS, count]), op=ALU.add)
                for q in range(CHUNKS):
                    for i in range(count):
                        nc.scalar.activation(
                            out=result[:, first_batch + i, q, :], in_=products[q][:, i, :], func=ACT.Relu,
                            bias=offset[:, q, i : i + 1], scale=factor[:, q, i : i + 1],
                        )

            rounds = [(first_batch, ROUND) for first_batch in range(0, BATCH, ROUND)]
            round_of = {}
            for first_batch, count in rounds:
                for b in range(first_batch, first_batch + count):
                    round_of[b] = (first_batch, count)
            MERGE_LAG = 6
            fetched_of = {}
            pooled_of = {}
            load(1)
            weave(0)
            for step in range(BATCH + 4 + MERGE_LAG):
                if step % 2 == 0 and 4 <= step + 4 < BATCH:
                    load(step // 2 + 2)
                if 0 <= step - 3 < BATCH:
                    third_level(step - 3)
                if 0 <= step - 2 < BATCH:
                    back_again(step - 2)
                if 0 <= step - 1 < BATCH:
                    second_level(step - 1)
                if step < BATCH:
                    first_level(step)
                if step + 1 < BATCH:
                    weave(step + 1)
                if step == 1:
                    with tc.tile_pool(name="setup", bufs=1) as setup:
                        prepare_rows(setup)
                if 0 <= step - 4 < BATCH and step % 2 == 0:
                    i = (step - 4) // 2
                    fetched_of[i] = fetch_pool.tile([P, 2, 2, SLOTS * ROW_WORDS], F32, name="fetched")
                    publish(i, turned_of[i], fetched_of[i])
                    if i == 0:
                        prepare_norm()
                done = step - 4 - MERGE_LAG
                if done >= 0 and done % 2 == 0:
                    first_batch, count = round_of[done]
                    if done == first_batch:
                        pooled_of[first_batch] = operand_pool.tile([P, count, PROPOSALS, PACK], BF16, align_bytes=64, name="pooled")
                    merge(done // 2, fetched_of[done // 2], pooled_of[first_batch], done - first_batch)
                    if done + 2 == first_batch + count:
                        finish_round(first_batch, count, pooled_of[first_batch])

            for first_batch, count in rounds:
                batches = slice(first_batch, first_batch + count)
                nc.sync.dma_start(
                    out=out[batches].rearrange("b (p q) n -> p b (q n)", q=CHUNKS), in_=result[:, batches].rearrange("p b q n -> p b (q n)")
                )
